import numpy as np
import ml_dtypes


def mxq(x, axis, fmt="e4m3"):
    dtype, down = {"e4m3": (ml_dtypes.float8_e4m3fn, 7), "e5m2": (ml_dtypes.float8_e5m2, 14)}[fmt]
    v = np.moveaxis(np.asarray(x, np.float32).astype(ml_dtypes.bfloat16).astype(np.float64), axis, -1)
    blocks = v.reshape(v.shape[:-1] + (-1, 32))
    amax = np.abs(blocks).max(-1, keepdims=True)
    byte = np.maximum(np.where(amax > 0, np.frexp(amax)[1] - 1 + 127, 0) - down, 1)
    scale = np.exp2(byte - 127.0)
    codes = (blocks / scale).astype(np.float32).astype(dtype).astype(np.float64)
    return np.moveaxis((codes * scale).reshape(v.shape), -1, axis)


WIDE = False


def mx_kscale(k):
    if not WIDE:
        return np.ones(k)
    levels = np.array([10, -10, 5, -5, 0])
    if k % 512:
        return np.exp2(np.random.permutation(np.resize(levels, k // 32))).repeat(32)
    a = np.empty((k // 512, 16))
    for p in range(k // 512):
        a[p, :8] = np.random.permutation(np.resize(levels, 8))
        for g in range(8):
            far = levels[np.abs(levels - a[p, g]) >= 10]
            a[p, g + 8] = far[np.random.randint(len(far))]
    return np.exp2(a.ravel()).repeat(32)


BF16 = ml_dtypes.bfloat16


def bf(x):
    return np.asarray(x, np.float32).astype(BF16)


def f64(x):
    return np.asarray(x).astype(np.float64)


B, S, H, NH, LAT = 4, 2048, 512, 4, 512
HD = H // NH
HALF = H // 2
R = HALF // 2
ROPE_BASE = 10000.0


def rope_table():
    inv_freq = 1.0 / ROPE_BASE ** (np.arange(0, R, 2) / R)
    freqs = np.outer(np.arange(S), inv_freq)
    emb = np.concatenate([freqs, freqs], -1)
    return np.cos(emb), np.sin(emb)


def apply_rotary(x, cos, sin):
    h = x.shape[-1] // 2
    x1, x2 = x[..., :h], x[..., h:]
    return np.concatenate([x1 * cos - x2 * sin, x1 * sin + x2 * cos], -1)


def draw0():
    s, t = mx_kscale(H), mx_kscale(LAT)
    cos, sin = rope_table()
    return {"hidden_states": bf(np.random.standard_normal((B, S, H)) * s),
            "Wq_down": bf(np.random.standard_normal((LAT, H)) / np.sqrt(H) * t[:, None] / s),
            "bq_down": bf(np.random.standard_normal(LAT) * 0.2 * t),
            "Wq_up": bf(np.random.standard_normal((HALF, LAT)) * 1.2 / np.sqrt(LAT) / t),
            "bq_up": bf(np.random.standard_normal(HALF) * 0.2),
            "rope_cos": bf(cos),
            "rope_sin": bf(sin)}


def core(hidden_states, Wq_down, bq_down, Wq_up, bq_up, rope_cos, rope_sin):
    q_lat = (mxq(f64(hidden_states), 2, "e4m3") @ mxq(f64(Wq_down), 1, "e4m3").T) + f64(bq_down)
    q_half = (mxq(q_lat, 2, "e4m3") @ mxq(f64(Wq_up), 1, "e4m3").T) + f64(bq_up)
    q = np.concatenate([q_half, apply_rotary(q_half, f64(rope_cos), f64(rope_sin))], -1)
    return q.reshape(B, S, NH, HD).transpose(0, 2, 1, 3)


def e4m3fn_bytes(y):
    return np.clip(np.asarray(y, np.float64), -448.0, 448.0).astype(np.float32).astype(ml_dtypes.float8_e4m3fn).view(np.uint8)


def e4m3fn_values(b):
    return np.asarray(b, np.uint8).view(ml_dtypes.float8_e4m3fn).astype(np.float64)


def setup_inputs():
    d = draw0()
    x0 = np.asarray(d['hidden_states']).astype(np.float64)
    s = (np.max(np.abs(x0), axis=(0, 1), keepdims=True) / 448.0).astype(np.float32)
    out = {}
    for k, v in d.items():
        if k == 'hidden_states':
            out['hidden_states_bytes'] = e4m3fn_bytes(x0 / s.astype(np.float64))
            out['hidden_states_scale'] = s
        else:
            out[k] = v
    return out


def reference(hidden_states_bytes, hidden_states_scale, Wq_down, bq_down, Wq_up, bq_up, rope_cos, rope_sin):
    return core(e4m3fn_values(hidden_states_bytes) * hidden_states_scale.astype(np.float64), Wq_down, bq_down, Wq_up, bq_up, rope_cos, rope_sin)

@@ -1,0 +1,304 @@
+from contextlib import ExitStack
+
+import concourse.mybir as mybir
+from concourse.masks import make_identity
+
+F32 = mybir.dt.float32
+BF16 = mybir.dt.bfloat16
+U32 = mybir.dt.uint32
+U8 = mybir.dt.uint8
+FP8 = mybir.dt.float8_e4m3fn
+FP8X4 = mybir.dt.float8_e4m3fn_x4
+ADD = mybir.AluOpType.add
+MULT = mybir.AluOpType.mult
+COPY = mybir.ActivationFunctionType.Copy
+IDENT = mybir.ActivationFunctionType.Identity
+
+B, S, H, LAT, HALF = 4, 2048, 512, 512, 256
+FLOPS = 2 * B * S * H * LAT + 2 * B * S * LAT * HALF
+
+P = 128
+T4 = 4
+J = 4
+GRP = P * J
+PG = S // GRP
+NG = B * PG
+
+
+def tile_multiheadlatentattention_pa_t_kernel(
+    tc, x_bytes, x_scale, wq_down, bq_down, wq_up, bq_up, rope_cos, rope_sin, out
+):
+    nc = tc.nc
+    with ExitStack() as ctx:
+        keep = ctx.enter_context(tc.tile_pool(name="keep", bufs=1))
+        sb = ctx.enter_context(tc.tile_pool(name="sb", bufs=3))
+        ps = ctx.enter_context(tc.psum_pool(name="ps", bufs=2))
+
+        xb = {}
+
+        def load_x(n):
+            pg, b = divmod(n, B)
+            t = sb.tile([P, J, H], U8, name="xbytes", bufs=6, align_bytes=64)
+            nc.sync.dma_start(
+                out=t[:],
+                in_=x_bytes[b, pg * GRP : (pg + 1) * GRP, :].rearrange("(p j) k -> p j k", j=J),
+            )
+            xb[n] = t
+
+        load_x(0)
+        sc = keep.tile([P, T4], F32, name="sc")
+        nc.sync.dma_start(out=sc[:], in_=x_scale.rearrange("a b (p t) -> p (a b t)", t=T4))
+        wd = keep.tile([P, T4, H], BF16, name="wd", align_bytes=64)
+        nc.sync.dma_start(out=wd[:], in_=wq_down.rearrange("(m t) k -> m t k", t=T4))
+        load_x(1)
+        bd = keep.tile([P, T4], BF16, name="bd")
+        nc.sync.dma_start(out=bd[:], in_=bq_down.rearrange("(p t) -> p t", t=T4))
+        wu = keep.tile([P, 2, LAT], BF16, name="wu", align_bytes=64)
+        nc.sync.dma_start(out=wu[:], in_=wq_up.rearrange("(h m) k -> m h k", h=2))
+        burow = keep.tile([P, P], BF16, name="burow")
+        nc.gpsimd.memset(burow[:], 0.0)
+        nc.sync.dma_start(out=burow[0:2, :], in_=bq_up.rearrange("(h c) -> h c", h=2))
+        load_x(2)
+        cosr = keep.tile([P, PG, J, P], BF16, name="cosr", align_bytes=64)
+        sinr = keep.tile([P, PG, J, P], BF16, name="sinr", align_bytes=64)
+        nc.sync.dma_start(out=cosr[:], in_=rope_cos.rearrange("(g p j) c -> p g j c", p=P, j=J))
+        nc.sync.dma_start(out=sinr[:], in_=rope_sin.rearrange("(g p j) c -> p g j c", p=P, j=J))
+
+        idf = keep.tile([P, P], F32, name="idf")
+        make_identity(nc, idf[:])
+        idb = keep.tile([P, P], BF16, name="idb")
+        nc.vector.tensor_copy(out=idb[:], in_=idf[:])
+
+        wdc = keep.tile([P, LAT], U32, name="wdc", align_bytes=64)
+        wds = keep.tile([P, LAT], U8, name="wds", align_bytes=64)
+        wuc = keep.tile([P, HALF], U32, name="wuc", align_bytes=64)
+        wus = keep.tile([P, HALF], U8, name="wus", align_bytes=64)
+        bu = keep.tile([P, 2], F32, name="bu")
+
+        xbf, xt, xg, xc, xs, qg, qc, qs, m1, m2, qt, pa, pb, tab = ({} for i in range(14))
+
+        def cast(n):
+            t = sb.tile([P, J, H], BF16, name="xbf", align_bytes=64)
+            nc.scalar.copy(out=t[:], in_=xb[n][:].bitcast(FP8))
+            xbf[n] = t
+
+        def turn(n, h):
+            words = xbf[n][:].bitcast(F32)
+            t = ps.tile([P, 2, 2 * P], F32, name="xt")
+            for jj in range(2):
+                for u in range(2):
+                    nc.tensor.transpose(
+                        t[:, u, jj * P : (jj + 1) * P], words[:, 2 * h + jj, u : H // 2 : 2], idf[:]
+                    )
+            xt[n, h] = t
+
+        def scale(n, h):
+            if h == 0:
+                t = sb.tile([P, GRP, T4], BF16, name="xg", align_bytes=64)
+                xg[n] = t
+            nc.vector.tensor_tensor(
+                out=xg[n][:, h * 2 * P : (h + 1) * 2 * P, :].rearrange("p r (u e) -> p r u e", e=2),
+                in0=xt[n, h][:].bitcast(BF16).rearrange("p u (r e) -> p r u e", e=2),
+                in1=sc[:].rearrange("p (u e) -> p u e", e=2).unsqueeze(1).to_broadcast([P, 2 * P, 2, 2]),
+                op=MULT,
+            )
+
+        def quant_x(n):
+            c = sb.tile([P, GRP], U32, name="xc", align_bytes=64)
+            s = sb.tile([P, GRP], U8, name="xs", align_bytes=64)
+            nc.vector.quantize_mx(
+                out=c[:].bitcast(FP8X4), scales=s[:], in_=xg[n][:].rearrange("p r t -> p (r t)")
+            )
+            xc[n], xs[n] = c, s
+
+        def down(n, j):
+            t = ps.tile([P, T4, P], F32, name="m1")
+            cols = slice(j * P, (j + 1) * P)
+            for k in range(T4):
+                ws = slice(k * P, (k + 1) * P)
+                nc.tensor.matmul_mx(
+                    out=t[:, k, :],
+                    lhsT=wdc[:, ws].bitcast(FP8X4),
+                    lhsT_scale=wds[:, ws],
+                    rhs=xc[n][:, cols].bitcast(FP8X4),
+                    rhs_scale=xs[n][:, cols],
+                    start=True,
+                    stop=True,
+                )
+            m1[n, j] = t
+
+        def lat(n, j):
+            if j == 0:
+                t = sb.tile([P, GRP, T4], BF16, name="qg", align_bytes=64)
+                qg[n] = t
+            nc.vector.tensor_tensor(
+                out=qg[n][:, j * P : (j + 1) * P, :],
+                in0=m1[n, j][:].rearrange("p t r -> p r t"),
+                in1=bd[:].unsqueeze(1).to_broadcast([P, P, T4]),
+                op=ADD,
+            )
+
+        def quant_q(n):
+            c = sb.tile([P, GRP], U32, name="qc", align_bytes=64)
+            s = sb.tile([P, GRP], U8, name="qs", align_bytes=64)
+            nc.vector.quantize_mx(
+                out=c[:].bitcast(FP8X4), scales=s[:], in_=qg[n][:].rearrange("p r t -> p (r t)")
+            )
+            qc[n], qs[n] = c, s
+
+        def up(n):
+            for h in range(2):
+                t = ps.tile([P, GRP], F32, name="m2")
+                ws = slice(h * P, (h + 1) * P)
+                nc.tensor.matmul_mx(
+                    out=t[:],
+                    lhsT=wuc[:, ws].bitcast(FP8X4),
+                    lhsT_scale=wus[:, ws],
+                    rhs=qc[n][:].bitcast(FP8X4),
+                    rhs_scale=qs[n][:],
+                    start=True,
+                    stop=True,
+                )
+                m2[n, h] = t
+
+        def half(n):
+            t = sb.tile([P, 2, GRP], F32, name="qt")
+            for h in range(2):
+                nc.scalar.activation(
+                    out=t[:, h, :], in_=m2[n, h][:], func=IDENT, bias=bu[:, h : h + 1]
+                )
+            qt[n] = t
+
+        def products(n):
+            pg = n // B
+            a = sb.tile([P, 2, GRP], F32, name="pa")
+            b = sb.tile([P, 2, GRP], F32, name="pb")
+            for i in range(2):
+                nc.gpsimd.tensor_tensor(
+                    out=a[:, i, :], in0=qt[n][:, 0, :], in1=tab[pg][:, 1 + i, :], op=MULT
+                )
+                nc.gpsimd.tensor_tensor(
+                    out=b[:, i, :], in0=qt[n][:, 1, :], in1=tab[pg][:, i, :], op=MULT
+                )
+            pa[n], pb[n] = a, b
+
+        osb = {}
+
+        def emit(n, j):
+            if j == 0:
+                t = sb.tile([P, 4, J, P], F32, name="osb", bufs=2)
+                osb[n] = t
+            o = ps.tile([P, 4, P], F32, name="ob")
+            cols = slice(j * P, (j + 1) * P)
+            for h in range(2):
+                nc.tensor.transpose(o[:, h, :], qt[n][:, h, cols], idf[:])
+            for i in range(2):
+                nc.tensor.matmul(
+                    o[:, 2 + i, :], lhsT=pa[n][:, i, cols], rhs=idf[:], start=True, stop=False, is_transpose=True
+                )
+                nc.tensor.matmul(
+                    o[:, 2 + i, :], lhsT=pb[n][:, i, cols], rhs=idf[:], start=False, stop=True, is_transpose=True
+                )
+            nc.scalar.copy(out=osb[n][:, :, j, :], in_=o[:])
+            if j == J - 1:
+                pg, b = divmod(n, B)
+                nc.sync.dma_start(
+                    out=out[b, :, pg * GRP : (pg + 1) * GRP, :].rearrange("h (p j) d -> p h (j d)", j=J),
+                    in_=osb[n][:].rearrange("p h j d -> p h (j d)"),
+                )
+
+        def table(pg):
+            t = sb.tile([P, 3, GRP], BF16, name="tab", bufs=2)
+            o = ps.tile([P, 2, J, P], BF16, name="ob")
+            for i, src in enumerate((cosr, sinr)):
+                for j in range(J):
+                    nc.tensor.transpose(o[:, i, j, :], src[:, pg, j, :], idb[:])
+            nc.scalar.copy(out=t[:, 1:3, :], in_=o[:].rearrange("p i j c -> p i (j c)"))
+            nc.scalar.activation(
+                out=t[:, 0, :], in_=o[:, 1, :, :].rearrange("p j c -> p (j c)"), func=COPY, scale=-1.0
+            )
+            tab[pg] = t
+
+        def prep_down():
+            g = keep.tile([P, LAT, T4], BF16, name="wdg", align_bytes=64)
+            words = wd[:].bitcast(F32)
+            for h in range(2):
+                t = ps.tile([P, 2, 2 * P], F32, name="m1")
+                for jj in range(2):
+                    for u in range(2):
+                        nc.tensor.transpose(
+                            t[:, u, jj * P : (jj + 1) * P], words[:, 2 * h + jj, u : H // 2 : 2], idf[:]
+                        )
+                nc.scalar.copy(
+                    out=g[:, h * 2 * P : (h + 1) * 2 * P, :].bitcast(F32), in_=t[:].rearrange("p u r -> p r u")
+                )
+            nc.vector.quantize_mx(
+                out=wdc[:].bitcast(FP8X4), scales=wds[:], in_=g[:].rearrange("p r t -> p (r t)")
+            )
+
+        def prep_up():
+            g = keep.tile([P, HALF, T4], BF16, name="wug", align_bytes=64)
+            words = wu[:].bitcast(F32)
+            t = ps.tile([P, 2, 2 * P], F32, name="m1")
+            for h in range(2):
+                for u in range(2):
+                    nc.tensor.transpose(
+                        t[:, u, h * P : (h + 1) * P], words[:, h, u : LAT // 2 : 2], idf[:]
+                    )
+            nc.scalar.copy(out=g[:].bitcast(F32), in_=t[:].rearrange("p u r -> p r u"))
+            nc.vector.quantize_mx(
+                out=wuc[:].bitcast(FP8X4), scales=wus[:], in_=g[:].rearrange("p r t -> p (r t)")
+            )
+            o = ps.tile([P, P], BF16, name="ob")
+            nc.tensor.transpose(o[:], burow[:], idb[:])
+            nc.scalar.copy(out=bu[:], in_=o[:, 0:2])
+
+        def ok(n):
+            return 0 <= n < NG
+
+        with tc.manual_schedule():
+            for s in range(-3, NG + 3):
+                if ok(s + 6):
+                    if s + 6 >= 3:
+                        load_x(s + 6)
+                if ok(s + 2):
+                    turn(s + 2, 0)
+                if ok(s + 3):
+                    cast(s + 3)
+                if s == -2:
+                    prep_down()
+                if s == -1:
+                    prep_up()
+                if ok(s):
+                    down(s, 0)
+                    down(s, 1)
+                    lat(s, 0)
+                    lat(s, 1)
+                if ok(s + 2):
+                    scale(s + 2, 0)
+                if ok(s + 1):
+                    quant_x(s + 1)
+                if ok(s - 1):
+                    up(s - 1)
+                    half(s - 1)
+                if ok(s - 3):
+                    emit(s - 3, 0)
+                    emit(s - 3, 1)
+                if ok(s) and s % B == 0:
+                    table(s // B)
+                if ok(s + 2):
+                    turn(s + 2, 1)
+                if ok(s):
+                    down(s, 2)
+                    down(s, 3)
+                    lat(s, 2)
+                    lat(s, 3)
+                if ok(s + 2):
+                    scale(s + 2, 1)
+                if ok(s):
+                    quant_q(s)
+                if ok(s - 2):
+                    products(s - 2)
+                if ok(s - 3):
+                    emit(s - 3, 2)
+                    emit(s - 3, 3)

@@ -21,8 +21,11 @@ P = 128
 T4 = 4
 J = 4
 GRP = P * J
+HG = GRP // 2
 PG = S // GRP
 NG = B * PG
+RING = 4
+SLOTS = 3
 
 
 def tile_multiheadlatentattention_pa_t_kernel(
@@ -32,37 +35,58 @@ def tile_multiheadlatentattention_pa_t_kernel(
     with ExitStack() as ctx:
         keep = ctx.enter_context(tc.tile_pool(name="keep", bufs=1))
         sb = ctx.enter_context(tc.tile_pool(name="sb", bufs=3))
-        ps = ctx.enter_context(tc.psum_pool(name="ps", bufs=2))
+        ps = ctx.enter_context(tc.psum_pool(name="ps", bufs=1))
+        ctx.enter_context(tc.manual_schedule())
+
+        used = {"v": 0, "s": 0}
+
+        def bank(ring, shape, dtype):
+            i = used[ring] % RING
+            used[ring] = used[ring] + 1
+            return ps.tile(shape, dtype, name="bank_%s%d" % (ring, i))
 
         xb = {}
 
-        def load_x(n):
+        def load_x(n, parts):
             pg, b = divmod(n, B)
-            t = sb.tile([P, J, H], U8, name="xbytes", bufs=6, align_bytes=64)
-            nc.sync.dma_start(
-                out=t[:],
-                in_=x_bytes[b, pg * GRP : (pg + 1) * GRP, :].rearrange("(p j) k -> p j k", j=J),
-            )
+            rows = x_bytes[b, pg * GRP : (pg + 1) * GRP, :].rearrange("(p j) k -> p j k", j=J)
+            t = sb.tile([P, J, H], U8, name="xbytes", bufs=NG, align_bytes=64)
+            w = J // parts
+            for i in range(parts):
+                nc.sync.dma_start(out=t[:, i * w : (i + 1) * w, :], in_=rows[:, i * w : (i + 1) * w, :])
             xb[n] = t
 
-        load_x(0)
+        rope = {}
+
+        def load_rope(pair):
+            for i, src in enumerate((rope_cos, rope_sin)):
+                t = keep.tile([P, 2, J, P], BF16, name="rope%d_%d" % (i, pair), align_bytes=64)
+                nc.sync.dma_start(
+                    out=t[:],
+                    in_=src[pair * 2 * GRP : (pair + 1) * 2 * GRP, :].rearrange("(g p j) c -> p g j c", p=P, j=J),
+                )
+                rope[i, pair] = t
+
+        load_x(0, 2)
         sc = keep.tile([P, T4], F32, name="sc")
         nc.sync.dma_start(out=sc[:], in_=x_scale.rearrange("a b (p t) -> p (a b t)", t=T4))
         wd = keep.tile([P, T4, H], BF16, name="wd", align_bytes=64)
         nc.sync.dma_start(out=wd[:], in_=wq_down.rearrange("(m t) k -> m t k", t=T4))
-        load_x(1)
+        load_x(1, 1)
         bd = keep.tile([P, T4], BF16, name="bd")
         nc.sync.dma_start(out=bd[:], in_=bq_down.rearrange("(p t) -> p t", t=T4))
+        load_x(2, 1)
         wu = keep.tile([P, 2, LAT], BF16, name="wu", align_bytes=64)
         nc.sync.dma_start(out=wu[:], in_=wq_up.rearrange("(h m) k -> m h k", h=2))
-        burow = keep.tile([P, P], BF16, name="burow")
-        nc.gpsimd.memset(burow[:], 0.0)
-        nc.sync.dma_start(out=burow[0:2, :], in_=bq_up.rearrange("(h c) -> h c", h=2))
-        load_x(2)
-        cosr = keep.tile([P, PG, J, P], BF16, name="cosr", align_bytes=64)
-        sinr = keep.tile([P, PG, J, P], BF16, name="sinr", align_bytes=64)
-        nc.sync.dma_start(out=cosr[:], in_=rope_cos.rearrange("(g p j) c -> p g j c", p=P, j=J))
-        nc.sync.dma_start(out=sinr[:], in_=rope_sin.rearrange("(g p j) c -> p g j c", p=P, j=J))
+        load_x(3, 1)
+        load_rope(0)
+        bu = keep.tile([P, 2, 2], BF16, name="bu")
+        with nc.allow_non_contiguous_dma(reason="one bias value for each partition and half"):
+            nc.sync.dma_start(out=bu[:, :, 0:1], in_=bq_up.rearrange("(h c o) -> c h o", h=2, o=1))
+        load_x(4, 1)
+        load_rope(1)
+        for n in range(5, NG):
+            load_x(n, 1)
 
         idf = keep.tile([P, P], F32, name="idf")
         make_identity(nc, idf[:])
@@ -73,46 +97,51 @@ def tile_multiheadlatentattention_pa_t_kernel(
         wds = keep.tile([P, LAT], U8, name="wds", align_bytes=64)
         wuc = keep.tile([P, HALF], U32, name="wuc", align_bytes=64)
         wus = keep.tile([P, HALF], U8, name="wus", align_bytes=64)
-        bu = keep.tile([P, 2], F32, name="bu")
+        wdg = keep.tile([P, LAT, T4], BF16, name="wdg", align_bytes=64)
+        wug = keep.tile([P, HALF, T4], BF16, name="wug", align_bytes=64)
 
-        xbf, xt, xg, xc, xs, qg, qc, qs, m1, m2, qt, pa, pb, tab = ({} for i in range(14))
+        xbf, xt, grouped, codes, scales, m1, m2, qt, prod, tab, osb = ({} for i in range(11))
 
         def cast(n):
             t = sb.tile([P, J, H], BF16, name="xbf", align_bytes=64)
-            nc.scalar.copy(out=t[:], in_=xb[n][:].bitcast(FP8))
+            for h in range(2):
+                nc.scalar.copy(out=t[:, 2 * h : 2 * h + 2, :], in_=xb[n][:, 2 * h : 2 * h + 2, :].bitcast(FP8))
             xbf[n] = t
 
-        def turn(n, h):
-            words = xbf[n][:].bitcast(F32)
-            t = ps.tile([P, 2, 2 * P], F32, name="xt")
+        def turn_words(ring, words):
+            t = bank(ring, [P, 2, 2 * P], F32)
             for jj in range(2):
                 for u in range(2):
-                    nc.tensor.transpose(
-                        t[:, u, jj * P : (jj + 1) * P], words[:, 2 * h + jj, u : H // 2 : 2], idf[:]
-                    )
-            xt[n, h] = t
+                    nc.tensor.transpose(t[:, u, jj * P : (jj + 1) * P], words[:, jj, u : H // 2 : 2], idf[:])
+            return t
+
+        def turn(n, h):
+            xt[n, h] = turn_words("v", xbf[n][:, 2 * h : 2 * h + 2, :].bitcast(F32))
 
         def scale(n, h):
+            s = n - 1
             if h == 0:
-                t = sb.tile([P, GRP, T4], BF16, name="xg", align_bytes=64)
-                xg[n] = t
+                grouped[s] = sb.tile([P, 2, GRP, T4], BF16, name="slot%d" % (s % SLOTS), bufs=1, align_bytes=64)
             nc.vector.tensor_tensor(
-                out=xg[n][:, h * 2 * P : (h + 1) * 2 * P, :].rearrange("p r (u e) -> p r u e", e=2),
+                out=grouped[s][:, 0, h * HG : (h + 1) * HG, :].rearrange("p r (u e) -> p r u e", e=2),
                 in0=xt[n, h][:].bitcast(BF16).rearrange("p u (r e) -> p r u e", e=2),
-                in1=sc[:].rearrange("p (u e) -> p u e", e=2).unsqueeze(1).to_broadcast([P, 2 * P, 2, 2]),
+                in1=sc[:].rearrange("p (u e) -> p u e", e=2).unsqueeze(1).to_broadcast([P, HG, 2, 2]),
                 op=MULT,
             )
 
-        def quant_x(n):
-            c = sb.tile([P, GRP], U32, name="xc", align_bytes=64)
-            s = sb.tile([P, GRP], U8, name="xs", align_bytes=64)
+        def quant(s):
+            c = sb.tile([P, 2, GRP], U32, name="codes", bufs=2, align_bytes=64)
+            z = sb.tile([P, 2, GRP], U8, name="scales", bufs=2, align_bytes=64)
+            part = slice(0 if s + 1 < NG else 1, 2 if s >= 0 else 1)
             nc.vector.quantize_mx(
-                out=c[:].bitcast(FP8X4), scales=s[:], in_=xg[n][:].rearrange("p r t -> p (r t)")
+                out=c[:, part, :].rearrange("p a r -> p (a r)").bitcast(FP8X4),
+                scales=z[:, part, :].rearrange("p a r -> p (a r)"),
+                in_=grouped[s][:, part, :, :].rearrange("p a r t -> p (a r t)"),
             )
-            xc[n], xs[n] = c, s
+            codes[s], scales[s] = c, z
 
         def down(n, j):
-            t = ps.tile([P, T4, P], F32, name="m1")
+            t = bank("v", [P, T4, P], F32)
             cols = slice(j * P, (j + 1) * P)
             for k in range(T4):
                 ws = slice(k * P, (k + 1) * P)
@@ -120,42 +149,33 @@ def tile_multiheadlatentattention_pa_t_kernel(
                     out=t[:, k, :],
                     lhsT=wdc[:, ws].bitcast(FP8X4),
                     lhsT_scale=wds[:, ws],
-                    rhs=xc[n][:, cols].bitcast(FP8X4),
-                    rhs_scale=xs[n][:, cols],
+                    rhs=codes[n - 1][:, 0, cols].bitcast(FP8X4),
+                    rhs_scale=scales[n - 1][:, 0, cols],
                     start=True,
                     stop=True,
                 )
             m1[n, j] = t
 
         def lat(n, j):
-            if j == 0:
-                t = sb.tile([P, GRP, T4], BF16, name="qg", align_bytes=64)
-                qg[n] = t
+            if n not in grouped:
+                grouped[n] = sb.tile([P, 2, GRP, T4], BF16, name="slot%d" % (n % SLOTS), bufs=1, align_bytes=64)
             nc.vector.tensor_tensor(
-                out=qg[n][:, j * P : (j + 1) * P, :],
+                out=grouped[n][:, 1, j * P : (j + 1) * P, :],
                 in0=m1[n, j][:].rearrange("p t r -> p r t"),
                 in1=bd[:].unsqueeze(1).to_broadcast([P, P, T4]),
                 op=ADD,
             )
 
-        def quant_q(n):
-            c = sb.tile([P, GRP], U32, name="qc", align_bytes=64)
-            s = sb.tile([P, GRP], U8, name="qs", align_bytes=64)
-            nc.vector.quantize_mx(
-                out=c[:].bitcast(FP8X4), scales=s[:], in_=qg[n][:].rearrange("p r t -> p (r t)")
-            )
-            qc[n], qs[n] = c, s
-
         def up(n):
             for h in range(2):
-                t = ps.tile([P, GRP], F32, name="m2")
+                t = bank("s", [P, GRP], F32)
                 ws = slice(h * P, (h + 1) * P)
                 nc.tensor.matmul_mx(
                     out=t[:],
                     lhsT=wuc[:, ws].bitcast(FP8X4),
                     lhsT_scale=wus[:, ws],
-                    rhs=qc[n][:].bitcast(FP8X4),
-                    rhs_scale=qs[n][:],
+                    rhs=codes[n][:, 1, :].bitcast(FP8X4),
+                    rhs_scale=scales[n][:, 1, :],
                     start=True,
                     stop=True,
                 )
@@ -164,141 +184,152 @@ def tile_multiheadlatentattention_pa_t_kernel(
         def half(n):
             t = sb.tile([P, 2, GRP], F32, name="qt")
             for h in range(2):
-                nc.scalar.activation(
-                    out=t[:, h, :], in_=m2[n, h][:], func=IDENT, bias=bu[:, h : h + 1]
-                )
+                nc.scalar.activation(out=t[:, h, :], in_=m2[n, h][:], func=IDENT, bias=bu[:, h, 0:1])
             qt[n] = t
 
-        def products(n):
-            pg = n // B
-            a = sb.tile([P, 2, GRP], F32, name="pa")
-            b = sb.tile([P, 2, GRP], F32, name="pb")
-            for i in range(2):
-                nc.gpsimd.tensor_tensor(
-                    out=a[:, i, :], in0=qt[n][:, 0, :], in1=tab[pg][:, 1 + i, :], op=MULT
-                )
-                nc.gpsimd.tensor_tensor(
-                    out=b[:, i, :], in0=qt[n][:, 1, :], in1=tab[pg][:, i, :], op=MULT
-                )
-            pa[n], pb[n] = a, b
+        def products_gpsimd(n, a, after_quant):
+            if after_quant:
+                t = sb.tile([P, 2, 2, HG], F32, name="slot%d" % ((n + 1) % SLOTS), bufs=1, align_bytes=64)
+            else:
+                t = sb.tile([P, 2, 2, HG], F32, name="prod", bufs=4)
+            nc.gpsimd.tensor_tensor(
+                out=t[:],
+                in0=qt[n][:, :, a * HG : (a + 1) * HG].unsqueeze(2).to_broadcast([P, 2, 2, HG]),
+                in1=tab[n // B][:, a, :, :, :],
+                op=MULT,
+            )
+            prod[n, a] = t
 
-        osb = {}
+        def products_vector(n, a, h):
+            if h == 0:
+                prod[n, a] = sb.tile([P, 2, 2, HG], F32, name="prod", bufs=4)
+            nc.vector.scalar_tensor_tensor(
+                out=prod[n, a][:, h, :, :],
+                in0=m2[n, h][:, a * HG : (a + 1) * HG].unsqueeze(1).to_broadcast([P, 2, HG]),
+                scalar=bu[:, h, 0:1],
+                in1=tab[n // B][:, a, h, :, :],
+                op0=ADD,
+                op1=MULT,
+            )
 
-        def emit(n, j):
+        def emit(n, j, copy, store):
             if j == 0:
-                t = sb.tile([P, 4, J, P], F32, name="osb", bufs=2)
-                osb[n] = t
-            o = ps.tile([P, 4, P], F32, name="ob")
-            cols = slice(j * P, (j + 1) * P)
+                osb[n] = sb.tile([P, 4, J, P], F32, name="osb", bufs=3)
+            o = bank("s", [P, 4, P], F32)
+            a, jj = divmod(j, 2)
+            cols = slice(jj * P, (jj + 1) * P)
             for h in range(2):
-                nc.tensor.transpose(o[:, h, :], qt[n][:, h, cols], idf[:])
+                nc.tensor.transpose(o[:, h, :], qt[n][:, h, j * P : (j + 1) * P], idf[:])
             for i in range(2):
-                nc.tensor.matmul(
-                    o[:, 2 + i, :], lhsT=pa[n][:, i, cols], rhs=idf[:], start=True, stop=False, is_transpose=True
-                )
-                nc.tensor.matmul(
-                    o[:, 2 + i, :], lhsT=pb[n][:, i, cols], rhs=idf[:], start=False, stop=True, is_transpose=True
-                )
-            nc.scalar.copy(out=osb[n][:, :, j, :], in_=o[:])
-            if j == J - 1:
+                for h in range(2):
+                    nc.tensor.matmul(
+                        o[:, 2 + i, :],
+                        lhsT=prod[n, a][:, h, i, cols],
+                        rhs=idf[:],
+                        start=h == 0,
+                        stop=h == 1,
+                        is_transpose=True,
+                    )
+            copy(out=osb[n][:, :, j, :], in_=o[:])
+            if (j + 1) % store == 0:
                 pg, b = divmod(n, B)
+                rows = out[b, :, pg * GRP : (pg + 1) * GRP, :].rearrange("h (p j) d -> p h j d", j=J)
+                js = slice(j + 1 - store, j + 1)
                 nc.sync.dma_start(
-                    out=out[b, :, pg * GRP : (pg + 1) * GRP, :].rearrange("h (p j) d -> p h (j d)", j=J),
-                    in_=osb[n][:].rearrange("p h j d -> p h (j d)"),
+                    out=rows[:, :, js, :].rearrange("p h j d -> p h (j d)"),
+                    in_=osb[n][:, :, js, :].rearrange("p h j d -> p h (j d)"),
                 )
 
         def table(pg):
-            t = sb.tile([P, 3, GRP], BF16, name="tab", bufs=2)
-            o = ps.tile([P, 2, J, P], BF16, name="ob")
-            for i, src in enumerate((cosr, sinr)):
+            t = keep.tile([P, 2, 2, 2, HG], BF16, name="tab%d" % pg)
+            o = bank("s", [P, 2, J, P], BF16)
+            for i in range(2):
                 for j in range(J):
-                    nc.tensor.transpose(o[:, i, j, :], src[:, pg, j, :], idb[:])
-            nc.scalar.copy(out=t[:, 1:3, :], in_=o[:].rearrange("p i j c -> p i (j c)"))
-            nc.scalar.activation(
-                out=t[:, 0, :], in_=o[:, 1, :, :].rearrange("p j c -> p (j c)"), func=COPY, scale=-1.0
-            )
+                    nc.tensor.transpose(o[:, i, j, :], rope[i, pg // 2][:, pg % 2, j, :], idb[:])
+            halves = o[:].rearrange("p i (a j) c -> p a i (j c)", a=2)
+            nc.scalar.copy(out=t[:, :, 0, :, :], in_=halves)
+            nc.scalar.activation(out=t[:, :, 1, 0, :], in_=halves[:, :, 1, :], func=COPY, scale=-1.0)
+            nc.scalar.copy(out=t[:, :, 1, 1, :], in_=halves[:, :, 0, :])
             tab[pg] = t
 
-        def prep_down():
-            g = keep.tile([P, LAT, T4], BF16, name="wdg", align_bytes=64)
-            words = wd[:].bitcast(F32)
-            for h in range(2):
-                t = ps.tile([P, 2, 2 * P], F32, name="m1")
-                for jj in range(2):
-                    for u in range(2):
-                        nc.tensor.transpose(
-                            t[:, u, jj * P : (jj + 1) * P], words[:, 2 * h + jj, u : H // 2 : 2], idf[:]
-                        )
+        def turn_weights(w, g, pairs):
+            for h in range(pairs):
+                t = turn_words("s", w[:, 2 * h : 2 * h + 2, :].bitcast(F32))
                 nc.scalar.copy(
                     out=g[:, h * 2 * P : (h + 1) * 2 * P, :].bitcast(F32), in_=t[:].rearrange("p u r -> p r u")
                 )
-            nc.vector.quantize_mx(
-                out=wdc[:].bitcast(FP8X4), scales=wds[:], in_=g[:].rearrange("p r t -> p (r t)")
-            )
 
-        def prep_up():
-            g = keep.tile([P, HALF, T4], BF16, name="wug", align_bytes=64)
-            words = wu[:].bitcast(F32)
-            t = ps.tile([P, 2, 2 * P], F32, name="m1")
-            for h in range(2):
-                for u in range(2):
-                    nc.tensor.transpose(
-                        t[:, u, h * P : (h + 1) * P], words[:, h, u : LAT // 2 : 2], idf[:]
-                    )
-            nc.scalar.copy(out=g[:].bitcast(F32), in_=t[:].rearrange("p u r -> p r u"))
-            nc.vector.quantize_mx(
-                out=wuc[:].bitcast(FP8X4), scales=wus[:], in_=g[:].rearrange("p r t -> p (r t)")
-            )
-            o = ps.tile([P, P], BF16, name="ob")
-            nc.tensor.transpose(o[:], burow[:], idb[:])
-            nc.scalar.copy(out=bu[:], in_=o[:, 0:2])
+        def quant_weights(g, c, z):
+            nc.vector.quantize_mx(out=c[:].bitcast(FP8X4), scales=z[:], in_=g[:].rearrange("p r t -> p (r t)"))
 
         def ok(n):
             return 0 <= n < NG
 
-        with tc.manual_schedule():
-            for s in range(-3, NG + 3):
-                if ok(s + 6):
-                    if s + 6 >= 3:
-                        load_x(s + 6)
-                if ok(s + 2):
-                    turn(s + 2, 0)
-                if ok(s + 3):
-                    cast(s + 3)
-                if s == -2:
-                    prep_down()
-                if s == -1:
-                    prep_up()
-                if ok(s):
-                    down(s, 0)
-                    down(s, 1)
-                    lat(s, 0)
-                    lat(s, 1)
-                if ok(s + 2):
-                    scale(s + 2, 0)
-                if ok(s + 1):
-                    quant_x(s + 1)
-                if ok(s - 1):
-                    up(s - 1)
-                    half(s - 1)
-                if ok(s - 3):
-                    emit(s - 3, 0)
-                    emit(s - 3, 1)
-                if ok(s) and s % B == 0:
-                    table(s // B)
-                if ok(s + 2):
-                    turn(s + 2, 1)
-                if ok(s):
-                    down(s, 2)
-                    down(s, 3)
-                    lat(s, 2)
-                    lat(s, 3)
-                if ok(s + 2):
-                    scale(s + 2, 1)
-                if ok(s):
-                    quant_q(s)
-                if ok(s - 2):
-                    products(s - 2)
-                if ok(s - 3):
-                    emit(s - 3, 2)
-                    emit(s - 3, 3)
+        last = NG - 1
+        for s in range(-3, NG + 1):
+            spare = s >= last - 1
+            if ok(s - 2) and s <= last - 1:
+                products_gpsimd(s - 2, 1, True)
+            if ok(s + 1):
+                scale(s + 1, 1)
+            if ok(s):
+                down(s, 0)
+            if ok(s - 1):
+                up(s - 1)
+            if ok(s):
+                for j in range(1, J):
+                    down(s, j)
+            if ok(s - 1):
+                half(s - 1)
+                if not spare:
+                    products_gpsimd(s - 1, 0, False)
+                elif s <= last:
+                    products_gpsimd(s - 1, 1, False)
+            if ok(s):
+                lat(s, 0)
+                lat(s, 1)
+            if spare:
+                products_vector(s - 1, 0, 0)
+            if ok(s):
+                lat(s, 2)
+                lat(s, 3)
+            if spare:
+                products_vector(s - 1, 0, 1)
+            if s > last:
+                products_vector(s - 1, 1, 0)
+                products_vector(s - 1, 1, 1)
+            if ok(s + 2):
+                turn(s + 2, 0)
+            if ok(s + 3):
+                cast(s + 3)
+            if s in (0, 1):
+                table(2 * s)
+                table(2 * s + 1)
+            if ok(s - 2):
+                for j in range(J if s <= last - 1 else 0):
+                    emit(s - 2, j, nc.scalar.copy, J)
+                for j in range(2 if s == last else J, J):
+                    emit(s - 2, j, nc.scalar.copy, J)
+            if s == last - 1:
+                for j in range(2):
+                    emit(s - 1, j, nc.scalar.copy, J)
+            if s == last:
+                for j in range(J):
+                    emit(s - 1, j, nc.scalar.copy, J)
+            if s > last:
+                for j in range(J):
+                    emit(s - 1, j, nc.vector.tensor_copy if j == J - 1 else nc.scalar.copy, 2)
+            if ok(s + 2):
+                turn(s + 2, 1)
+            if s == -2:
+                turn_weights(wd, wdg, 2)
+            if s == -1:
+                turn_weights(wu, wug, 1)
+            if ok(s + 2):
+                scale(s + 2, 0)
+            if s == -1:
+                quant_weights(wdg, wdc, wds)
+            if s == 0:
+                quant_weights(wug, wuc, wus)
+            if -1 <= s <= last:
+                quant(s)

@@ -25,7 +25,8 @@ HG = GRP // 2
 PG = S // GRP
 NG = B * PG
 RING = 4
-SLOTS = 3
+SLOTS = 4
+SHARE = 48
 
 
 def tile_multiheadlatentattention_pa_t_kernel(
@@ -78,8 +79,8 @@ def tile_multiheadlatentattention_pa_t_kernel(
         load_x(2, 1)
         wu = keep.tile([P, 2, LAT], BF16, name="wu", align_bytes=64)
         nc.sync.dma_start(out=wu[:], in_=wq_up.rearrange("(h m) k -> m h k", h=2))
-        load_x(3, 1)
         load_rope(0)
+        load_x(3, 1)
         bu = keep.tile([P, 2, 2], BF16, name="bu")
         with nc.allow_non_contiguous_dma(reason="one bias value for each partition and half"):
             nc.sync.dma_start(out=bu[:, :, 0:1], in_=bq_up.rearrange("(h c o) -> c h o", h=2, o=1))
@@ -87,6 +88,9 @@ def tile_multiheadlatentattention_pa_t_kernel(
         load_rope(1)
         for n in range(5, NG):
             load_x(n, 1)
+
+        bias_row = keep.tile([P, HALF], BF16, name="bias_row")
+        nc.sync.dma_start(out=bias_row[:], in_=bq_up.partition_broadcast(P))
 
         idf = keep.tile([P, P], F32, name="idf")
         make_identity(nc, idf[:])
@@ -100,13 +104,13 @@ def tile_multiheadlatentattention_pa_t_kernel(
         wdg = keep.tile([P, LAT, T4], BF16, name="wdg", align_bytes=64)
         wug = keep.tile([P, HALF, T4], BF16, name="wug", align_bytes=64)
 
-        xbf, xt, grouped, codes, scales, m1, m2, qt, prod, tab, osb = ({} for i in range(11))
+        xbf, xt, grouped, codes, scales, m1, m2, m3, qt, prod, tab, osb = ({} for i in range(12))
 
-        def cast(n):
-            t = sb.tile([P, J, H], BF16, name="xbf", align_bytes=64)
-            for h in range(2):
-                nc.scalar.copy(out=t[:, 2 * h : 2 * h + 2, :], in_=xb[n][:, 2 * h : 2 * h + 2, :].bitcast(FP8))
-            xbf[n] = t
+        def cast(n, h):
+            t = sb.tile([P, 2, H], BF16, name="xbf", bufs=4, align_bytes=64)
+            copy = nc.vector.tensor_copy if (n, h) == (0, 0) else nc.scalar.copy
+            copy(out=t[:], in_=xb[n][:, 2 * h : 2 * h + 2, :].bitcast(FP8))
+            xbf[n, h] = t
 
         def turn_words(ring, words):
             t = bank(ring, [P, 2, 2 * P], F32)
@@ -116,10 +120,10 @@ def tile_multiheadlatentattention_pa_t_kernel(
             return t
 
         def turn(n, h):
-            xt[n, h] = turn_words("v", xbf[n][:, 2 * h : 2 * h + 2, :].bitcast(F32))
+            xt[n, h] = turn_words("v", xbf[n, h][:].bitcast(F32))
 
         def scale(n, h):
-            s = n - 1
+            s = n - 2
             if h == 0:
                 grouped[s] = sb.tile([P, 2, GRP, T4], BF16, name="slot%d" % (s % SLOTS), bufs=1, align_bytes=64)
             nc.vector.tensor_tensor(
@@ -130,9 +134,9 @@ def tile_multiheadlatentattention_pa_t_kernel(
             )
 
         def quant(s):
-            c = sb.tile([P, 2, GRP], U32, name="codes", bufs=2, align_bytes=64)
-            z = sb.tile([P, 2, GRP], U8, name="scales", bufs=2, align_bytes=64)
-            part = slice(0 if s + 1 < NG else 1, 2 if s >= 0 else 1)
+            c = sb.tile([P, 2, GRP], U32, name="codes", bufs=3, align_bytes=64)
+            z = sb.tile([P, 2, GRP], U8, name="scales", bufs=3, align_bytes=64)
+            part = slice(0 if s + 2 < NG else 1, 2 if s >= 0 else 1)
             nc.vector.quantize_mx(
                 out=c[:, part, :].rearrange("p a r -> p (a r)").bitcast(FP8X4),
                 scales=z[:, part, :].rearrange("p a r -> p (a r)"),
@@ -149,8 +153,8 @@ def tile_multiheadlatentattention_pa_t_kernel(
                     out=t[:, k, :],
                     lhsT=wdc[:, ws].bitcast(FP8X4),
                     lhsT_scale=wds[:, ws],
-                    rhs=codes[n - 1][:, 0, cols].bitcast(FP8X4),
-                    rhs_scale=scales[n - 1][:, 0, cols],
+                    rhs=codes[n - 2][:, 0, cols].bitcast(FP8X4),
+                    rhs_scale=scales[n - 2][:, 0, cols],
                     start=True,
                     stop=True,
                 )
@@ -181,50 +185,52 @@ def tile_multiheadlatentattention_pa_t_kernel(
                 )
                 m2[n, h] = t
 
-        def half(n):
-            t = sb.tile([P, 2, GRP], F32, name="qt")
-            for h in range(2):
-                nc.scalar.activation(out=t[:, h, :], in_=m2[n, h][:], func=IDENT, bias=bu[:, h, 0:1])
-            qt[n] = t
+        def half(n, h, lo=0):
+            if n not in qt:
+                qt[n] = sb.tile([P, 2, GRP], F32, name="qt", bufs=4)
+            nc.scalar.activation(out=qt[n][:, h, lo:GRP], in_=m2[n, h][:, lo:GRP], func=IDENT, bias=bu[:, h, 0:1])
 
-        def products_gpsimd(n, a, after_quant):
-            if after_quant:
-                t = sb.tile([P, 2, 2, HG], F32, name="slot%d" % ((n + 1) % SLOTS), bufs=1, align_bytes=64)
-            else:
-                t = sb.tile([P, 2, 2, HG], F32, name="prod", bufs=4)
+        def product_tile(n, a, behind):
+            if (n, a) not in prod:
+                if behind is None:
+                    t = sb.tile([P, 2, 2, HG], F32, name="prod", bufs=4, align_bytes=64)
+                else:
+                    t = sb.tile([P, 2, 2, HG], F32, name="slot%d" % (behind % SLOTS), bufs=1, align_bytes=64)
+                prod[n, a] = t
+            return prod[n, a]
+
+        def products_gpsimd(n, a, lo, behind=None):
+            cols = slice(a * HG + lo, (a + 1) * HG)
             nc.gpsimd.tensor_tensor(
-                out=t[:],
-                in0=qt[n][:, :, a * HG : (a + 1) * HG].unsqueeze(2).to_broadcast([P, 2, 2, HG]),
-                in1=tab[n // B][:, a, :, :, :],
+                out=product_tile(n, a, behind)[:, :, :, lo:HG],
+                in0=qt[n][:, :, cols].unsqueeze(2).to_broadcast([P, 2, 2, HG - lo]),
+                in1=tab[n // B][:, :, :, cols],
                 op=MULT,
             )
-            prod[n, a] = t
 
-        def products_vector(n, a, h):
-            if h == 0:
-                prod[n, a] = sb.tile([P, 2, 2, HG], F32, name="prod", bufs=4)
+        def products_vector(n, a, h, hi):
+            cols = slice(a * HG, a * HG + hi)
             nc.vector.scalar_tensor_tensor(
-                out=prod[n, a][:, h, :, :],
-                in0=m2[n, h][:, a * HG : (a + 1) * HG].unsqueeze(1).to_broadcast([P, 2, HG]),
+                out=product_tile(n, a, None)[:, h, :, 0:hi],
+                in0=m2[n, h][:, cols].unsqueeze(1).to_broadcast([P, 2, hi]),
                 scalar=bu[:, h, 0:1],
-                in1=tab[n // B][:, a, h, :, :],
+                in1=tab[n // B][:, h, :, cols],
                 op0=ADD,
                 op1=MULT,
             )
 
         def emit(n, j, copy, store):
             if j == 0:
-                osb[n] = sb.tile([P, 4, J, P], F32, name="osb", bufs=3)
+                osb[n] = sb.tile([P, 4, J, P], F32, name="osb", bufs=4)
             o = bank("s", [P, 4, P], F32)
-            a, jj = divmod(j, 2)
-            cols = slice(jj * P, (jj + 1) * P)
+            cols = slice(j * P, (j + 1) * P)
             for h in range(2):
-                nc.tensor.transpose(o[:, h, :], qt[n][:, h, j * P : (j + 1) * P], idf[:])
+                nc.tensor.transpose(o[:, h, :], qt[n][:, h, cols], idf[:])
             for i in range(2):
                 for h in range(2):
                     nc.tensor.matmul(
                         o[:, 2 + i, :],
-                        lhsT=prod[n, a][:, h, i, cols],
+                        lhsT=prod[n, j // 2][:, h, i, (j % 2) * P : (j % 2 + 1) * P],
                         rhs=idf[:],
                         start=h == 0,
                         stop=h == 1,
@@ -240,16 +246,65 @@ def tile_multiheadlatentattention_pa_t_kernel(
                     in_=osb[n][:, :, js, :].rearrange("p h j d -> p h (j d)"),
                 )
 
+        def store_part(n, heads, a):
+            pg, b = divmod(n, B)
+            rows = out[b, heads, pg * GRP : (pg + 1) * GRP, :].rearrange("h (p j) d -> p h j d", j=J)
+            nc.sync.dma_start(
+                out=rows[:, :, 2 * a : 2 * a + 2, :].rearrange("p h j d -> p h (j d)"),
+                in_=osb[n][:, heads, 2 * a : 2 * a + 2, :].rearrange("p h j d -> p h (j d)"),
+            )
+
+        def up_tokens(n):
+            osb[n] = sb.tile([P, 4, J, P], F32, name="osb", bufs=4)
+            for a in range(2):
+                t = bank("v", [P, 2, HALF], F32)
+                for jj in range(2):
+                    cols = slice((2 * a + jj) * P, (2 * a + jj + 1) * P)
+                    nc.tensor.matmul_mx(
+                        out=t[:, jj, :],
+                        lhsT=codes[n][:, 1, cols].bitcast(FP8X4),
+                        lhsT_scale=scales[n][:, 1, cols],
+                        rhs=wuc[:].bitcast(FP8X4),
+                        rhs_scale=wus[:],
+                        start=True,
+                        stop=True,
+                    )
+                m3[n, a] = t
+
+        def plain(n, a):
+            nc.vector.tensor_tensor(
+                out=osb[n][:, 0:2, 2 * a : 2 * a + 2, :],
+                in0=m3[n, a][:].rearrange("p j (h d) -> p h j d", h=2),
+                in1=bias_row[:].rearrange("p (h d) -> p h d", h=2).unsqueeze(2).to_broadcast([P, 2, 2, P]),
+                op=ADD,
+            )
+            store_part(n, slice(0, 2), a)
+
+        def rotated(n, a):
+            o = bank("s", [P, 2, 2, P], F32)
+            for jj in range(2):
+                for i in range(2):
+                    for h in range(2):
+                        nc.tensor.matmul(
+                            o[:, i, jj, :],
+                            lhsT=prod[n, a][:, h, i, jj * P : (jj + 1) * P],
+                            rhs=idf[:],
+                            start=h == 0,
+                            stop=h == 1,
+                            is_transpose=True,
+                        )
+            nc.scalar.copy(out=osb[n][:, 2:4, 2 * a : 2 * a + 2, :], in_=o[:])
+            store_part(n, slice(2, 4), a)
+
         def table(pg):
-            t = keep.tile([P, 2, 2, 2, HG], BF16, name="tab%d" % pg)
-            o = bank("s", [P, 2, J, P], BF16)
+            t = keep.tile([P, 2, 2, GRP], BF16, name="tab%d" % pg)
+            o = bank("s", [P, 2, GRP], BF16)
             for i in range(2):
                 for j in range(J):
-                    nc.tensor.transpose(o[:, i, j, :], rope[i, pg // 2][:, pg % 2, j, :], idb[:])
-            halves = o[:].rearrange("p i (a j) c -> p a i (j c)", a=2)
-            nc.scalar.copy(out=t[:, :, 0, :, :], in_=halves)
-            nc.scalar.activation(out=t[:, :, 1, 0, :], in_=halves[:, :, 1, :], func=COPY, scale=-1.0)
-            nc.scalar.copy(out=t[:, :, 1, 1, :], in_=halves[:, :, 0, :])
+                    nc.tensor.transpose(o[:, i, j * P : (j + 1) * P], rope[i, pg // 2][:, pg % 2, j, :], idb[:])
+            nc.scalar.copy(out=t[:, 0, :, :], in_=o[:])
+            nc.scalar.activation(out=t[:, 1, 0, :], in_=o[:, 1, :], func=COPY, scale=-1.0)
+            nc.scalar.copy(out=t[:, 1, 1, :], in_=o[:, 0, :])
             tab[pg] = t
 
         def turn_weights(w, g, pairs):
@@ -266,70 +321,119 @@ def tile_multiheadlatentattention_pa_t_kernel(
             return 0 <= n < NG
 
         last = NG - 1
-        for s in range(-3, NG + 1):
-            spare = s >= last - 1
-            if ok(s - 2) and s <= last - 1:
-                products_gpsimd(s - 2, 1, True)
-            if ok(s + 1):
-                scale(s + 1, 1)
-            if ok(s):
-                down(s, 0)
+        on_scalar = nc.scalar.copy
+        for s in range(-4, last - 1):
+            if ok(s - 2):
+                products_gpsimd(s - 2, 1, 0, s - 1)
             if ok(s - 1):
                 up(s - 1)
-            if ok(s):
-                for j in range(1, J):
-                    down(s, j)
-            if ok(s - 1):
-                half(s - 1)
-                if not spare:
-                    products_gpsimd(s - 1, 0, False)
-                elif s <= last:
-                    products_gpsimd(s - 1, 1, False)
+                half(s - 1, 0)
+                half(s - 1, 1)
             if ok(s):
                 lat(s, 0)
                 lat(s, 1)
-            if spare:
-                products_vector(s - 1, 0, 0)
+            if ok(s + 2):
+                scale(s + 2, 1)
+            share = SHARE if ok(s + 3) else HG
+            if ok(s - 1) and share < HG:
+                products_vector(s - 1, 0, 0, share)
+                products_vector(s - 1, 0, 1, share)
+                products_gpsimd(s - 1, 0, share)
+            if ok(s - 1) and share == HG:
+                products_vector(s - 1, 0, 0, share)
+            if ok(s - 2):
+                emit(s - 2, 0, on_scalar, J)
             if ok(s):
+                down(s, 2)
+                down(s, 3)
                 lat(s, 2)
                 lat(s, 3)
-            if spare:
-                products_vector(s - 1, 0, 1)
-            if s > last:
-                products_vector(s - 1, 1, 0)
-                products_vector(s - 1, 1, 1)
-            if ok(s + 2):
-                turn(s + 2, 0)
+            if ok(s - 1) and share == HG:
+                products_vector(s - 1, 0, 1, share)
+            if ok(s + 3) and s >= -3:
+                cast(s + 3, 1)
             if ok(s + 3):
-                cast(s + 3)
-            if s in (0, 1):
-                table(2 * s)
-                table(2 * s + 1)
+                turn(s + 3, 0)
+                scale(s + 3, 0)
             if ok(s - 2):
-                for j in range(J if s <= last - 1 else 0):
-                    emit(s - 2, j, nc.scalar.copy, J)
-                for j in range(2 if s == last else J, J):
-                    emit(s - 2, j, nc.scalar.copy, J)
-            if s == last - 1:
-                for j in range(2):
-                    emit(s - 1, j, nc.scalar.copy, J)
-            if s == last:
-                for j in range(J):
-                    emit(s - 1, j, nc.scalar.copy, J)
-            if s > last:
-                for j in range(J):
-                    emit(s - 1, j, nc.vector.tensor_copy if j == J - 1 else nc.scalar.copy, 2)
-            if ok(s + 2):
-                turn(s + 2, 1)
-            if s == -2:
-                turn_weights(wd, wdg, 2)
+                emit(s - 2, 1, on_scalar, J)
+            if ok(s - 2):
+                emit(s - 2, 2, on_scalar, J)
+            for pg in {-1: (0,), 0: (1, 2), 1: (3,)}.get(s, ()):
+                table(pg)
             if s == -1:
                 turn_weights(wu, wug, 1)
-            if ok(s + 2):
-                scale(s + 2, 0)
-            if s == -1:
+            if ok(s + 1) and s >= 0:
+                down(s + 1, 0)
+                down(s + 1, 1)
+            if ok(s + 4):
+                cast(s + 4, 0)
+            if ok(s - 2):
+                emit(s - 2, 3, on_scalar, J)
+            if ok(s + 3):
+                turn(s + 3, 1)
+            if s == -3:
+                turn_weights(wd, wdg, 2)
+            if s == -2:
                 quant_weights(wdg, wdc, wds)
             if s == 0:
                 quant_weights(wug, wuc, wus)
-            if -1 <= s <= last:
+            if s >= -2:
                 quant(s)
+            if s == -2:
+                down(0, 0)
+                down(0, 1)
+
+        s = last - 1
+        products_gpsimd(s - 2, 1, 0, s - 1)
+        up(s - 1)
+        lat(s, 0)
+        lat(s, 1)
+        down(s, 2)
+        down(s, 3)
+        half(s - 1, 1)
+        products_vector(s - 1, 0, 0, HG)
+        half(s - 1, 0)
+        products_gpsimd(s - 1, 1, 0)
+        lat(s, 2)
+        products_vector(s - 1, 0, 1, HG)
+        emit(s - 2, 0, on_scalar, 2)
+        emit(s - 2, 1, on_scalar, 2)
+        lat(s, 3)
+        down(last, 0)
+        down(last, 1)
+        lat(last, 0)
+        lat(last, 1)
+        emit(s - 2, 2, on_scalar, 2)
+        down(last, 2)
+        down(last, 3)
+        lat(last, 2)
+        quant(s)
+        lat(last, 3)
+        emit(s - 2, 3, on_scalar, 2)
+        emit(s - 1, 0, on_scalar, 2)
+        emit(s - 1, 1, on_scalar, 2)
+        up(s)
+        up_tokens(s)
+        products_vector(s, 0, 0, HG)
+        quant(last)
+        half(s, 1, HG)
+        half(s, 0, HG)
+        products_vector(s, 0, 1, HG)
+        products_gpsimd(s, 1, 0, last)
+        emit(s - 1, 2, on_scalar, 2)
+        up(last)
+        up_tokens(last)
+        plain(s, 0)
+        products_vector(last, 0, 0, HG)
+        products_vector(last, 0, 1, HG)
+        emit(s - 1, 3, on_scalar, 2)
+        rotated(s, 0)
+        plain(s, 1)
+        products_vector(last, 1, 0, HG)
+        products_vector(last, 1, 1, HG)
+        rotated(s, 1)
+        rotated(last, 0)
+        plain(last, 0)
+        plain(last, 1)
+        rotated(last, 1)

@@ -24,9 +24,8 @@ GRP = P * J
 HG = GRP // 2
 PG = S // GRP
 NG = B * PG
-RING = 4
 SLOTS = 4
-SHARE = 48
+SHARE = 32
 
 
 def tile_multiheadlatentattention_pa_t_kernel(
@@ -39,10 +38,11 @@ def tile_multiheadlatentattention_pa_t_kernel(
         ps = ctx.enter_context(tc.psum_pool(name="ps", bufs=1))
         ctx.enter_context(tc.manual_schedule())
 
-        used = {"v": 0, "s": 0}
+        used = {"v": 0, "m": 0, "o": 0}
+        depth = {"v": 4, "m": 2, "o": 2}
 
         def bank(ring, shape, dtype):
-            i = used[ring] % RING
+            i = used[ring] % depth[ring]
             used[ring] = used[ring] + 1
             return ps.tile(shape, dtype, name="bank_%s%d" % (ring, i))
 
@@ -71,9 +71,9 @@ def tile_multiheadlatentattention_pa_t_kernel(
         load_x(0, 2)
         sc = keep.tile([P, T4], F32, name="sc")
         nc.sync.dma_start(out=sc[:], in_=x_scale.rearrange("a b (p t) -> p (a b t)", t=T4))
+        load_x(1, 1)
         wd = keep.tile([P, T4, H], BF16, name="wd", align_bytes=64)
         nc.sync.dma_start(out=wd[:], in_=wq_down.rearrange("(m t) k -> m t k", t=T4))
-        load_x(1, 1)
         bd = keep.tile([P, T4], BF16, name="bd")
         nc.sync.dma_start(out=bd[:], in_=bq_down.rearrange("(p t) -> p t", t=T4))
         load_x(2, 1)
@@ -106,11 +106,11 @@ def tile_multiheadlatentattention_pa_t_kernel(
 
         xbf, xt, grouped, codes, scales, m1, m2, m3, qt, prod, tab, osb = ({} for i in range(12))
 
-        def cast(n, h):
+        def cast(m):
             t = sb.tile([P, 2, H], BF16, name="xbf", bufs=4, align_bytes=64)
-            copy = nc.vector.tensor_copy if (n, h) == (0, 0) else nc.scalar.copy
-            copy(out=t[:], in_=xb[n][:, 2 * h : 2 * h + 2, :].bitcast(FP8))
-            xbf[n, h] = t
+            copy = nc.vector.tensor_copy if m == 0 else nc.scalar.copy
+            copy(out=t[:], in_=xb[m // 2][:, 2 * (m % 2) : 2 * (m % 2) + 2, :].bitcast(FP8))
+            xbf[m] = t
 
         def turn_words(ring, words):
             t = bank(ring, [P, 2, 2 * P], F32)
@@ -119,52 +119,53 @@ def tile_multiheadlatentattention_pa_t_kernel(
                     nc.tensor.transpose(t[:, u, jj * P : (jj + 1) * P], words[:, jj, u : H // 2 : 2], idf[:])
             return t
 
-        def turn(n, h):
-            xt[n, h] = turn_words("v", xbf[n, h][:].bitcast(F32))
+        def turn(m):
+            xt[m] = turn_words("v", xbf[m][:].bitcast(F32))
 
-        def scale(n, h):
-            s = n - 2
-            if h == 0:
-                grouped[s] = sb.tile([P, 2, GRP, T4], BF16, name="slot%d" % (s % SLOTS), bufs=1, align_bytes=64)
+        def staging(s):
+            if s not in grouped:
+                grouped[s] = sb.tile([P, 2 * GRP, T4], BF16, name="slot%d" % (s % SLOTS), bufs=1, align_bytes=64)
+            return grouped[s]
+
+        def scale(m):
+            s, pos = divmod(m - 3, 2)
             nc.vector.tensor_tensor(
-                out=grouped[s][:, 0, h * HG : (h + 1) * HG, :].rearrange("p r (u e) -> p r u e", e=2),
-                in0=xt[n, h][:].bitcast(BF16).rearrange("p u (r e) -> p r u e", e=2),
+                out=staging(s)[:, pos * HG : (pos + 1) * HG, :].rearrange("p r (u e) -> p r u e", e=2),
+                in0=xt[m][:].bitcast(BF16).rearrange("p u (r e) -> p r u e", e=2),
                 in1=sc[:].rearrange("p (u e) -> p u e", e=2).unsqueeze(1).to_broadcast([P, HG, 2, 2]),
                 op=MULT,
             )
 
-        def quant(s):
-            c = sb.tile([P, 2, GRP], U32, name="codes", bufs=3, align_bytes=64)
-            z = sb.tile([P, 2, GRP], U8, name="scales", bufs=3, align_bytes=64)
-            part = slice(0 if s + 2 < NG else 1, 2 if s >= 0 else 1)
+        def quant(s, lo, hi):
+            if s not in codes:
+                codes[s] = sb.tile([P, 2 * GRP], U32, name="codes", bufs=3, align_bytes=64)
+                scales[s] = sb.tile([P, 2 * GRP], U8, name="scales", bufs=3, align_bytes=64)
             nc.vector.quantize_mx(
-                out=c[:, part, :].rearrange("p a r -> p (a r)").bitcast(FP8X4),
-                scales=z[:, part, :].rearrange("p a r -> p (a r)"),
-                in_=grouped[s][:, part, :, :].rearrange("p a r t -> p (a r t)"),
+                out=codes[s][:, lo:hi].bitcast(FP8X4),
+                scales=scales[s][:, lo:hi],
+                in_=grouped[s][:, lo:hi, :].rearrange("p r t -> p (r t)"),
             )
-            codes[s], scales[s] = c, z
 
         def down(n, j):
             t = bank("v", [P, T4, P], F32)
-            cols = slice(j * P, (j + 1) * P)
+            s, pos = divmod(2 * n + j // 2 - 3, 2)
+            cols = slice(pos * HG + (j % 2) * P, pos * HG + (j % 2 + 1) * P)
             for k in range(T4):
                 ws = slice(k * P, (k + 1) * P)
                 nc.tensor.matmul_mx(
                     out=t[:, k, :],
                     lhsT=wdc[:, ws].bitcast(FP8X4),
                     lhsT_scale=wds[:, ws],
-                    rhs=codes[n - 2][:, 0, cols].bitcast(FP8X4),
-                    rhs_scale=scales[n - 2][:, 0, cols],
+                    rhs=codes[s][:, cols].bitcast(FP8X4),
+                    rhs_scale=scales[s][:, cols],
                     start=True,
                     stop=True,
                 )
             m1[n, j] = t
 
         def lat(n, j):
-            if n not in grouped:
-                grouped[n] = sb.tile([P, 2, GRP, T4], BF16, name="slot%d" % (n % SLOTS), bufs=1, align_bytes=64)
             nc.vector.tensor_tensor(
-                out=grouped[n][:, 1, j * P : (j + 1) * P, :],
+                out=staging(n)[:, GRP + j * P : GRP + (j + 1) * P, :],
                 in0=m1[n, j][:].rearrange("p t r -> p r t"),
                 in1=bd[:].unsqueeze(1).to_broadcast([P, P, T4]),
                 op=ADD,
@@ -172,14 +173,14 @@ def tile_multiheadlatentattention_pa_t_kernel(
 
         def up(n):
             for h in range(2):
-                t = bank("s", [P, GRP], F32)
+                t = bank("m", [P, GRP], F32)
                 ws = slice(h * P, (h + 1) * P)
                 nc.tensor.matmul_mx(
                     out=t[:],
                     lhsT=wuc[:, ws].bitcast(FP8X4),
                     lhsT_scale=wus[:, ws],
-                    rhs=codes[n][:, 1, :].bitcast(FP8X4),
-                    rhs_scale=scales[n][:, 1, :],
+                    rhs=codes[n][:, GRP : 2 * GRP].bitcast(FP8X4),
+                    rhs_scale=scales[n][:, GRP : 2 * GRP],
                     start=True,
                     stop=True,
                 )
@@ -222,7 +223,7 @@ def tile_multiheadlatentattention_pa_t_kernel(
         def emit(n, j, copy, store):
             if j == 0:
                 osb[n] = sb.tile([P, 4, J, P], F32, name="osb", bufs=4)
-            o = bank("s", [P, 4, P], F32)
+            o = bank("o", [P, 4, P], F32)
             cols = slice(j * P, (j + 1) * P)
             for h in range(2):
                 nc.tensor.transpose(o[:, h, :], qt[n][:, h, cols], idf[:])
@@ -259,11 +260,11 @@ def tile_multiheadlatentattention_pa_t_kernel(
             for a in range(2):
                 t = bank("v", [P, 2, HALF], F32)
                 for jj in range(2):
-                    cols = slice((2 * a + jj) * P, (2 * a + jj + 1) * P)
+                    cols = slice(GRP + (2 * a + jj) * P, GRP + (2 * a + jj + 1) * P)
                     nc.tensor.matmul_mx(
                         out=t[:, jj, :],
-                        lhsT=codes[n][:, 1, cols].bitcast(FP8X4),
-                        lhsT_scale=scales[n][:, 1, cols],
+                        lhsT=codes[n][:, cols].bitcast(FP8X4),
+                        lhsT_scale=scales[n][:, cols],
                         rhs=wuc[:].bitcast(FP8X4),
                         rhs_scale=wus[:],
                         start=True,
@@ -281,7 +282,7 @@ def tile_multiheadlatentattention_pa_t_kernel(
             store_part(n, slice(0, 2), a)
 
         def rotated(n, a):
-            o = bank("s", [P, 2, 2, P], F32)
+            o = bank("o", [P, 2, 2, P], F32)
             for jj in range(2):
                 for i in range(2):
                     for h in range(2):
@@ -298,7 +299,7 @@ def tile_multiheadlatentattention_pa_t_kernel(
 
         def table(pg):
             t = keep.tile([P, 2, 2, GRP], BF16, name="tab%d" % pg)
-            o = bank("s", [P, 2, GRP], BF16)
+            o = bank("o", [P, 2, GRP], BF16)
             for i in range(2):
                 for j in range(J):
                     nc.tensor.transpose(o[:, i, j * P : (j + 1) * P], rope[i, pg // 2][:, pg % 2, j, :], idb[:])
@@ -309,7 +310,7 @@ def tile_multiheadlatentattention_pa_t_kernel(
 
         def turn_weights(w, g, pairs):
             for h in range(pairs):
-                t = turn_words("s", w[:, 2 * h : 2 * h + 2, :].bitcast(F32))
+                t = turn_words("o", w[:, 2 * h : 2 * h + 2, :].bitcast(F32))
                 nc.scalar.copy(
                     out=g[:, h * 2 * P : (h + 1) * 2 * P, :].bitcast(F32), in_=t[:].rearrange("p u r -> p r u")
                 )
@@ -322,118 +323,126 @@ def tile_multiheadlatentattention_pa_t_kernel(
 
         last = NG - 1
         on_scalar = nc.scalar.copy
-        for s in range(-4, last - 1):
+
+        cast(0)
+        cast(1)
+        turn(0)
+        scale(0)
+        turn(1)
+        scale(1)
+        cast(2)
+        turn(2)
+        scale(2)
+        cast(3)
+        turn_weights(wd, wdg, 2)
+        turn(3)
+        cast(4)
+        quant_weights(wdg, wdc, wds)
+        quant(-2, HG, GRP)
+        quant(-1, 0, GRP)
+        table(0)
+        table(1)
+        down(0, 0)
+        down(0, 1)
+        turn_weights(wu, wug, 1)
+        cast(5)
+
+        for s in range(last - 1):
             if ok(s - 2):
                 products_gpsimd(s - 2, 1, 0, s - 1)
             if ok(s - 1):
                 up(s - 1)
                 half(s - 1, 0)
                 half(s - 1, 1)
-            if ok(s):
-                lat(s, 0)
-                lat(s, 1)
-            if ok(s + 2):
-                scale(s + 2, 1)
-            share = SHARE if ok(s + 3) else HG
-            if ok(s - 1) and share < HG:
-                products_vector(s - 1, 0, 0, share)
-                products_vector(s - 1, 0, 1, share)
-                products_gpsimd(s - 1, 0, share)
-            if ok(s - 1) and share == HG:
-                products_vector(s - 1, 0, 0, share)
+                products_gpsimd(s - 1, 0, SHARE)
+            if s == 0:
+                scale(3)
+            lat(s, 0)
+            lat(s, 1)
+            if s > 0:
+                scale(2 * s + 3)
+            turn(2 * s + 4)
+            scale(2 * s + 4)
             if ok(s - 2):
-                emit(s - 2, 0, on_scalar, J)
-            if ok(s):
-                down(s, 2)
-                down(s, 3)
-                lat(s, 2)
-                lat(s, 3)
-            if ok(s - 1) and share == HG:
-                products_vector(s - 1, 0, 1, share)
-            if ok(s + 3) and s >= -3:
-                cast(s + 3, 1)
-            if ok(s + 3):
-                turn(s + 3, 0)
-                scale(s + 3, 0)
+                emit(s - 2, 0, on_scalar, 2)
+            down(s, 2)
+            down(s, 3)
+            lat(s, 2)
+            lat(s, 3)
+            if ok(s - 1):
+                products_vector(s - 1, 0, 0, SHARE)
+                products_vector(s - 1, 0, 1, SHARE)
+            if s > 0:
+                cast(2 * s + 5)
+            if s == 0:
+                table(2)
             if ok(s - 2):
-                emit(s - 2, 1, on_scalar, J)
+                emit(s - 2, 1, on_scalar, 2)
+                emit(s - 2, 2, on_scalar, 2)
+            down(s + 1, 0)
+            down(s + 1, 1)
+            if 2 * s + 6 < 2 * NG:
+                cast(2 * s + 6)
+            if s == 0:
+                table(3)
             if ok(s - 2):
-                emit(s - 2, 2, on_scalar, J)
-            for pg in {-1: (0,), 0: (1, 2), 1: (3,)}.get(s, ()):
-                table(pg)
-            if s == -1:
-                turn_weights(wu, wug, 1)
-            if ok(s + 1) and s >= 0:
-                down(s + 1, 0)
-                down(s + 1, 1)
-            if ok(s + 4):
-                cast(s + 4, 0)
-            if ok(s - 2):
-                emit(s - 2, 3, on_scalar, J)
-            if ok(s + 3):
-                turn(s + 3, 1)
-            if s == -3:
-                turn_weights(wd, wdg, 2)
-            if s == -2:
-                quant_weights(wdg, wdc, wds)
+                emit(s - 2, 3, on_scalar, 2)
+            turn(2 * s + 5)
             if s == 0:
                 quant_weights(wug, wuc, wus)
-            if s >= -2:
-                quant(s)
-            if s == -2:
-                down(0, 0)
-                down(0, 1)
+            quant(s, 0, 2 * GRP)
 
         s = last - 1
         products_gpsimd(s - 2, 1, 0, s - 1)
         up(s - 1)
+        half(s - 1, 0)
+        half(s - 1, 1)
+        products_gpsimd(s - 1, 0, 0)
         lat(s, 0)
         lat(s, 1)
+        scale(2 * NG - 1)
+        emit(s - 2, 0, on_scalar, 2)
         down(s, 2)
         down(s, 3)
-        half(s - 1, 1)
-        products_vector(s - 1, 0, 0, HG)
-        half(s - 1, 0)
-        products_gpsimd(s - 1, 1, 0)
         lat(s, 2)
-        products_vector(s - 1, 0, 1, HG)
-        emit(s - 2, 0, on_scalar, 2)
-        emit(s - 2, 1, on_scalar, 2)
         lat(s, 3)
+        emit(s - 2, 1, on_scalar, 2)
         down(last, 0)
         down(last, 1)
         lat(last, 0)
         lat(last, 1)
         emit(s - 2, 2, on_scalar, 2)
+        emit(s - 2, 3, on_scalar, 2)
+        quant(s, 0, HG)
+        quant(s, GRP, 2 * GRP)
+        products_gpsimd(s - 1, 1, 0, s)
         down(last, 2)
         down(last, 3)
+        up(s)
         lat(last, 2)
-        quant(s)
         lat(last, 3)
-        emit(s - 2, 3, on_scalar, 2)
+        products_vector(s, 0, 0, HG)
+        half(s, 1, HG)
+        products_vector(s, 0, 1, HG)
+        half(s, 0, HG)
         emit(s - 1, 0, on_scalar, 2)
         emit(s - 1, 1, on_scalar, 2)
-        up(s)
         up_tokens(s)
-        products_vector(s, 0, 0, HG)
-        quant(last)
-        half(s, 1, HG)
-        half(s, 0, HG)
-        products_vector(s, 0, 1, HG)
+        quant(last, GRP, 2 * GRP)
         products_gpsimd(s, 1, 0, last)
-        emit(s - 1, 2, on_scalar, 2)
-        up(last)
-        up_tokens(last)
         plain(s, 0)
+        rotated(s, 0)
+        up(last)
+        plain(s, 1)
+        emit(s - 1, 2, on_scalar, 2)
+        emit(s - 1, 3, on_scalar, 2)
         products_vector(last, 0, 0, HG)
         products_vector(last, 0, 1, HG)
-        emit(s - 1, 3, on_scalar, 2)
-        rotated(s, 0)
-        plain(s, 1)
         products_vector(last, 1, 0, HG)
         products_vector(last, 1, 1, HG)
-        rotated(s, 1)
+        up_tokens(last)
         rotated(last, 0)
+        rotated(s, 1)
         plain(last, 0)
         plain(last, 1)
         rotated(last, 1)

@@ -25,7 +25,7 @@ HG = GRP // 2
 PG = S // GRP
 NG = B * PG
 SLOTS = 4
-SHARE = 32
+SHARE = 64
 
 
 def tile_multiheadlatentattention_pa_t_kernel(

@@ -25,7 +25,6 @@ HG = GRP // 2
 PG = S // GRP
 NG = B * PG
 SLOTS = 4
-SHARE = 64
 
 
 def tile_multiheadlatentattention_pa_t_kernel(
@@ -38,8 +37,8 @@ def tile_multiheadlatentattention_pa_t_kernel(
         ps = ctx.enter_context(tc.psum_pool(name="ps", bufs=1))
         ctx.enter_context(tc.manual_schedule())
 
-        used = {"v": 0, "m": 0, "o": 0}
-        depth = {"v": 4, "m": 2, "o": 2}
+        used = {"v": 0, "o": 0}
+        depth = {"v": 3, "o": 5}
 
         def bank(ring, shape, dtype):
             i = used[ring] % depth[ring]
@@ -48,14 +47,13 @@ def tile_multiheadlatentattention_pa_t_kernel(
 
         xb = {}
 
-        def load_x(n, parts):
+        def load_x(n, cuts):
             pg, b = divmod(n, B)
             rows = x_bytes[b, pg * GRP : (pg + 1) * GRP, :].rearrange("(p j) k -> p j k", j=J)
-            t = sb.tile([P, J, H], U8, name="xbytes", bufs=NG, align_bytes=64)
-            w = J // parts
-            for i in range(parts):
-                nc.sync.dma_start(out=t[:, i * w : (i + 1) * w, :], in_=rows[:, i * w : (i + 1) * w, :])
-            xb[n] = t
+            if n not in xb:
+                xb[n] = sb.tile([P, J, H], U8, name="xbytes", bufs=NG, align_bytes=64)
+            for lo, hi in zip(cuts, cuts[1:]):
+                nc.sync.dma_start(out=xb[n][:, lo:hi, :], in_=rows[:, lo:hi, :])
 
         rope = {}
 
@@ -68,27 +66,29 @@ def tile_multiheadlatentattention_pa_t_kernel(
                 )
                 rope[i, pair] = t
 
-        load_x(0, 2)
+        load_x(0, (0, 1, 2, J))
         sc = keep.tile([P, T4], F32, name="sc")
         nc.sync.dma_start(out=sc[:], in_=x_scale.rearrange("a b (p t) -> p (a b t)", t=T4))
-        load_x(1, 1)
         wd = keep.tile([P, T4, H], BF16, name="wd", align_bytes=64)
-        nc.sync.dma_start(out=wd[:], in_=wq_down.rearrange("(m t) k -> m t k", t=T4))
+        wd_rows = wq_down.rearrange("(m t) k -> m t k", t=T4)
+        load_x(1, (0, 2))
+        nc.sync.dma_start(out=wd[:, 0:2, :], in_=wd_rows[:, 0:2, :])
+        nc.sync.dma_start(out=wd[:, 2:4, :], in_=wd_rows[:, 2:4, :])
+        load_x(1, (2, J))
         bd = keep.tile([P, T4], BF16, name="bd")
         nc.sync.dma_start(out=bd[:], in_=bq_down.rearrange("(p t) -> p t", t=T4))
-        load_x(2, 1)
+        load_x(2, (0, J))
+        load_rope(0)
         wu = keep.tile([P, 2, LAT], BF16, name="wu", align_bytes=64)
         nc.sync.dma_start(out=wu[:], in_=wq_up.rearrange("(h m) k -> m h k", h=2))
-        load_rope(0)
-        load_x(3, 1)
+        load_x(3, (0, J))
+        load_rope(1)
         bu = keep.tile([P, 2, 2], BF16, name="bu")
         with nc.allow_non_contiguous_dma(reason="one bias value for each partition and half"):
             nc.sync.dma_start(out=bu[:, :, 0:1], in_=bq_up.rearrange("(h c o) -> c h o", h=2, o=1))
-        load_x(4, 1)
-        load_rope(1)
+        load_x(4, (0, J))
         for n in range(5, NG):
-            load_x(n, 1)
-
+            load_x(n, (0, J))
         bias_row = keep.tile([P, HALF], BF16, name="bias_row")
         nc.sync.dma_start(out=bias_row[:], in_=bq_up.partition_broadcast(P))
 
@@ -101,208 +101,230 @@ def tile_multiheadlatentattention_pa_t_kernel(
         wds = keep.tile([P, LAT], U8, name="wds", align_bytes=64)
         wuc = keep.tile([P, HALF], U32, name="wuc", align_bytes=64)
         wus = keep.tile([P, HALF], U8, name="wus", align_bytes=64)
-        wdg = keep.tile([P, LAT, T4], BF16, name="wdg", align_bytes=64)
-        wug = keep.tile([P, HALF, T4], BF16, name="wug", align_bytes=64)
+        wdg = sb.tile([P, LAT, T4], BF16, name="slot0", bufs=1, align_bytes=64)
+        wug = sb.tile([P, HALF, T4], BF16, name="slot1", bufs=1, align_bytes=64)
 
-        xbf, xt, grouped, codes, scales, m1, m2, m3, qt, prod, tab, osb = ({} for i in range(12))
+        xbf, xt, staged, codes, scales, m1, m2, m3, planes, qt, prod, tab, osb = ({} for i in range(13))
 
-        def cast(m):
-            t = sb.tile([P, 2, H], BF16, name="xbf", bufs=4, align_bytes=64)
-            copy = nc.vector.tensor_copy if m == 0 else nc.scalar.copy
-            copy(out=t[:], in_=xb[m // 2][:, 2 * (m % 2) : 2 * (m % 2) + 2, :].bitcast(FP8))
-            xbf[m] = t
+        def widen(m, copy, lo=0, hi=2):
+            if lo == 0:
+                xbf[m] = sb.tile([P, 2, H], BF16, name="xbf", bufs=6, align_bytes=64)
+            j = 2 * (m % 2)
+            copy(out=xbf[m][:, lo:hi, :], in_=xb[m // 2][:, j + lo : j + hi, :].bitcast(FP8))
 
         def turn_words(ring, words):
-            t = bank(ring, [P, 2, 2 * P], F32)
-            for jj in range(2):
+            tiles = words.shape[1]
+            t = bank(ring, [P, 2, tiles * P], F32)
+            for jj in range(tiles):
                 for u in range(2):
                     nc.tensor.transpose(t[:, u, jj * P : (jj + 1) * P], words[:, jj, u : H // 2 : 2], idf[:])
             return t
 
-        def turn(m):
-            xt[m] = turn_words("v", xbf[m][:].bitcast(F32))
+        def turn(m, lo=0, hi=2):
+            xt[m, lo] = turn_words("v", xbf[m][:, lo:hi, :].bitcast(F32))
 
         def staging(s):
-            if s not in grouped:
-                grouped[s] = sb.tile([P, 2 * GRP, T4], BF16, name="slot%d" % (s % SLOTS), bufs=1, align_bytes=64)
-            return grouped[s]
+            if s not in staged:
+                staged[s] = sb.tile([P, 2 * GRP, T4], BF16, name="slot%d" % (s % SLOTS), bufs=1, align_bytes=64)
+            return staged[s]
 
-        def scale(m):
-            s, pos = divmod(m - 3, 2)
+        def x_place(m):
+            return divmod(m - 3, 2) if m < 2 * NG - 1 else (NG - 1, 0)
+
+        def q_place(n):
+            return (n, GRP) if n < NG - 1 else (NG - 2, 0)
+
+        def scale(m, lo=0, hi=2):
+            s, pos = x_place(m)
             nc.vector.tensor_tensor(
-                out=staging(s)[:, pos * HG : (pos + 1) * HG, :].rearrange("p r (u e) -> p r u e", e=2),
-                in0=xt[m][:].bitcast(BF16).rearrange("p u (r e) -> p r u e", e=2),
-                in1=sc[:].rearrange("p (u e) -> p u e", e=2).unsqueeze(1).to_broadcast([P, HG, 2, 2]),
+                out=staging(s)[:, pos * HG + lo * P : pos * HG + hi * P, :].rearrange("p r (u e) -> p r u e", e=2),
+                in0=xt[m, lo][:].bitcast(BF16).rearrange("p u (r e) -> p r u e", e=2),
+                in1=sc[:].rearrange("p (u e) -> p u e", e=2).unsqueeze(1).to_broadcast([P, (hi - lo) * P, 2, 2]),
                 op=MULT,
             )
 
         def quant(s, lo, hi):
             if s not in codes:
-                codes[s] = sb.tile([P, 2 * GRP], U32, name="codes", bufs=3, align_bytes=64)
-                scales[s] = sb.tile([P, 2 * GRP], U8, name="scales", bufs=3, align_bytes=64)
+                codes[s] = sb.tile([P, 2 * GRP], U32, name="codes", bufs=4, align_bytes=64)
+                scales[s] = sb.tile([P, 2 * GRP], U8, name="scales", bufs=4, align_bytes=64)
             nc.vector.quantize_mx(
                 out=codes[s][:, lo:hi].bitcast(FP8X4),
                 scales=scales[s][:, lo:hi],
-                in_=grouped[s][:, lo:hi, :].rearrange("p r t -> p (r t)"),
+                in_=staged[s][:, lo:hi, :].rearrange("p r t -> p (r t)"),
+            )
+
+        def down_pass(dst, t, s, cols):
+            ws = slice(t * P, (t + 1) * P)
+            nc.tensor.matmul_mx(
+                out=dst,
+                lhsT=wdc[:, ws].bitcast(FP8X4),
+                lhsT_scale=wds[:, ws],
+                rhs=codes[s][:, cols].bitcast(FP8X4),
+                rhs_scale=scales[s][:, cols],
+                start=True,
+                stop=True,
             )
 
         def down(n, j):
-            t = bank("v", [P, T4, P], F32)
-            s, pos = divmod(2 * n + j // 2 - 3, 2)
-            cols = slice(pos * HG + (j % 2) * P, pos * HG + (j % 2 + 1) * P)
-            for k in range(T4):
-                ws = slice(k * P, (k + 1) * P)
-                nc.tensor.matmul_mx(
-                    out=t[:, k, :],
-                    lhsT=wdc[:, ws].bitcast(FP8X4),
-                    lhsT_scale=wds[:, ws],
-                    rhs=codes[s][:, cols].bitcast(FP8X4),
-                    rhs_scale=scales[s][:, cols],
-                    start=True,
-                    stop=True,
-                )
-            m1[n, j] = t
+            o = bank("v", [P, T4, P], F32)
+            s, pos = x_place(2 * n + j // 2)
+            lo = pos * HG + (j % 2) * P
+            for t in range(T4):
+                down_pass(o[:, t, :], t, s, slice(lo, lo + P))
+            m1[n, j] = o
 
         def lat(n, j):
+            s, lo = q_place(n)
             nc.vector.tensor_tensor(
-                out=staging(n)[:, GRP + j * P : GRP + (j + 1) * P, :],
+                out=staging(s)[:, lo + j * P : lo + (j + 1) * P, :],
                 in0=m1[n, j][:].rearrange("p t r -> p r t"),
                 in1=bd[:].unsqueeze(1).to_broadcast([P, P, T4]),
                 op=ADD,
             )
 
+        def down_planes(n):
+            s, pos = x_place(2 * n)
+            planes[n] = sb.tile([P, T4, HG], BF16, name="planes", bufs=2)
+            for pair in range(2):
+                o = bank("o", [P, 2, HG], F32)
+                for e in range(2):
+                    down_pass(o[:, e, :], 2 * pair + e, s, slice(pos * HG, (pos + 1) * HG))
+                for e in range(2):
+                    t = 2 * pair + e
+                    nc.scalar.activation(out=planes[n][:, t, :], in_=o[:, e, :], func=IDENT, bias=bd[:, t : t + 1])
+
+        def weave(n):
+            nc.gpsimd.tensor_scalar(
+                out=staging(n)[:, GRP : GRP + HG, :],
+                in0=planes[n][:].rearrange("p t r -> p r t"),
+                scalar1=1.0,
+                scalar2=0.0,
+                op0=MULT,
+                op1=ADD,
+            )
+
         def up(n):
+            s, lo = q_place(n)
             for h in range(2):
-                t = bank("m", [P, GRP], F32)
+                o = bank("o", [P, GRP], F32)
                 ws = slice(h * P, (h + 1) * P)
                 nc.tensor.matmul_mx(
-                    out=t[:],
+                    out=o[:],
                     lhsT=wuc[:, ws].bitcast(FP8X4),
                     lhsT_scale=wus[:, ws],
-                    rhs=codes[n][:, GRP : 2 * GRP].bitcast(FP8X4),
-                    rhs_scale=scales[n][:, GRP : 2 * GRP],
+                    rhs=codes[s][:, lo : lo + GRP].bitcast(FP8X4),
+                    rhs_scale=scales[s][:, lo : lo + GRP],
                     start=True,
                     stop=True,
                 )
-                m2[n, h] = t
+                m2[n, h] = o
 
         def half(n, h, lo=0):
             if n not in qt:
                 qt[n] = sb.tile([P, 2, GRP], F32, name="qt", bufs=4)
             nc.scalar.activation(out=qt[n][:, h, lo:GRP], in_=m2[n, h][:, lo:GRP], func=IDENT, bias=bu[:, h, 0:1])
 
-        def product_tile(n, a, behind):
-            if (n, a) not in prod:
-                if behind is None:
-                    t = sb.tile([P, 2, 2, HG], F32, name="prod", bufs=4, align_bytes=64)
-                else:
-                    t = sb.tile([P, 2, 2, HG], F32, name="slot%d" % (behind % SLOTS), bufs=1, align_bytes=64)
-                prod[n, a] = t
-            return prod[n, a]
-
-        def products_gpsimd(n, a, lo, behind=None):
-            cols = slice(a * HG + lo, (a + 1) * HG)
+        def products_gpsimd(n, behind):
+            t = sb.tile([P, 2, 2, HG], F32, name="slot%d" % (behind % SLOTS), bufs=1, align_bytes=64)
             nc.gpsimd.tensor_tensor(
-                out=product_tile(n, a, behind)[:, :, :, lo:HG],
-                in0=qt[n][:, :, cols].unsqueeze(2).to_broadcast([P, 2, 2, HG - lo]),
-                in1=tab[n // B][:, :, :, cols],
+                out=t[:],
+                in0=qt[n][:, :, HG:GRP].unsqueeze(2).to_broadcast([P, 2, 2, HG]),
+                in1=tab[n // B][:, :, :, HG:GRP],
                 op=MULT,
             )
+            prod[n, 1] = t
 
-        def products_vector(n, a, h, hi):
-            cols = slice(a * HG, a * HG + hi)
+        def products_vector(n, a, h, lo=0, hi=HG):
+            if (n, a) not in prod:
+                prod[n, a] = sb.tile([P, 2, 2, HG], F32, name="prod", bufs=4, align_bytes=64)
+            cols = slice(a * HG + lo, a * HG + hi)
             nc.vector.scalar_tensor_tensor(
-                out=product_tile(n, a, None)[:, h, :, 0:hi],
-                in0=m2[n, h][:, cols].unsqueeze(1).to_broadcast([P, 2, hi]),
+                out=prod[n, a][:, h, :, lo:hi],
+                in0=m2[n, h][:, cols].unsqueeze(1).to_broadcast([P, 2, hi - lo]),
                 scalar=bu[:, h, 0:1],
                 in1=tab[n // B][:, h, :, cols],
                 op0=ADD,
                 op1=MULT,
             )
 
-        def emit(n, j, copy, store):
-            if j == 0:
+        def result(n):
+            if n not in osb:
                 osb[n] = sb.tile([P, 4, J, P], F32, name="osb", bufs=4)
-            o = bank("o", [P, 4, P], F32)
-            cols = slice(j * P, (j + 1) * P)
-            for h in range(2):
-                nc.tensor.transpose(o[:, h, :], qt[n][:, h, cols], idf[:])
-            for i in range(2):
-                for h in range(2):
-                    nc.tensor.matmul(
-                        o[:, 2 + i, :],
-                        lhsT=prod[n, j // 2][:, h, i, (j % 2) * P : (j % 2 + 1) * P],
-                        rhs=idf[:],
-                        start=h == 0,
-                        stop=h == 1,
-                        is_transpose=True,
-                    )
-            copy(out=osb[n][:, :, j, :], in_=o[:])
-            if (j + 1) % store == 0:
-                pg, b = divmod(n, B)
-                rows = out[b, :, pg * GRP : (pg + 1) * GRP, :].rearrange("h (p j) d -> p h j d", j=J)
-                js = slice(j + 1 - store, j + 1)
-                nc.sync.dma_start(
-                    out=rows[:, :, js, :].rearrange("p h j d -> p h (j d)"),
-                    in_=osb[n][:, :, js, :].rearrange("p h j d -> p h (j d)"),
-                )
+            return osb[n]
 
-        def store_part(n, heads, a):
+        def store(n, heads, lo, hi):
             pg, b = divmod(n, B)
             rows = out[b, heads, pg * GRP : (pg + 1) * GRP, :].rearrange("h (p j) d -> p h j d", j=J)
             nc.sync.dma_start(
-                out=rows[:, :, 2 * a : 2 * a + 2, :].rearrange("p h j d -> p h (j d)"),
-                in_=osb[n][:, heads, 2 * a : 2 * a + 2, :].rearrange("p h j d -> p h (j d)"),
+                out=rows[:, :, lo:hi, :].rearrange("p h j d -> p h (j d)"),
+                in_=osb[n][:, heads, lo:hi, :].rearrange("p h j d -> p h (j d)"),
             )
 
-        def up_tokens(n):
-            osb[n] = sb.tile([P, 4, J, P], F32, name="osb", bufs=4)
-            for a in range(2):
-                t = bank("v", [P, 2, HALF], F32)
-                for jj in range(2):
-                    cols = slice(GRP + (2 * a + jj) * P, GRP + (2 * a + jj + 1) * P)
-                    nc.tensor.matmul_mx(
-                        out=t[:, jj, :],
-                        lhsT=codes[n][:, cols].bitcast(FP8X4),
-                        lhsT_scale=scales[n][:, cols],
-                        rhs=wuc[:].bitcast(FP8X4),
-                        rhs_scale=wus[:],
-                        start=True,
-                        stop=True,
-                    )
-                m3[n, a] = t
+        def turn_rotated(dst, n, j, i):
+            for h in range(2):
+                nc.tensor.matmul(
+                    dst,
+                    lhsT=prod[n, j // 2][:, h, i, (j % 2) * P : (j % 2 + 1) * P],
+                    rhs=idf[:],
+                    start=h == 0,
+                    stop=h == 1,
+                    is_transpose=True,
+                )
+
+        def emit(n, j):
+            o = bank("o", [P, 4, P], F32)
+            for h in range(2):
+                nc.tensor.transpose(o[:, h, :], qt[n][:, h, j * P : (j + 1) * P], idf[:])
+            for i in range(2):
+                turn_rotated(o[:, 2 + i, :], n, j, i)
+            nc.scalar.copy(out=result(n)[:, :, j, :], in_=o[:])
+            if j % 2:
+                store(n, slice(0, 4), j - 1, j + 1)
+
+        def up_tokens(n, a):
+            s, lo = q_place(n)
+            o = bank("v", [P, 2, HALF], F32)
+            for jj in range(2):
+                cols = slice(lo + (2 * a + jj) * P, lo + (2 * a + jj + 1) * P)
+                nc.tensor.matmul_mx(
+                    out=o[:, jj, :],
+                    lhsT=codes[s][:, cols].bitcast(FP8X4),
+                    lhsT_scale=scales[s][:, cols],
+                    rhs=wuc[:].bitcast(FP8X4),
+                    rhs_scale=wus[:],
+                    start=True,
+                    stop=True,
+                )
+            m3[n, a] = o
 
         def plain(n, a):
             nc.vector.tensor_tensor(
-                out=osb[n][:, 0:2, 2 * a : 2 * a + 2, :],
+                out=result(n)[:, 0:2, 2 * a : 2 * a + 2, :],
                 in0=m3[n, a][:].rearrange("p j (h d) -> p h j d", h=2),
                 in1=bias_row[:].rearrange("p (h d) -> p h d", h=2).unsqueeze(2).to_broadcast([P, 2, 2, P]),
                 op=ADD,
             )
-            store_part(n, slice(0, 2), a)
 
-        def rotated(n, a):
-            o = bank("o", [P, 2, 2, P], F32)
-            for jj in range(2):
+        def rotated(n, lo, hi):
+            o = bank("o", [P, 2, hi - lo, P], F32)
+            for j in range(lo, hi):
                 for i in range(2):
-                    for h in range(2):
-                        nc.tensor.matmul(
-                            o[:, i, jj, :],
-                            lhsT=prod[n, a][:, h, i, jj * P : (jj + 1) * P],
-                            rhs=idf[:],
-                            start=h == 0,
-                            stop=h == 1,
-                            is_transpose=True,
-                        )
-            nc.scalar.copy(out=osb[n][:, 2:4, 2 * a : 2 * a + 2, :], in_=o[:])
-            store_part(n, slice(2, 4), a)
+                    turn_rotated(o[:, i, j - lo, :], n, j, i)
+            nc.scalar.copy(out=result(n)[:, 2:4, lo:hi, :], in_=o[:])
+            store(n, slice(2, 4), lo, hi)
 
         def table(pg):
             t = keep.tile([P, 2, 2, GRP], BF16, name="tab%d" % pg)
             o = bank("o", [P, 2, GRP], BF16)
             for i in range(2):
                 for j in range(J):
-                    nc.tensor.transpose(o[:, i, j * P : (j + 1) * P], rope[i, pg // 2][:, pg % 2, j, :], idb[:])
+                    nc.tensor.matmul(
+                        o[:, i, j * P : (j + 1) * P],
+                        lhsT=rope[i, pg // 2][:, pg % 2, j, :],
+                        rhs=idb[:],
+                        start=True,
+                        stop=True,
+                    )
             nc.scalar.copy(out=t[:, 0, :, :], in_=o[:])
             nc.scalar.activation(out=t[:, 1, 0, :], in_=o[:, 1, :], func=COPY, scale=-1.0)
             nc.scalar.copy(out=t[:, 1, 1, :], in_=o[:, 0, :])
@@ -318,131 +340,142 @@ def tile_multiheadlatentattention_pa_t_kernel(
         def quant_weights(g, c, z):
             nc.vector.quantize_mx(out=c[:].bitcast(FP8X4), scales=z[:], in_=g[:].rearrange("p r t -> p (r t)"))
 
-        def ok(n):
-            return 0 <= n < NG
-
         last = NG - 1
-        on_scalar = nc.scalar.copy
 
-        cast(0)
-        cast(1)
-        turn(0)
-        scale(0)
+        widen(0, nc.scalar.copy, 0, 1)
+        widen(0, nc.scalar.copy, 1, 2)
+        widen(1, nc.scalar.copy)
+        for jj in range(2):
+            turn(0, jj, jj + 1)
+            scale(0, jj, jj + 1)
         turn(1)
         scale(1)
-        cast(2)
+        widen(2, nc.scalar.copy)
         turn(2)
         scale(2)
-        cast(3)
+        widen(3, nc.scalar.copy)
         turn_weights(wd, wdg, 2)
         turn(3)
-        cast(4)
+        widen(4, nc.scalar.copy)
         quant_weights(wdg, wdc, wds)
         quant(-2, HG, GRP)
         quant(-1, 0, GRP)
+        widen(5, nc.scalar.copy)
         table(0)
         table(1)
+        scale(3)
         down(0, 0)
         down(0, 1)
+        widen(6, nc.scalar.copy)
         turn_weights(wu, wug, 1)
-        cast(5)
+        lat(0, 0)
+        turn(4)
+        lat(0, 1)
+        scale(4)
+        down(0, 2)
+        down(0, 3)
+        down_planes(1)
+        widen(7, nc.scalar.copy)
+        lat(0, 2)
+        turn(5)
+        lat(0, 3)
+        turn(6)
+        table(2)
+        quant_weights(wug, wuc, wus)
+        quant(0, 0, 2 * GRP)
+        weave(1)
 
-        for s in range(last - 1):
-            if ok(s - 2):
-                products_gpsimd(s - 2, 1, 0, s - 1)
-            if ok(s - 1):
-                up(s - 1)
-                half(s - 1, 0)
-                half(s - 1, 1)
-                products_gpsimd(s - 1, 0, SHARE)
-            if s == 0:
-                scale(3)
-            lat(s, 0)
-            lat(s, 1)
-            if s > 0:
-                scale(2 * s + 3)
-            turn(2 * s + 4)
-            scale(2 * s + 4)
-            if ok(s - 2):
-                emit(s - 2, 0, on_scalar, 2)
+        for s in range(1, last - 1):
+            if s >= 2:
+                products_gpsimd(s - 2, s - 1)
+            down_planes(s + 1)
+            weave(s + 1)
+            up(s - 1)
+            half(s - 1, 0)
+            half(s - 1, 1)
+            if s == 1:
+                widen(8, nc.scalar.copy)
+            scale(2 * s + 3)
             down(s, 2)
-            down(s, 3)
+            scale(2 * s + 4)
             lat(s, 2)
+            products_vector(s - 1, 0, 0)
+            products_vector(s - 1, 0, 1)
+            if s >= 2:
+                emit(s - 2, 0)
+                emit(s - 2, 1)
+            down(s, 3)
             lat(s, 3)
-            if ok(s - 1):
-                products_vector(s - 1, 0, 0, SHARE)
-                products_vector(s - 1, 0, 1, SHARE)
-            if s > 0:
-                cast(2 * s + 5)
-            if s == 0:
-                table(2)
-            if ok(s - 2):
-                emit(s - 2, 1, on_scalar, 2)
-                emit(s - 2, 2, on_scalar, 2)
-            down(s + 1, 0)
-            down(s + 1, 1)
-            if 2 * s + 6 < 2 * NG:
-                cast(2 * s + 6)
-            if s == 0:
-                table(3)
-            if ok(s - 2):
-                emit(s - 2, 3, on_scalar, 2)
+            if s < last - 2:
+                widen(2 * s + 7, nc.scalar.copy)
             turn(2 * s + 5)
-            if s == 0:
-                quant_weights(wug, wuc, wus)
-            quant(s, 0, 2 * GRP)
+            if s >= 2:
+                emit(s - 2, 2)
+                emit(s - 2, 3)
+            if s == 1:
+                table(3)
+            if s < last - 3:
+                widen(2 * s + 8, nc.scalar.copy)
+            if s < last - 2:
+                turn(2 * s + 6)
+            quant(s, 0, GRP)
+            quant(s, GRP, 2 * GRP)
 
         s = last - 1
-        products_gpsimd(s - 2, 1, 0, s - 1)
+        products_gpsimd(s - 2, s - 1)
+        emit(s - 2, 0)
+        emit(s - 2, 1)
+        scale(2 * NG - 1)
+        down(s, 2)
         up(s - 1)
+        down(s, 3)
         half(s - 1, 0)
         half(s - 1, 1)
-        products_gpsimd(s - 1, 0, 0)
-        lat(s, 0)
-        lat(s, 1)
-        scale(2 * NG - 1)
-        emit(s - 2, 0, on_scalar, 2)
-        down(s, 2)
-        down(s, 3)
         lat(s, 2)
         lat(s, 3)
-        emit(s - 2, 1, on_scalar, 2)
         down(last, 0)
         down(last, 1)
+        products_vector(s - 1, 0, 0)
+        quant(last, 0, HG)
+        products_gpsimd(s - 1, last)
+        products_vector(s - 1, 0, 1)
+        emit(s - 2, 2)
+        emit(s - 2, 3)
+        emit(s - 1, 0)
         lat(last, 0)
-        lat(last, 1)
-        emit(s - 2, 2, on_scalar, 2)
-        emit(s - 2, 3, on_scalar, 2)
-        quant(s, 0, HG)
-        quant(s, GRP, 2 * GRP)
-        products_gpsimd(s - 1, 1, 0, s)
         down(last, 2)
+        lat(last, 1)
         down(last, 3)
-        up(s)
         lat(last, 2)
         lat(last, 3)
-        products_vector(s, 0, 0, HG)
-        half(s, 1, HG)
-        products_vector(s, 0, 1, HG)
+        emit(s - 1, 1)
+        quant(s, GRP, 2 * GRP)
+        quant(s, 0, GRP)
+        emit(s - 1, 2)
+        emit(s - 1, 3)
+        up(s)
+        products_vector(s, 0, 0)
         half(s, 0, HG)
-        emit(s - 1, 0, on_scalar, 2)
-        emit(s - 1, 1, on_scalar, 2)
-        up_tokens(s)
-        quant(last, GRP, 2 * GRP)
-        products_gpsimd(s, 1, 0, last)
-        plain(s, 0)
-        rotated(s, 0)
+        products_vector(s, 0, 1)
+        half(s, 1, HG)
+        products_gpsimd(s, s)
+        up_tokens(s, 0)
+        up_tokens(s, 1)
         up(last)
+        plain(s, 0)
         plain(s, 1)
-        emit(s - 1, 2, on_scalar, 2)
-        emit(s - 1, 3, on_scalar, 2)
-        products_vector(last, 0, 0, HG)
-        products_vector(last, 0, 1, HG)
-        products_vector(last, 1, 0, HG)
-        products_vector(last, 1, 1, HG)
-        up_tokens(last)
-        rotated(last, 0)
-        rotated(s, 1)
+        store(s, slice(0, 2), 0, J)
+        rotated(s, 0, 2)
+        up_tokens(last, 0)
+        products_vector(last, 0, 0)
+        products_vector(last, 0, 1)
+        up_tokens(last, 1)
         plain(last, 0)
         plain(last, 1)
-        rotated(last, 1)
+        store(last, slice(0, 2), 0, J)
+        rotated(last, 0, 2)
+        rotated(s, 2, J)
+        for jj in range(2):
+            products_vector(last, 1, 0, jj * P, (jj + 1) * P)
+            products_vector(last, 1, 1, jj * P, (jj + 1) * P)
+            rotated(last, 2 + jj, 3 + jj)

@@ -11,7 +11,6 @@ FP8 = mybir.dt.float8_e4m3fn
 FP8X4 = mybir.dt.float8_e4m3fn_x4
 ADD = mybir.AluOpType.add
 MULT = mybir.AluOpType.mult
-COPY = mybir.ActivationFunctionType.Copy
 IDENT = mybir.ActivationFunctionType.Identity
 
 B, S, H, LAT, HALF = 4, 2048, 512, 512, 256
@@ -96,6 +95,8 @@ def tile_multiheadlatentattention_pa_t_kernel(
         make_identity(nc, idf[:])
         idb = keep.tile([P, P], BF16, name="idb")
         nc.vector.tensor_copy(out=idb[:], in_=idf[:])
+        idn = keep.tile([P, P], BF16, name="idn")
+        nc.vector.tensor_scalar(out=idn[:], in0=idf[:], scalar1=-1.0, scalar2=None, op0=MULT)
 
         wdc = keep.tile([P, LAT], U32, name="wdc", align_bytes=64)
         wds = keep.tile([P, LAT], U8, name="wds", align_bytes=64)
@@ -313,22 +314,20 @@ def tile_multiheadlatentattention_pa_t_kernel(
             nc.scalar.copy(out=result(n)[:, 2:4, lo:hi, :], in_=o[:])
             store(n, slice(2, 4), lo, hi)
 
-        def table(pg):
-            t = keep.tile([P, 2, 2, GRP], BF16, name="tab%d" % pg)
-            o = bank("o", [P, 2, GRP], BF16)
-            for i in range(2):
-                for j in range(J):
+        def table(pg, a):
+            if pg not in tab:
+                tab[pg] = keep.tile([P, 2, 2, GRP], BF16, name="tab%d" % pg)
+            o = bank("o", [P, 2, 2, HG], BF16)
+            for h, i, src, ident in ((0, 0, 0, idb), (1, 1, 0, idb), (0, 1, 1, idb), (1, 0, 1, idn)):
+                for jj in range(2):
                     nc.tensor.matmul(
-                        o[:, i, j * P : (j + 1) * P],
-                        lhsT=rope[i, pg // 2][:, pg % 2, j, :],
-                        rhs=idb[:],
+                        o[:, h, i, jj * P : (jj + 1) * P],
+                        lhsT=rope[src, pg // 2][:, pg % 2, 2 * a + jj, :],
+                        rhs=ident[:],
                         start=True,
                         stop=True,
                     )
-            nc.scalar.copy(out=t[:, 0, :, :], in_=o[:])
-            nc.scalar.activation(out=t[:, 1, 0, :], in_=o[:, 1, :], func=COPY, scale=-1.0)
-            nc.scalar.copy(out=t[:, 1, 1, :], in_=o[:, 0, :])
-            tab[pg] = t
+            nc.scalar.copy(out=tab[pg][:, :, :, a * HG : (a + 1) * HG], in_=o[:])
 
         def turn_weights(w, g, pairs):
             for h in range(pairs):
@@ -361,26 +360,25 @@ def tile_multiheadlatentattention_pa_t_kernel(
         quant(-2, HG, GRP)
         quant(-1, 0, GRP)
         widen(5, nc.scalar.copy)
-        table(0)
-        table(1)
-        scale(3)
-        down(0, 0)
-        down(0, 1)
-        widen(6, nc.scalar.copy)
-        turn_weights(wu, wug, 1)
-        lat(0, 0)
+        table(0, 0)
         turn(4)
-        lat(0, 1)
-        scale(4)
-        down(0, 2)
-        down(0, 3)
-        down_planes(1)
+        widen(6, nc.scalar.copy)
+        scale(3)
+        down_planes(0)
+        weave(0)
         widen(7, nc.scalar.copy)
+        down(0, 2)
+        scale(4)
+        down(0, 3)
+        turn_weights(wu, wug, 1)
+        table(0, 1)
+        down_planes(1)
         lat(0, 2)
         turn(5)
         lat(0, 3)
         turn(6)
-        table(2)
+        table(1, 0)
+        table(1, 1)
         quant_weights(wug, wuc, wus)
         quant(0, 0, 2 * GRP)
         weave(1)
@@ -397,15 +395,15 @@ def tile_multiheadlatentattention_pa_t_kernel(
                 widen(8, nc.scalar.copy)
             scale(2 * s + 3)
             down(s, 2)
+            down(s, 3)
             scale(2 * s + 4)
             lat(s, 2)
+            lat(s, 3)
             products_vector(s - 1, 0, 0)
             products_vector(s - 1, 0, 1)
             if s >= 2:
                 emit(s - 2, 0)
                 emit(s - 2, 1)
-            down(s, 3)
-            lat(s, 3)
             if s < last - 2:
                 widen(2 * s + 7, nc.scalar.copy)
             turn(2 * s + 5)
@@ -413,7 +411,11 @@ def tile_multiheadlatentattention_pa_t_kernel(
                 emit(s - 2, 2)
                 emit(s - 2, 3)
             if s == 1:
-                table(3)
+                table(2, 0)
+                table(2, 1)
+                table(3, 0)
+            if s == last - 3:
+                table(3, 1)
             if s < last - 3:
                 widen(2 * s + 8, nc.scalar.copy)
             if s < last - 2:

@@ -24,6 +24,12 @@ HG = GRP // 2
 PG = S // GRP
 NG = B * PG
 SLOTS = 4
+NV = 384
+KP = 192
+OUT_BUFS = 12
+PROD_BUFS = {"prod_g": 3, "prod_v": 6}
+KT = 64
+NT = 384
 
 
 def tile_multiheadlatentattention_pa_t_kernel(
@@ -37,7 +43,7 @@ def tile_multiheadlatentattention_pa_t_kernel(
         ctx.enter_context(tc.manual_schedule())
 
         used = {"v": 0, "o": 0}
-        depth = {"v": 3, "o": 5}
+        depth = {"v": 4, "o": 4}
 
         def bank(ring, shape, dtype):
             i = used[ring] % depth[ring]
@@ -166,8 +172,8 @@ def tile_multiheadlatentattention_pa_t_kernel(
                 stop=True,
             )
 
-        def down(n, j):
-            o = bank("v", [P, T4, P], F32)
+        def down(n, j, ring="v"):
+            o = bank(ring, [P, T4, P], F32)
             s, pos = x_place(2 * n + j // 2)
             lo = pos * HG + (j % 2) * P
             for t in range(T4):
@@ -204,130 +210,156 @@ def tile_multiheadlatentattention_pa_t_kernel(
                 op1=ADD,
             )
 
-        def up(n):
+        def up(n, h, ring):
             s, lo = q_place(n)
-            for h in range(2):
-                o = bank("o", [P, GRP], F32)
-                ws = slice(h * P, (h + 1) * P)
-                nc.tensor.matmul_mx(
-                    out=o[:],
-                    lhsT=wuc[:, ws].bitcast(FP8X4),
-                    lhsT_scale=wus[:, ws],
-                    rhs=codes[s][:, lo : lo + GRP].bitcast(FP8X4),
-                    rhs_scale=scales[s][:, lo : lo + GRP],
-                    start=True,
-                    stop=True,
-                )
-                m2[n, h] = o
+            o = bank(ring, [P, GRP], F32)
+            ws = slice(h * P, (h + 1) * P)
+            nc.tensor.matmul_mx(
+                out=o[:],
+                lhsT=wuc[:, ws].bitcast(FP8X4),
+                lhsT_scale=wus[:, ws],
+                rhs=codes[s][:, lo : lo + GRP].bitcast(FP8X4),
+                rhs_scale=scales[s][:, lo : lo + GRP],
+                start=True,
+                stop=True,
+            )
+            m2[n, h] = o
 
-        def half(n, h, lo=0):
+        def half(n, h, lo=0, hi=GRP):
             if n not in qt:
-                qt[n] = sb.tile([P, 2, GRP], F32, name="qt", bufs=4)
-            nc.scalar.activation(out=qt[n][:, h, lo:GRP], in_=m2[n, h][:, lo:GRP], func=IDENT, bias=bu[:, h, 0:1])
+                qt[n] = sb.tile([P, 2 * GRP], F32, name="qt", bufs=4, align_bytes=64)
+            nc.scalar.activation(
+                out=qt[n][:, h * GRP + lo : h * GRP + hi], in_=m2[n, h][:, lo:hi], func=IDENT, bias=bu[:, h, 0:1]
+            )
 
-        def products_gpsimd(n, behind):
-            t = sb.tile([P, 2, 2, HG], F32, name="slot%d" % (behind % SLOTS), bufs=1, align_bytes=64)
+        def piece(n, lo):
+            nc.vector.tensor_scalar(
+                out=qt[n][:, lo:GRP], in0=m2[n, 0][:, lo:GRP], scalar1=bu[:, 0, 0:1], scalar2=None, op0=ADD
+            )
+
+        def new_prod(n, lo, hi, name):
+            t = sb.tile([P, 2, hi - lo], F32, name=name, bufs=PROD_BUFS[name], align_bytes=64)
+            for c in range(lo // P, hi // P):
+                prod[n, c] = (t, c * P - lo)
+            return t
+
+        def products_gpsimd(n, lo, hi=2 * GRP):
+            t = new_prod(n, lo, hi, "prod_g")
             nc.gpsimd.tensor_tensor(
                 out=t[:],
-                in0=qt[n][:, :, HG:GRP].unsqueeze(2).to_broadcast([P, 2, 2, HG]),
-                in1=tab[n // B][:, :, :, HG:GRP],
+                in0=qt[n][:, lo:hi].unsqueeze(1).to_broadcast([P, 2, hi - lo]),
+                in1=tab[n // B][:, :, lo:hi],
                 op=MULT,
             )
-            prod[n, 1] = t
 
-        def products_vector(n, a, h, lo=0, hi=HG):
-            if (n, a) not in prod:
-                prod[n, a] = sb.tile([P, 2, 2, HG], F32, name="prod", bufs=4, align_bytes=64)
-            cols = slice(a * HG + lo, a * HG + hi)
+        def products_vector(n, lo, hi):
+            h = lo // GRP
+            t = new_prod(n, lo, hi, "prod_v")
             nc.vector.scalar_tensor_tensor(
-                out=prod[n, a][:, h, :, lo:hi],
-                in0=m2[n, h][:, cols].unsqueeze(1).to_broadcast([P, 2, hi - lo]),
+                out=t[:],
+                in0=m2[n, h][:, lo - h * GRP : hi - h * GRP].unsqueeze(1).to_broadcast([P, 2, hi - lo]),
                 scalar=bu[:, h, 0:1],
-                in1=tab[n // B][:, h, :, cols],
+                in1=tab[n // B][:, :, lo:hi],
                 op0=ADD,
                 op1=MULT,
             )
 
-        def result(n):
-            if n not in osb:
-                osb[n] = sb.tile([P, 4, J, P], F32, name="osb", bufs=4)
-            return osb[n]
+        def result(n, h):
+            if (n, h) not in osb:
+                osb[n, h] = sb.tile([P, J, P], F32, name="osb", bufs=OUT_BUFS)
+            return osb[n, h]
 
-        def store(n, heads, lo, hi):
+        def store(n, h, lo=0, hi=J):
             pg, b = divmod(n, B)
-            rows = out[b, heads, pg * GRP : (pg + 1) * GRP, :].rearrange("h (p j) d -> p h j d", j=J)
+            rows = out[b, h, pg * GRP : (pg + 1) * GRP, :].rearrange("(p j) d -> p j d", j=J)
+            nc.sync.dma_start(out=rows[:, lo:hi, :], in_=osb[n, h][:, lo:hi, :])
+
+        def head_plain(n, h):
+            o = bank("o", [P, J, P], F32)
+            for j in range(J):
+                nc.tensor.transpose(o[:, j, :], qt[n][:, h * GRP + j * P : h * GRP + (j + 1) * P], idf[:])
+            nc.scalar.copy(out=result(n, h)[:], in_=o[:])
+            store(n, h)
+
+        def head_rotated(n, i, lo=0, hi=J):
+            o = bank("o", [P, hi - lo, P], F32)
+            for j in range(lo, hi):
+                for h in range(2):
+                    t, at = prod[n, h * J + j]
+                    nc.tensor.matmul(
+                        o[:, j - lo, :],
+                        lhsT=t[:, i, at : at + P],
+                        rhs=idf[:],
+                        start=h == 0,
+                        stop=h == 1,
+                        is_transpose=True,
+                    )
+            nc.scalar.copy(out=result(n, 2 + i)[:, lo:hi, :], in_=o[:])
+            store(n, 2 + i, lo, hi)
+
+        def both_rotated(n, lo, hi):
+            o = bank("o", [P, 2, hi - lo, P], F32)
+            for i in range(2):
+                for j in range(lo, hi):
+                    for h in range(2):
+                        t, at = prod[n, h * J + j]
+                        nc.tensor.matmul(
+                            o[:, i, j - lo, :],
+                            lhsT=t[:, i, at : at + P],
+                            rhs=idf[:],
+                            start=h == 0,
+                            stop=h == 1,
+                            is_transpose=True,
+                        )
+            t = sb.tile([P, 2, hi - lo, P], F32, name="osb", bufs=OUT_BUFS)
+            nc.scalar.copy(out=t[:], in_=o[:])
+            pg, b = divmod(n, B)
+            rows = out[b, 2:4, pg * GRP : (pg + 1) * GRP, :].rearrange("h (p j) d -> p h j d", j=J)
             nc.sync.dma_start(
-                out=rows[:, :, lo:hi, :].rearrange("p h j d -> p h (j d)"),
-                in_=osb[n][:, heads, lo:hi, :].rearrange("p h j d -> p h (j d)"),
+                out=rows[:, :, lo:hi, :].rearrange("p h j d -> p h (j d)"), in_=t[:].rearrange("p h j d -> p h (j d)")
             )
 
-        def turn_rotated(dst, n, j, i):
-            for h in range(2):
-                nc.tensor.matmul(
-                    dst,
-                    lhsT=prod[n, j // 2][:, h, i, (j % 2) * P : (j % 2 + 1) * P],
-                    rhs=idf[:],
-                    start=h == 0,
-                    stop=h == 1,
-                    is_transpose=True,
-                )
-
-        def emit(n, j):
-            o = bank("o", [P, 4, P], F32)
-            for h in range(2):
-                nc.tensor.transpose(o[:, h, :], qt[n][:, h, j * P : (j + 1) * P], idf[:])
-            for i in range(2):
-                turn_rotated(o[:, 2 + i, :], n, j, i)
-            nc.scalar.copy(out=result(n)[:, :, j, :], in_=o[:])
-            if j % 2:
-                store(n, slice(0, 4), j - 1, j + 1)
-
-        def up_tokens(n, a):
+        def up_tokens(n, h, ring="v"):
             s, lo = q_place(n)
-            o = bank("v", [P, 2, HALF], F32)
-            for jj in range(2):
-                cols = slice(lo + (2 * a + jj) * P, lo + (2 * a + jj + 1) * P)
+            o = bank(ring, [P, J, P], F32)
+            ws = slice(h * P, (h + 1) * P)
+            for j in range(J):
+                cols = slice(lo + j * P, lo + (j + 1) * P)
                 nc.tensor.matmul_mx(
-                    out=o[:, jj, :],
+                    out=o[:, j, :],
                     lhsT=codes[s][:, cols].bitcast(FP8X4),
                     lhsT_scale=scales[s][:, cols],
-                    rhs=wuc[:].bitcast(FP8X4),
-                    rhs_scale=wus[:],
+                    rhs=wuc[:, ws].bitcast(FP8X4),
+                    rhs_scale=wus[:, ws],
                     start=True,
                     stop=True,
                 )
-            m3[n, a] = o
+            m3[n, h] = o
 
-        def plain(n, a):
+        def plain(n, h):
             nc.vector.tensor_tensor(
-                out=result(n)[:, 0:2, 2 * a : 2 * a + 2, :],
-                in0=m3[n, a][:].rearrange("p j (h d) -> p h j d", h=2),
-                in1=bias_row[:].rearrange("p (h d) -> p h d", h=2).unsqueeze(2).to_broadcast([P, 2, 2, P]),
+                out=result(n, h)[:],
+                in0=m3[n, h][:],
+                in1=bias_row[:, h * P : (h + 1) * P].unsqueeze(1).to_broadcast([P, J, P]),
                 op=ADD,
             )
+            store(n, h)
 
-        def rotated(n, lo, hi):
-            o = bank("o", [P, 2, hi - lo, P], F32)
-            for j in range(lo, hi):
-                for i in range(2):
-                    turn_rotated(o[:, i, j - lo, :], n, j, i)
-            nc.scalar.copy(out=result(n)[:, 2:4, lo:hi, :], in_=o[:])
-            store(n, slice(2, 4), lo, hi)
-
-        def table(pg, a):
+        def table(pg, h):
             if pg not in tab:
-                tab[pg] = keep.tile([P, 2, 2, GRP], BF16, name="tab%d" % pg)
-            o = bank("o", [P, 2, 2, HG], BF16)
-            for h, i, src, ident in ((0, 0, 0, idb), (1, 1, 0, idb), (0, 1, 1, idb), (1, 0, 1, idn)):
-                for jj in range(2):
+                tab[pg] = keep.tile([P, 2, 2 * GRP], BF16, name="tab%d" % pg, align_bytes=64)
+            o = bank("o", [P, 2, GRP], BF16)
+            for i in range(2):
+                ident = idn if (h, i) == (1, 0) else idb
+                for j in range(J):
                     nc.tensor.matmul(
-                        o[:, h, i, jj * P : (jj + 1) * P],
-                        lhsT=rope[src, pg // 2][:, pg % 2, 2 * a + jj, :],
+                        o[:, i, j * P : (j + 1) * P],
+                        lhsT=rope[(h + i) % 2, pg // 2][:, pg % 2, j, :],
                         rhs=ident[:],
                         start=True,
                         stop=True,
                     )
-            nc.scalar.copy(out=tab[pg][:, :, :, a * HG : (a + 1) * HG], in_=o[:])
+            nc.scalar.copy(out=tab[pg][:, :, h * GRP : (h + 1) * GRP], in_=o[:])
 
         def turn_weights(w, g, pairs):
             for h in range(pairs):
@@ -340,7 +372,6 @@ def tile_multiheadlatentattention_pa_t_kernel(
             nc.vector.quantize_mx(out=c[:].bitcast(FP8X4), scales=z[:], in_=g[:].rearrange("p r t -> p (r t)"))
 
         last = NG - 1
-
         widen(0, nc.scalar.copy, 0, 1)
         widen(0, nc.scalar.copy, 1, 2)
         widen(1, nc.scalar.copy)
@@ -366,17 +397,18 @@ def tile_multiheadlatentattention_pa_t_kernel(
         scale(3)
         down_planes(0)
         weave(0)
-        widen(7, nc.scalar.copy)
         down(0, 2)
         scale(4)
         down(0, 3)
         turn_weights(wu, wug, 1)
-        table(0, 1)
         down_planes(1)
+        table(0, 1)
         lat(0, 2)
         turn(5)
         lat(0, 3)
         turn(6)
+        widen(7, nc.scalar.copy)
+        widen(8, nc.scalar.copy)
         table(1, 0)
         table(1, 1)
         quant_weights(wug, wuc, wus)
@@ -385,99 +417,95 @@ def tile_multiheadlatentattention_pa_t_kernel(
 
         for s in range(1, last - 1):
             if s >= 2:
-                products_gpsimd(s - 2, s - 1)
+                products_gpsimd(s - 2, NV)
             down_planes(s + 1)
             weave(s + 1)
-            up(s - 1)
-            half(s - 1, 0)
+            up(s - 1, 1, "o")
             half(s - 1, 1)
-            if s == 1:
-                widen(8, nc.scalar.copy)
             scale(2 * s + 3)
+            scale(2 * s + 4)
             down(s, 2)
             down(s, 3)
-            scale(2 * s + 4)
+            up(s - 1, 0, "v")
+            kp = KP if s < last - 3 else KT
+            half(s - 1, 0, 0, GRP - kp)
             lat(s, 2)
             lat(s, 3)
-            products_vector(s - 1, 0, 0)
-            products_vector(s - 1, 0, 1)
-            if s >= 2:
-                emit(s - 2, 0)
-                emit(s - 2, 1)
+            products_vector(s - 1, 0, NV)
+            piece(s - 1, GRP - kp)
             if s < last - 2:
                 widen(2 * s + 7, nc.scalar.copy)
-            turn(2 * s + 5)
             if s >= 2:
-                emit(s - 2, 2)
-                emit(s - 2, 3)
-            if s == 1:
-                table(2, 0)
-                table(2, 1)
-                table(3, 0)
-            if s == last - 3:
-                table(3, 1)
+                head_plain(s - 2, 0)
+            turn(2 * s + 5)
             if s < last - 3:
                 widen(2 * s + 8, nc.scalar.copy)
             if s < last - 2:
                 turn(2 * s + 6)
-            quant(s, 0, GRP)
-            quant(s, GRP, 2 * GRP)
+            head_plain(s - 1, 1)
+            if s == 1:
+                table(2, 0)
+                table(2, 1)
+                table(3, 0)
+            if s == last - 2:
+                table(3, 1)
+            if s >= 2:
+                head_rotated(s - 2, 0)
+                head_rotated(s - 2, 1)
+            quant(s, 0, 2 * GRP)
 
         s = last - 1
-        products_gpsimd(s - 2, s - 1)
-        emit(s - 2, 0)
-        emit(s - 2, 1)
-        scale(2 * NG - 1)
+        products_gpsimd(s - 2, NV)
         down(s, 2)
-        up(s - 1)
         down(s, 3)
-        half(s - 1, 0)
+        up(s - 1, 0, "v")
+        up(s - 1, 1, "o")
+        half(s - 1, 0, 0, GRP - KT)
         half(s - 1, 1)
-        lat(s, 2)
-        lat(s, 3)
+        scale(2 * NG - 1)
         down(last, 0)
+        lat(s, 2)
         down(last, 1)
-        products_vector(s - 1, 0, 0)
+        lat(s, 3)
+        head_plain(s - 2, 0)
+        head_plain(s - 1, 1)
+        products_vector(s - 1, 0, NT)
         quant(last, 0, HG)
-        products_gpsimd(s - 1, last)
-        products_vector(s - 1, 0, 1)
-        emit(s - 2, 2)
-        emit(s - 2, 3)
-        emit(s - 1, 0)
+        piece(s - 1, GRP - KT)
+        quant(s, GRP, 2 * GRP)
+        products_gpsimd(s - 1, NT)
+        head_rotated(s - 2, 0)
         lat(last, 0)
         down(last, 2)
         lat(last, 1)
         down(last, 3)
+        up(s, 1, "o")
+        up(s, 0, "v")
+        half(s, 1)
+        half(s, 0, 0, GRP - KT)
+        head_rotated(s - 2, 1)
+        head_plain(s - 1, 0)
+        head_plain(s, 1)
         lat(last, 2)
         lat(last, 3)
-        emit(s - 1, 1)
-        quant(s, GRP, 2 * GRP)
+        piece(s, GRP - KT)
         quant(s, 0, GRP)
-        emit(s - 1, 2)
-        emit(s - 1, 3)
-        up(s)
-        products_vector(s, 0, 0)
-        half(s, 0, HG)
-        products_vector(s, 0, 1)
-        half(s, 1, HG)
-        products_gpsimd(s, s)
-        up_tokens(s, 0)
-        up_tokens(s, 1)
-        up(last)
-        plain(s, 0)
-        plain(s, 1)
-        store(s, slice(0, 2), 0, J)
-        rotated(s, 0, 2)
+        products_gpsimd(s, NT)
+        products_vector(s, 0, NT)
+        head_rotated(s - 1, 0)
+        up(last, 1, "v")
+        up(last, 0, "v")
         up_tokens(last, 0)
-        products_vector(last, 0, 0)
-        products_vector(last, 0, 1)
-        up_tokens(last, 1)
+        head_rotated(s - 1, 1)
+        head_plain(s, 0)
+        products_vector(last, GRP, GRP + HG)
+        products_vector(last, 0, HG)
         plain(last, 0)
+        up_tokens(last, 1)
+        both_rotated(last, 0, 2)
+        products_vector(last, GRP + HG, 2 * GRP)
+        products_vector(last, HG, GRP)
+        head_rotated(s, 0)
         plain(last, 1)
-        store(last, slice(0, 2), 0, J)
-        rotated(last, 0, 2)
-        rotated(s, 2, J)
-        for jj in range(2):
-            products_vector(last, 1, 0, jj * P, (jj + 1) * P)
-            products_vector(last, 1, 1, jj * P, (jj + 1) * P)
-            rotated(last, 2 + jj, 3 + jj)
+        head_rotated(s, 1)
+        both_rotated(last, 2, 4)

@@ -24,12 +24,12 @@ HG = GRP // 2
 PG = S // GRP
 NG = B * PG
 SLOTS = 4
-NV = 384
-KP = 192
+NV = 480
+KP = 32
 OUT_BUFS = 12
-PROD_BUFS = {"prod_g": 3, "prod_v": 6}
-KT = 64
-NT = 384
+PROD_BUFS = 4
+KT = 32
+NT = 480
 
 
 def tile_multiheadlatentattention_pa_t_kernel(
@@ -237,26 +237,23 @@ def tile_multiheadlatentattention_pa_t_kernel(
                 out=qt[n][:, lo:GRP], in0=m2[n, 0][:, lo:GRP], scalar1=bu[:, 0, 0:1], scalar2=None, op0=ADD
             )
 
-        def new_prod(n, lo, hi, name):
-            t = sb.tile([P, 2, hi - lo], F32, name=name, bufs=PROD_BUFS[name], align_bytes=64)
-            for c in range(lo // P, hi // P):
-                prod[n, c] = (t, c * P - lo)
-            return t
+        def products(n):
+            if n not in prod:
+                prod[n] = sb.tile([P, 2, 2 * GRP], F32, name="prod", bufs=PROD_BUFS, align_bytes=64)
+            return prod[n]
 
-        def products_gpsimd(n, lo, hi=2 * GRP):
-            t = new_prod(n, lo, hi, "prod_g")
+        def products_gpsimd(n, lo):
             nc.gpsimd.tensor_tensor(
-                out=t[:],
-                in0=qt[n][:, lo:hi].unsqueeze(1).to_broadcast([P, 2, hi - lo]),
-                in1=tab[n // B][:, :, lo:hi],
+                out=products(n)[:, :, lo:],
+                in0=qt[n][:, lo:].unsqueeze(1).to_broadcast([P, 2, 2 * GRP - lo]),
+                in1=tab[n // B][:, :, lo:],
                 op=MULT,
             )
 
         def products_vector(n, lo, hi):
             h = lo // GRP
-            t = new_prod(n, lo, hi, "prod_v")
             nc.vector.scalar_tensor_tensor(
-                out=t[:],
+                out=products(n)[:, :, lo:hi],
                 in0=m2[n, h][:, lo - h * GRP : hi - h * GRP].unsqueeze(1).to_broadcast([P, 2, hi - lo]),
                 scalar=bu[:, h, 0:1],
                 in1=tab[n // B][:, :, lo:hi],
@@ -285,10 +282,9 @@ def tile_multiheadlatentattention_pa_t_kernel(
             o = bank("o", [P, hi - lo, P], F32)
             for j in range(lo, hi):
                 for h in range(2):
-                    t, at = prod[n, h * J + j]
                     nc.tensor.matmul(
                         o[:, j - lo, :],
-                        lhsT=t[:, i, at : at + P],
+                        lhsT=prod[n][:, i, h * GRP + j * P : h * GRP + (j + 1) * P],
                         rhs=idf[:],
                         start=h == 0,
                         stop=h == 1,
@@ -302,10 +298,9 @@ def tile_multiheadlatentattention_pa_t_kernel(
             for i in range(2):
                 for j in range(lo, hi):
                     for h in range(2):
-                        t, at = prod[n, h * J + j]
                         nc.tensor.matmul(
                             o[:, i, j - lo, :],
-                            lhsT=t[:, i, at : at + P],
+                            lhsT=prod[n][:, i, h * GRP + j * P : h * GRP + (j + 1) * P],
                             rhs=idf[:],
                             start=h == 0,
                             stop=h == 1,

@@ -25,11 +25,11 @@ PG = S // GRP
 NG = B * PG
 SLOTS = 4
 NV = 480
-KP = 32
+KP = 64
 OUT_BUFS = 12
 PROD_BUFS = 4
-KT = 32
-NT = 480
+KT = 64
+NT = 256
 
 
 def tile_multiheadlatentattention_pa_t_kernel(
@@ -191,14 +191,17 @@ def tile_multiheadlatentattention_pa_t_kernel(
 
         def down_planes(n):
             s, pos = x_place(2 * n)
-            planes[n] = sb.tile([P, T4, HG], BF16, name="planes", bufs=2)
             for pair in range(2):
-                o = bank("o", [P, 2, HG], F32)
+                m1[n, "planes", pair] = bank("o", [P, 2, HG], F32)
                 for e in range(2):
-                    down_pass(o[:, e, :], 2 * pair + e, s, slice(pos * HG, (pos + 1) * HG))
-                for e in range(2):
-                    t = 2 * pair + e
-                    nc.scalar.activation(out=planes[n][:, t, :], in_=o[:, e, :], func=IDENT, bias=bd[:, t : t + 1])
+                    down_pass(m1[n, "planes", pair][:, e, :], 2 * pair + e, s, slice(pos * HG, (pos + 1) * HG))
+
+        def lat_planes(n):
+            planes[n] = sb.tile([P, T4, HG], BF16, name="planes", bufs=2)
+            for t in range(T4):
+                nc.scalar.activation(
+                    out=planes[n][:, t, :], in_=m1[n, "planes", t // 2][:, t % 2, :], func=IDENT, bias=bd[:, t : t + 1]
+                )
 
         def weave(n):
             nc.gpsimd.tensor_scalar(
@@ -232,9 +235,16 @@ def tile_multiheadlatentattention_pa_t_kernel(
                 out=qt[n][:, h * GRP + lo : h * GRP + hi], in_=m2[n, h][:, lo:hi], func=IDENT, bias=bu[:, h, 0:1]
             )
 
-        def piece(n, lo):
+        def piece(n, lo, hi):
+            if n not in qt:
+                qt[n] = sb.tile([P, 2 * GRP], F32, name="qt", bufs=4, align_bytes=64)
+            h = lo // GRP
             nc.vector.tensor_scalar(
-                out=qt[n][:, lo:GRP], in0=m2[n, 0][:, lo:GRP], scalar1=bu[:, 0, 0:1], scalar2=None, op0=ADD
+                out=qt[n][:, lo:hi],
+                in0=m2[n, h][:, lo - h * GRP : hi - h * GRP],
+                scalar1=bu[:, h, 0:1],
+                scalar2=None,
+                op0=ADD,
             )
 
         def products(n):
@@ -278,20 +288,27 @@ def tile_multiheadlatentattention_pa_t_kernel(
             nc.scalar.copy(out=result(n, h)[:], in_=o[:])
             store(n, h)
 
-        def head_rotated(n, i, lo=0, hi=J):
-            o = bank("o", [P, hi - lo, P], F32)
-            for j in range(lo, hi):
+        def turn_rotated(n, i):
+            o = bank("o", [P, J, P], F32)
+            for j in range(J):
                 for h in range(2):
                     nc.tensor.matmul(
-                        o[:, j - lo, :],
+                        o[:, j, :],
                         lhsT=prod[n][:, i, h * GRP + j * P : h * GRP + (j + 1) * P],
                         rhs=idf[:],
                         start=h == 0,
                         stop=h == 1,
                         is_transpose=True,
                     )
-            nc.scalar.copy(out=result(n, 2 + i)[:, lo:hi, :], in_=o[:])
-            store(n, 2 + i, lo, hi)
+            m3[n, 2 + i] = o
+
+        def copy_out(n, h):
+            nc.scalar.copy(out=result(n, h)[:], in_=m3[n, h][:])
+            store(n, h)
+
+        def head_rotated(n, i):
+            turn_rotated(n, i)
+            copy_out(n, 2 + i)
 
         def both_rotated(n, lo, hi):
             o = bank("o", [P, 2, hi - lo, P], F32)
@@ -391,12 +408,14 @@ def tile_multiheadlatentattention_pa_t_kernel(
         widen(6, nc.scalar.copy)
         scale(3)
         down_planes(0)
+        lat_planes(0)
         weave(0)
         down(0, 2)
         scale(4)
         down(0, 3)
         turn_weights(wu, wug, 1)
         down_planes(1)
+        lat_planes(1)
         table(0, 1)
         lat(0, 2)
         turn(5)
@@ -407,96 +426,105 @@ def tile_multiheadlatentattention_pa_t_kernel(
         table(1, 0)
         table(1, 1)
         quant_weights(wug, wuc, wus)
-        quant(0, 0, 2 * GRP)
+        quant(0, 0, GRP)
+        quant(0, GRP, 2 * GRP)
         weave(1)
 
         for s in range(1, last - 1):
             if s >= 2:
                 products_gpsimd(s - 2, NV)
             down_planes(s + 1)
+            if s >= 2:
+                half(s - 2, 0, 0, GRP - KP)
+            if s >= 3:
+                copy_out(s - 3, 3)
+            lat_planes(s + 1)
             weave(s + 1)
-            up(s - 1, 1, "o")
-            half(s - 1, 1)
+            if s < last - 2:
+                widen(2 * s + 7, nc.scalar.copy)
             scale(2 * s + 3)
             scale(2 * s + 4)
             down(s, 2)
             down(s, 3)
+            up(s - 1, 1, "o")
             up(s - 1, 0, "v")
-            kp = KP if s < last - 3 else KT
-            half(s - 1, 0, 0, GRP - kp)
+            half(s - 1, 1)
             lat(s, 2)
             lat(s, 3)
             products_vector(s - 1, 0, NV)
-            piece(s - 1, GRP - kp)
-            if s < last - 2:
-                widen(2 * s + 7, nc.scalar.copy)
             if s >= 2:
                 head_plain(s - 2, 0)
+            if s == last - 2:
+                table(3, 1)
             turn(2 * s + 5)
             if s < last - 3:
                 widen(2 * s + 8, nc.scalar.copy)
-            if s < last - 2:
-                turn(2 * s + 6)
-            head_plain(s - 1, 1)
             if s == 1:
                 table(2, 0)
                 table(2, 1)
                 table(3, 0)
-            if s == last - 2:
-                table(3, 1)
             if s >= 2:
                 head_rotated(s - 2, 0)
-                head_rotated(s - 2, 1)
-            quant(s, 0, 2 * GRP)
+            head_plain(s - 1, 1)
+            if s < last - 2:
+                turn(2 * s + 6)
+            if s >= 2:
+                turn_rotated(s - 2, 1)
+            quant(s, 0, GRP)
+            piece(s - 1, GRP - KP, GRP)
+            quant(s, GRP, 2 * GRP)
 
         s = last - 1
         products_gpsimd(s - 2, NV)
+        half(s - 2, 0, 0, GRP - KP)
+        copy_out(s - 3, 3)
+        scale(2 * NG - 1)
         down(s, 2)
         down(s, 3)
-        up(s - 1, 0, "v")
         up(s - 1, 1, "o")
-        half(s - 1, 0, 0, GRP - KT)
+        up(s - 1, 0, "v")
         half(s - 1, 1)
-        scale(2 * NG - 1)
-        down(last, 0)
         lat(s, 2)
-        down(last, 1)
+        down(last, 0)
         lat(s, 3)
+        down(last, 1)
         head_plain(s - 2, 0)
         head_plain(s - 1, 1)
-        products_vector(s - 1, 0, NT)
+        products_vector(s - 1, 0, NV)
         quant(last, 0, HG)
-        piece(s - 1, GRP - KT)
+        piece(s - 1, GRP - KP, GRP)
         quant(s, GRP, 2 * GRP)
-        products_gpsimd(s - 1, NT)
+        half(s - 1, 0, 0, GRP - KP)
+        products_gpsimd(s - 1, NV)
         head_rotated(s - 2, 0)
         lat(last, 0)
-        down(last, 2)
+        down(last, 2, "o")
         lat(last, 1)
         down(last, 3)
         up(s, 1, "o")
         up(s, 0, "v")
         half(s, 1)
-        half(s, 0, 0, GRP - KT)
+        half(s, 0, 0, GRP - KP)
         head_rotated(s - 2, 1)
         head_plain(s - 1, 0)
         head_plain(s, 1)
         lat(last, 2)
         lat(last, 3)
-        piece(s, GRP - KT)
-        quant(s, 0, GRP)
-        products_gpsimd(s, NT)
-        products_vector(s, 0, NT)
+        quant(s, 0, HG)
+        piece(s, GRP - KP, GRP)
+        quant(s, HG, GRP)
+        products_gpsimd(s, NV)
+        products_vector(s, 0, NV)
         head_rotated(s - 1, 0)
+        head_plain(s, 0)
         up(last, 1, "v")
         up(last, 0, "v")
         up_tokens(last, 0)
         head_rotated(s - 1, 1)
-        head_plain(s, 0)
         products_vector(last, GRP, GRP + HG)
         products_vector(last, 0, HG)
-        plain(last, 0)
         up_tokens(last, 1)
+        plain(last, 0)
         both_rotated(last, 0, 2)
         products_vector(last, GRP + HG, 2 * GRP)
         products_vector(last, HG, GRP)

@@ -26,7 +26,7 @@ NG = B * PG
 SLOTS = 4
 NV = 480
 KP = 64
-OUT_BUFS = 12
+OUT_BUFS = 5
 PROD_BUFS = 4
 KT = 64
 NT = 256
@@ -111,7 +111,7 @@ def tile_multiheadlatentattention_pa_t_kernel(
         wdg = sb.tile([P, LAT, T4], BF16, name="slot0", bufs=1, align_bytes=64)
         wug = sb.tile([P, HALF, T4], BF16, name="slot1", bufs=1, align_bytes=64)
 
-        xbf, xt, staged, codes, scales, m1, m2, m3, planes, qt, prod, tab, osb = ({} for i in range(13))
+        xbf, xt, staged, codes, scales, m1, m2, m3, planes, qt, prod, tab, osb, written = ({} for i in range(14))
 
         def widen(m, copy, lo=0, hi=2):
             if lo == 0:
@@ -272,20 +272,26 @@ def tile_multiheadlatentattention_pa_t_kernel(
             )
 
         def result(n, h):
-            if (n, h) not in osb:
-                osb[n, h] = sb.tile([P, J, P], F32, name="osb", bufs=OUT_BUFS)
-            return osb[n, h]
+            if n not in osb:
+                osb[n] = sb.tile([P, 4, J, P], F32, name="osb", bufs=OUT_BUFS)
+            return osb[n][:, h, :, :]
 
-        def store(n, h, lo=0, hi=J):
+        def store(n, h):
+            written.setdefault(n, []).append(h)
+            heads = slice(h, h + 1)
+            if n < NG - OUT_BUFS:
+                if len(written[n]) < 4:
+                    return
+                heads = slice(0, 4)
             pg, b = divmod(n, B)
-            rows = out[b, h, pg * GRP : (pg + 1) * GRP, :].rearrange("(p j) d -> p j d", j=J)
-            nc.sync.dma_start(out=rows[:, lo:hi, :], in_=osb[n, h][:, lo:hi, :])
+            rows = out[b, heads, pg * GRP : (pg + 1) * GRP, :].rearrange("h (p j) d -> p h (j d)", j=J)
+            nc.sync.dma_start(out=rows, in_=osb[n][:, heads, :, :].rearrange("p h j d -> p h (j d)"))
 
         def head_plain(n, h):
             o = bank("o", [P, J, P], F32)
             for j in range(J):
                 nc.tensor.transpose(o[:, j, :], qt[n][:, h * GRP + j * P : h * GRP + (j + 1) * P], idf[:])
-            nc.scalar.copy(out=result(n, h)[:], in_=o[:])
+            nc.scalar.copy(out=result(n, h), in_=o[:])
             store(n, h)
 
         def turn_rotated(n, i):
@@ -303,7 +309,7 @@ def tile_multiheadlatentattention_pa_t_kernel(
             m3[n, 2 + i] = o
 
         def copy_out(n, h):
-            nc.scalar.copy(out=result(n, h)[:], in_=m3[n, h][:])
+            nc.scalar.copy(out=result(n, h), in_=m3[n, h][:])
             store(n, h)
 
         def head_rotated(n, i):
@@ -323,12 +329,13 @@ def tile_multiheadlatentattention_pa_t_kernel(
                             stop=h == 1,
                             is_transpose=True,
                         )
-            t = sb.tile([P, 2, hi - lo, P], F32, name="osb", bufs=OUT_BUFS)
-            nc.scalar.copy(out=t[:], in_=o[:])
+            result(n, 2)
+            t = osb[n][:, 2:4, lo:hi, :]
+            nc.scalar.copy(out=t, in_=o[:])
             pg, b = divmod(n, B)
             rows = out[b, 2:4, pg * GRP : (pg + 1) * GRP, :].rearrange("h (p j) d -> p h j d", j=J)
             nc.sync.dma_start(
-                out=rows[:, :, lo:hi, :].rearrange("p h j d -> p h (j d)"), in_=t[:].rearrange("p h j d -> p h (j d)")
+                out=rows[:, :, lo:hi, :].rearrange("p h j d -> p h (j d)"), in_=t.rearrange("p h j d -> p h (j d)")
             )
 
         def up_tokens(n, h, ring="v"):
@@ -350,7 +357,7 @@ def tile_multiheadlatentattention_pa_t_kernel(
 
         def plain(n, h):
             nc.vector.tensor_tensor(
-                out=result(n, h)[:],
+                out=result(n, h),
                 in0=m3[n, h][:],
                 in1=bias_row[:, h * P : (h + 1) * P].unsqueeze(1).to_broadcast([P, J, P]),
                 op=ADD,

@@ -196,8 +196,13 @@ def tile_multiheadlatentattention_pa_t_kernel(
                 for e in range(2):
                     down_pass(m1[n, "planes", pair][:, e, :], 2 * pair + e, s, slice(pos * HG, (pos + 1) * HG))
 
+        def biased(n):
+            if n not in qt:
+                qt[n] = sb.tile([P, 2 * GRP], F32, name="qt", bufs=5, align_bytes=64)
+            return qt[n]
+
         def lat_planes(n):
-            planes[n] = sb.tile([P, T4, HG], BF16, name="planes", bufs=2)
+            planes[n] = biased(n - 1)[:, 0:GRP].bitcast(BF16).rearrange("p (t r) -> p t r", t=T4)
             for t in range(T4):
                 nc.scalar.activation(
                     out=planes[n][:, t, :], in_=m1[n, "planes", t // 2][:, t % 2, :], func=IDENT, bias=bd[:, t : t + 1]
@@ -206,7 +211,7 @@ def tile_multiheadlatentattention_pa_t_kernel(
         def weave(n):
             nc.gpsimd.tensor_scalar(
                 out=staging(n)[:, GRP : GRP + HG, :],
-                in0=planes[n][:].rearrange("p t r -> p r t"),
+                in0=planes[n].rearrange("p t r -> p r t"),
                 scalar1=1.0,
                 scalar2=0.0,
                 op0=MULT,
@@ -229,15 +234,13 @@ def tile_multiheadlatentattention_pa_t_kernel(
             m2[n, h] = o
 
         def half(n, h, lo=0, hi=GRP):
-            if n not in qt:
-                qt[n] = sb.tile([P, 2 * GRP], F32, name="qt", bufs=4, align_bytes=64)
+            biased(n)
             nc.scalar.activation(
                 out=qt[n][:, h * GRP + lo : h * GRP + hi], in_=m2[n, h][:, lo:hi], func=IDENT, bias=bu[:, h, 0:1]
             )
 
         def piece(n, lo, hi):
-            if n not in qt:
-                qt[n] = sb.tile([P, 2 * GRP], F32, name="qt", bufs=4, align_bytes=64)
+            biased(n)
             h = lo // GRP
             nc.vector.tensor_scalar(
                 out=qt[n][:, lo:hi],
@@ -433,8 +436,7 @@ def tile_multiheadlatentattention_pa_t_kernel(
         table(1, 0)
         table(1, 1)
         quant_weights(wug, wuc, wus)
-        quant(0, 0, GRP)
-        quant(0, GRP, 2 * GRP)
+        quant(0, 0, 2 * GRP)
         weave(1)
 
         for s in range(1, last - 1):

@@ -11,6 +11,7 @@ FP8 = mybir.dt.float8_e4m3fn
 FP8X4 = mybir.dt.float8_e4m3fn_x4
 ADD = mybir.AluOpType.add
 MULT = mybir.AluOpType.mult
+SUB = mybir.AluOpType.subtract
 IDENT = mybir.ActivationFunctionType.Identity
 
 B, S, H, LAT, HALF = 4, 2048, 512, 512, 256
@@ -25,11 +26,11 @@ PG = S // GRP
 NG = B * PG
 SLOTS = 4
 NV = 480
-KP = 64
+KP = 32
 OUT_BUFS = 5
 PROD_BUFS = 4
 KT = 64
-NT = 256
+NT = 192
 
 
 def tile_multiheadlatentattention_pa_t_kernel(
@@ -42,13 +43,24 @@ def tile_multiheadlatentattention_pa_t_kernel(
         ps = ctx.enter_context(tc.psum_pool(name="ps", bufs=1))
         ctx.enter_context(tc.manual_schedule())
 
-        used = {"v": 0, "o": 0}
-        depth = {"v": 4, "o": 4}
+        free = {"v": list(range(0, 4)), "o": list(range(4, 8))}
+        held = {}
+        merged = []
 
-        def bank(ring, shape, dtype):
-            i = used[ring] % depth[ring]
-            used[ring] = used[ring] + 1
-            return ps.tile(shape, dtype, name="bank_%s%d" % (ring, i))
+        def bank(key, ring, shape, dtype):
+            if merged:
+                ring = "v"
+            i = free[ring].pop(0)
+            held[key] = (ps.tile(shape, dtype, name="bank%d" % i), ring, i)
+            return held[key][0]
+
+        def give_back(key):
+            t, ring, i = held.pop(key)
+            free["v" if merged else ring].append(i)
+
+        def merge_rings():
+            merged.append(1)
+            free["v"].extend(free["o"])
 
         xb = {}
 
@@ -71,20 +83,20 @@ def tile_multiheadlatentattention_pa_t_kernel(
                 )
                 rope[i, pair] = t
 
-        load_x(0, (0, 1, 2, J))
         sc = keep.tile([P, T4], F32, name="sc")
-        nc.sync.dma_start(out=sc[:], in_=x_scale.rearrange("a b (p t) -> p (a b t)", t=T4))
         wd = keep.tile([P, T4, H], BF16, name="wd", align_bytes=64)
         wd_rows = wq_down.rearrange("(m t) k -> m t k", t=T4)
+        bd = keep.tile([P, T4], BF16, name="bd")
+        wu = keep.tile([P, 2, LAT], BF16, name="wu", align_bytes=64)
+        load_x(0, (0, 1, 2, J))
+        nc.sync.dma_start(out=sc[:], in_=x_scale.rearrange("a b (p t) -> p (a b t)", t=T4))
         load_x(1, (0, 2))
         nc.sync.dma_start(out=wd[:, 0:2, :], in_=wd_rows[:, 0:2, :])
         nc.sync.dma_start(out=wd[:, 2:4, :], in_=wd_rows[:, 2:4, :])
         load_x(1, (2, J))
-        bd = keep.tile([P, T4], BF16, name="bd")
         nc.sync.dma_start(out=bd[:], in_=bq_down.rearrange("(p t) -> p t", t=T4))
         load_x(2, (0, J))
         load_rope(0)
-        wu = keep.tile([P, 2, LAT], BF16, name="wu", align_bytes=64)
         nc.sync.dma_start(out=wu[:], in_=wq_up.rearrange("(h m) k -> m h k", h=2))
         load_x(3, (0, J))
         load_rope(1)
@@ -119,16 +131,16 @@ def tile_multiheadlatentattention_pa_t_kernel(
             j = 2 * (m % 2)
             copy(out=xbf[m][:, lo:hi, :], in_=xb[m // 2][:, j + lo : j + hi, :].bitcast(FP8))
 
-        def turn_words(ring, words):
+        def turn_words(key, ring, words):
             tiles = words.shape[1]
-            t = bank(ring, [P, 2, tiles * P], F32)
+            t = bank(key, ring, [P, 2, tiles * P], F32)
             for jj in range(tiles):
                 for u in range(2):
                     nc.tensor.transpose(t[:, u, jj * P : (jj + 1) * P], words[:, jj, u : H // 2 : 2], idf[:])
             return t
 
         def turn(m, lo=0, hi=2):
-            xt[m, lo] = turn_words("v", xbf[m][:, lo:hi, :].bitcast(F32))
+            xt[m, lo] = turn_words(("x", m, lo), "v", xbf[m][:, lo:hi, :].bitcast(F32))
 
         def staging(s):
             if s not in staged:
@@ -149,6 +161,7 @@ def tile_multiheadlatentattention_pa_t_kernel(
                 in1=sc[:].rearrange("p (u e) -> p u e", e=2).unsqueeze(1).to_broadcast([P, (hi - lo) * P, 2, 2]),
                 op=MULT,
             )
+            give_back(("x", m, lo))
 
         def quant(s, lo, hi):
             if s not in codes:
@@ -173,7 +186,7 @@ def tile_multiheadlatentattention_pa_t_kernel(
             )
 
         def down(n, j, ring="v"):
-            o = bank(ring, [P, T4, P], F32)
+            o = bank(("lat", n, j), ring, [P, T4, P], F32)
             s, pos = x_place(2 * n + j // 2)
             lo = pos * HG + (j % 2) * P
             for t in range(T4):
@@ -188,11 +201,12 @@ def tile_multiheadlatentattention_pa_t_kernel(
                 in1=bd[:].unsqueeze(1).to_broadcast([P, P, T4]),
                 op=ADD,
             )
+            give_back(("lat", n, j))
 
         def down_planes(n):
             s, pos = x_place(2 * n)
             for pair in range(2):
-                m1[n, "planes", pair] = bank("o", [P, 2, HG], F32)
+                m1[n, "planes", pair] = bank(("planes", n, pair), "o", [P, 2, HG], F32)
                 for e in range(2):
                     down_pass(m1[n, "planes", pair][:, e, :], 2 * pair + e, s, slice(pos * HG, (pos + 1) * HG))
 
@@ -207,6 +221,8 @@ def tile_multiheadlatentattention_pa_t_kernel(
                 nc.scalar.activation(
                     out=planes[n][:, t, :], in_=m1[n, "planes", t // 2][:, t % 2, :], func=IDENT, bias=bd[:, t : t + 1]
                 )
+                if t % 2:
+                    give_back(("planes", n, t // 2))
 
         def weave(n):
             nc.gpsimd.tensor_scalar(
@@ -220,7 +236,7 @@ def tile_multiheadlatentattention_pa_t_kernel(
 
         def up(n, h, ring):
             s, lo = q_place(n)
-            o = bank(ring, [P, GRP], F32)
+            o = bank(("up", n, h), ring, [P, GRP], F32)
             ws = slice(h * P, (h + 1) * P)
             nc.tensor.matmul_mx(
                 out=o[:],
@@ -232,6 +248,36 @@ def tile_multiheadlatentattention_pa_t_kernel(
                 stop=True,
             )
             m2[n, h] = o
+
+        def up_both(n, a):
+            s, lo = q_place(n)
+            o = bank(("both", n, a), "v", [P, 2, HG], F32)
+            cols = slice(lo + a * HG, lo + (a + 1) * HG)
+            for h in range(2):
+                ws = slice(h * P, (h + 1) * P)
+                nc.tensor.matmul_mx(
+                    out=o[:, h, :],
+                    lhsT=wuc[:, ws].bitcast(FP8X4),
+                    lhsT_scale=wus[:, ws],
+                    rhs=codes[s][:, cols].bitcast(FP8X4),
+                    rhs_scale=scales[s][:, cols],
+                    start=True,
+                    stop=True,
+                )
+            m2[n, "both", a] = o
+
+        def products_last(n, a):
+            for h in range(2):
+                cols = slice(h * GRP + a * HG, h * GRP + (a + 1) * HG)
+                nc.vector.scalar_tensor_tensor(
+                    out=products(n)[:, :, cols],
+                    in0=m2[n, "both", a][:, h, :].unsqueeze(1).to_broadcast([P, 2, HG]),
+                    scalar=bu[:, h, 0:1],
+                    in1=tab[n // B][:, :, cols],
+                    op0=ADD,
+                    op1=MULT,
+                )
+            give_back(("both", n, a))
 
         def half(n, h, lo=0, hi=GRP):
             biased(n)
@@ -290,15 +336,18 @@ def tile_multiheadlatentattention_pa_t_kernel(
             rows = out[b, heads, pg * GRP : (pg + 1) * GRP, :].rearrange("h (p j) d -> p h (j d)", j=J)
             nc.sync.dma_start(out=rows, in_=osb[n][:, heads, :, :].rearrange("p h j d -> p h (j d)"))
 
-        def head_plain(n, h):
-            o = bank("o", [P, J, P], F32)
+        def turn_plain(n, h):
+            o = bank(("out", n, h), "o", [P, J, P], F32)
             for j in range(J):
                 nc.tensor.transpose(o[:, j, :], qt[n][:, h * GRP + j * P : h * GRP + (j + 1) * P], idf[:])
-            nc.scalar.copy(out=result(n, h), in_=o[:])
-            store(n, h)
+            m3[n, h] = o
+
+        def head_plain(n, h):
+            turn_plain(n, h)
+            copy_out(n, h)
 
         def turn_rotated(n, i):
-            o = bank("o", [P, J, P], F32)
+            o = bank(("out", n, 2 + i), "o", [P, J, P], F32)
             for j in range(J):
                 for h in range(2):
                     nc.tensor.matmul(
@@ -313,6 +362,7 @@ def tile_multiheadlatentattention_pa_t_kernel(
 
         def copy_out(n, h):
             nc.scalar.copy(out=result(n, h), in_=m3[n, h][:])
+            give_back(("out", n, h))
             store(n, h)
 
         def head_rotated(n, i):
@@ -320,7 +370,7 @@ def tile_multiheadlatentattention_pa_t_kernel(
             copy_out(n, 2 + i)
 
         def both_rotated(n, lo, hi):
-            o = bank("o", [P, 2, hi - lo, P], F32)
+            o = bank(("pair", n, lo), "o", [P, 2, hi - lo, P], F32)
             for i in range(2):
                 for j in range(lo, hi):
                     for h in range(2):
@@ -335,6 +385,7 @@ def tile_multiheadlatentattention_pa_t_kernel(
             result(n, 2)
             t = osb[n][:, 2:4, lo:hi, :]
             nc.scalar.copy(out=t, in_=o[:])
+            give_back(("pair", n, lo))
             pg, b = divmod(n, B)
             rows = out[b, 2:4, pg * GRP : (pg + 1) * GRP, :].rearrange("h (p j) d -> p h j d", j=J)
             nc.sync.dma_start(
@@ -343,7 +394,7 @@ def tile_multiheadlatentattention_pa_t_kernel(
 
         def up_tokens(n, h, ring="v"):
             s, lo = q_place(n)
-            o = bank(ring, [P, J, P], F32)
+            o = bank(("out", n, h), ring, [P, J, P], F32)
             ws = slice(h * P, (h + 1) * P)
             for j in range(J):
                 cols = slice(lo + j * P, lo + (j + 1) * P)
@@ -365,12 +416,66 @@ def tile_multiheadlatentattention_pa_t_kernel(
                 in1=bias_row[:, h * P : (h + 1) * P].unsqueeze(1).to_broadcast([P, J, P]),
                 op=ADD,
             )
+            give_back(("out", n, h))
             store(n, h)
 
-        def table(pg, h):
+        def up_rows(n, a):
+            s, lo = q_place(n)
+            o = bank(("rows", n, a), "v", [P, 2, HALF], F32)
+            for jj in range(2):
+                cols = slice(lo + (2 * a + jj) * P, lo + (2 * a + jj + 1) * P)
+                nc.tensor.matmul_mx(
+                    out=o[:, jj, :],
+                    lhsT=codes[s][:, cols].bitcast(FP8X4),
+                    lhsT_scale=scales[s][:, cols],
+                    rhs=wuc[:].bitcast(FP8X4),
+                    rhs_scale=wus[:],
+                    start=True,
+                    stop=True,
+                )
+            m3[n, "rows", a] = o
+
+        def store_pair(n, heads, a):
+            pg, b = divmod(n, B)
+            rows = out[b, heads, pg * GRP : (pg + 1) * GRP, :].rearrange("h (p j) d -> p h j d", j=J)
+            nc.sync.dma_start(
+                out=rows[:, :, 2 * a : 2 * a + 2, :].rearrange("p h j d -> p h (j d)"),
+                in_=osb[n][:, heads, 2 * a : 2 * a + 2, :].rearrange("p h j d -> p h (j d)"),
+            )
+
+        def plain_rows(n, a):
+            result(n, 0)
+            t = osb[n][:, 0:2, 2 * a : 2 * a + 2, :]
+            nc.vector.tensor_tensor(
+                out=t,
+                in0=m3[n, "rows", a][:].rearrange("p j (h d) -> p h j d", h=2),
+                in1=bias_row[:].rearrange("p (h d) -> p h d", h=2).unsqueeze(2).to_broadcast([P, 2, 2, P]),
+                op=ADD,
+            )
+            give_back(("rows", n, a))
+            store_pair(n, slice(0, 2), a)
+
+        def products_rows(n, a, i):
+            pg = n // B
+            angles = rope[i, pg // 2][:, pg % 2, 2 * a : 2 * a + 2, :].rearrange("p j d -> p (j d)")
+            nc.vector.tensor_tensor(
+                out=products((n, "rows"))[:, a, i * GRP : (i + 1) * GRP].rearrange("p (h r) -> p h r", h=2),
+                in0=osb[n][:, 0:2, 2 * a : 2 * a + 2, :].rearrange("p h j d -> p h (j d)"),
+                in1=angles.unsqueeze(1).to_broadcast([P, 2, HG]),
+                op=MULT,
+            )
+
+        def rotated_rows(n, a):
+            t = osb[n][:, 2:4, 2 * a : 2 * a + 2, :].rearrange("p h j d -> p h (j d)")
+            x1c, x2c, x1s, x2s = (prod[n, "rows"][:, a, q * HG : (q + 1) * HG] for q in range(4))
+            nc.vector.tensor_tensor(out=t[:, 0, :], in0=x1c, in1=x2s, op=SUB)
+            nc.vector.tensor_tensor(out=t[:, 1, :], in0=x1s, in1=x2c, op=ADD)
+            store_pair(n, slice(2, 4), a)
+
+        def table(pg, h, copy=nc.scalar.copy):
             if pg not in tab:
                 tab[pg] = keep.tile([P, 2, 2 * GRP], BF16, name="tab%d" % pg, align_bytes=64)
-            o = bank("o", [P, 2, GRP], BF16)
+            o = bank(("tab", pg, h), "o", [P, 2, GRP], BF16)
             for i in range(2):
                 ident = idn if (h, i) == (1, 0) else idb
                 for j in range(J):
@@ -381,14 +486,16 @@ def tile_multiheadlatentattention_pa_t_kernel(
                         start=True,
                         stop=True,
                     )
-            nc.scalar.copy(out=tab[pg][:, :, h * GRP : (h + 1) * GRP], in_=o[:])
+            copy(out=tab[pg][:, :, h * GRP : (h + 1) * GRP], in_=o[:])
+            give_back(("tab", pg, h))
 
-        def turn_weights(w, g, pairs):
-            for h in range(pairs):
-                t = turn_words("o", w[:, 2 * h : 2 * h + 2, :].bitcast(F32))
-                nc.scalar.copy(
+        def turn_weights(w, g, pairs, copy=nc.scalar.copy):
+            for h in pairs:
+                t = turn_words("w", "o", w[:, 2 * h : 2 * h + 2, :].bitcast(F32))
+                copy(
                     out=g[:, h * 2 * P : (h + 1) * 2 * P, :].bitcast(F32), in_=t[:].rearrange("p u r -> p r u")
                 )
+                give_back("w")
 
         def quant_weights(g, c, z):
             nc.vector.quantize_mx(out=c[:].bitcast(FP8X4), scales=z[:], in_=g[:].rearrange("p r t -> p (r t)"))
@@ -397,16 +504,17 @@ def tile_multiheadlatentattention_pa_t_kernel(
         widen(0, nc.scalar.copy, 0, 1)
         widen(0, nc.scalar.copy, 1, 2)
         widen(1, nc.scalar.copy)
-        for jj in range(2):
-            turn(0, jj, jj + 1)
-            scale(0, jj, jj + 1)
+        turn(0, 0, 1)
+        scale(0, 0, 1)
+        turn(0, 1, 2)
+        scale(0, 1, 2)
         turn(1)
         scale(1)
         widen(2, nc.scalar.copy)
         turn(2)
         scale(2)
         widen(3, nc.scalar.copy)
-        turn_weights(wd, wdg, 2)
+        turn_weights(wd, wdg, (0, 1))
         turn(3)
         widen(4, nc.scalar.copy)
         quant_weights(wdg, wdc, wds)
@@ -423,7 +531,7 @@ def tile_multiheadlatentattention_pa_t_kernel(
         down(0, 2)
         scale(4)
         down(0, 3)
-        turn_weights(wu, wug, 1)
+        turn_weights(wu, wug, (0,))
         down_planes(1)
         lat_planes(1)
         table(0, 1)
@@ -439,105 +547,124 @@ def tile_multiheadlatentattention_pa_t_kernel(
         quant(0, 0, 2 * GRP)
         weave(1)
 
+        merge_rings()
         for s in range(1, last - 1):
             if s >= 2:
                 products_gpsimd(s - 2, NV)
             down_planes(s + 1)
-            if s >= 2:
-                half(s - 2, 0, 0, GRP - KP)
-            if s >= 3:
-                copy_out(s - 3, 3)
-            lat_planes(s + 1)
-            weave(s + 1)
-            if s < last - 2:
-                widen(2 * s + 7, nc.scalar.copy)
-            scale(2 * s + 3)
-            scale(2 * s + 4)
             down(s, 2)
             down(s, 3)
             up(s - 1, 1, "o")
-            up(s - 1, 0, "v")
-            half(s - 1, 1)
-            lat(s, 2)
-            lat(s, 3)
-            products_vector(s - 1, 0, NV)
             if s >= 2:
-                head_plain(s - 2, 0)
-            if s == last - 2:
-                table(3, 1)
+                half(s - 2, 0, 0, GRP - KP)
+                give_back(("up", s - 2, 0))
+            up(s - 1, 0, "v")
+            scale(2 * s + 3)
+            lat_planes(s + 1)
+            weave(s + 1)
+            if s >= 3:
+                turn_rotated(s - 3, 1)
+            if s >= 2:
+                turn_plain(s - 2, 0)
             turn(2 * s + 5)
+            scale(2 * s + 4)
+            if s < last - 2:
+                widen(2 * s + 7, nc.scalar.copy)
+            lat(s, 2)
+            half(s - 1, 1)
+            give_back(("up", s - 1, 1))
+            lat(s, 3)
+            if s >= 3:
+                copy_out(s - 3, 3)
+            if s >= 2:
+                copy_out(s - 2, 0)
             if s < last - 3:
                 widen(2 * s + 8, nc.scalar.copy)
             if s == 1:
                 table(2, 0)
                 table(2, 1)
                 table(3, 0)
+            if s == last - 2:
+                table(3, 1)
             if s >= 2:
-                head_rotated(s - 2, 0)
-            head_plain(s - 1, 1)
+                turn_rotated(s - 2, 0)
+            turn_plain(s - 1, 1)
             if s < last - 2:
                 turn(2 * s + 6)
-            if s >= 2:
+            else:
                 turn_rotated(s - 2, 1)
+            products_vector(s - 1, 0, NV)
+            if s >= 2:
+                copy_out(s - 2, 2)
+            copy_out(s - 1, 1)
             quant(s, 0, GRP)
             piece(s - 1, GRP - KP, GRP)
             quant(s, GRP, 2 * GRP)
 
         s = last - 1
         products_gpsimd(s - 2, NV)
-        half(s - 2, 0, 0, GRP - KP)
-        copy_out(s - 3, 3)
-        scale(2 * NG - 1)
         down(s, 2)
         down(s, 3)
         up(s - 1, 1, "o")
+        half(s - 2, 0, 0, GRP - KP)
+        give_back(("up", s - 2, 0))
+        copy_out(s - 3, 3)
         up(s - 1, 0, "v")
-        half(s - 1, 1)
-        lat(s, 2)
         down(last, 0)
-        lat(s, 3)
+        scale(2 * NG - 1)
         down(last, 1)
-        head_plain(s - 2, 0)
-        head_plain(s - 1, 1)
+        half(s - 1, 1)
+        give_back(("up", s - 1, 1))
+        turn_plain(s - 2, 0)
+        lat(s, 2)
+        lat(s, 3)
+        turn_plain(s - 1, 1)
+        turn_rotated(s - 2, 0)
+        copy_out(s - 2, 0)
+        turn_rotated(s - 2, 1)
+        copy_out(s - 1, 1)
         products_vector(s - 1, 0, NV)
         quant(last, 0, HG)
         piece(s - 1, GRP - KP, GRP)
         quant(s, GRP, 2 * GRP)
+        copy_out(s - 2, 2)
         half(s - 1, 0, 0, GRP - KP)
+        give_back(("up", s - 1, 0))
+        copy_out(s - 2, 3)
         products_gpsimd(s - 1, NV)
-        head_rotated(s - 2, 0)
-        lat(last, 0)
-        down(last, 2, "o")
-        lat(last, 1)
+        down(last, 2)
         down(last, 3)
         up(s, 1, "o")
+        lat(last, 0)
         up(s, 0, "v")
+        lat(last, 1)
         half(s, 1)
-        half(s, 0, 0, GRP - KP)
-        head_rotated(s - 2, 1)
+        give_back(("up", s, 1))
         head_plain(s - 1, 0)
         head_plain(s, 1)
         lat(last, 2)
         lat(last, 3)
+        products_vector(s, 0, NT)
         quant(s, 0, HG)
         piece(s, GRP - KP, GRP)
         quant(s, HG, GRP)
         products_gpsimd(s, NV)
-        products_vector(s, 0, NV)
+        products_vector(s, NT, NV)
         head_rotated(s - 1, 0)
+        up_rows(last, 0)
+        up_rows(last, 1)
+        turn_rotated(s - 1, 1)
+        half(s, 0, 0, GRP - KP)
+        give_back(("up", s, 0))
+        plain_rows(last, 0)
+        plain_rows(last, 1)
+        copy_out(s - 1, 3)
         head_plain(s, 0)
-        up(last, 1, "v")
-        up(last, 0, "v")
-        up_tokens(last, 0)
-        head_rotated(s - 1, 1)
-        products_vector(last, GRP, GRP + HG)
-        products_vector(last, 0, HG)
-        up_tokens(last, 1)
-        plain(last, 0)
-        both_rotated(last, 0, 2)
-        products_vector(last, GRP + HG, 2 * GRP)
-        products_vector(last, HG, GRP)
+        products_rows(last, 0, 0)
+        products_rows(last, 0, 1)
+        products_rows(last, 1, 0)
         head_rotated(s, 0)
-        plain(last, 1)
+        rotated_rows(last, 0)
+        products_rows(last, 1, 1)
         head_rotated(s, 1)
-        both_rotated(last, 2, 4)
+        rotated_rows(last, 1)

@@ -31,6 +31,7 @@ OUT_BUFS = 5
 PROD_BUFS = 4
 KT = 64
 NT = 192
+NH = 896
 
 
 def tile_multiheadlatentattention_pa_t_kernel(
@@ -301,11 +302,11 @@ def tile_multiheadlatentattention_pa_t_kernel(
                 prod[n] = sb.tile([P, 2, 2 * GRP], F32, name="prod", bufs=PROD_BUFS, align_bytes=64)
             return prod[n]
 
-        def products_gpsimd(n, lo):
+        def products_gpsimd(n, lo, hi=2 * GRP):
             nc.gpsimd.tensor_tensor(
-                out=products(n)[:, :, lo:],
-                in0=qt[n][:, lo:].unsqueeze(1).to_broadcast([P, 2, 2 * GRP - lo]),
-                in1=tab[n // B][:, :, lo:],
+                out=products(n)[:, :, lo:hi],
+                in0=qt[n][:, lo:hi].unsqueeze(1).to_broadcast([P, 2, hi - lo]),
+                in1=tab[n // B][:, :, lo:hi],
                 op=MULT,
             )
 
@@ -419,58 +420,23 @@ def tile_multiheadlatentattention_pa_t_kernel(
             give_back(("out", n, h))
             store(n, h)
 
-        def up_rows(n, a):
-            s, lo = q_place(n)
-            o = bank(("rows", n, a), "v", [P, 2, HALF], F32)
-            for jj in range(2):
-                cols = slice(lo + (2 * a + jj) * P, lo + (2 * a + jj + 1) * P)
-                nc.tensor.matmul_mx(
-                    out=o[:, jj, :],
-                    lhsT=codes[s][:, cols].bitcast(FP8X4),
-                    lhsT_scale=scales[s][:, cols],
-                    rhs=wuc[:].bitcast(FP8X4),
-                    rhs_scale=wus[:],
-                    start=True,
-                    stop=True,
-                )
-            m3[n, "rows", a] = o
-
-        def store_pair(n, heads, a):
-            pg, b = divmod(n, B)
-            rows = out[b, heads, pg * GRP : (pg + 1) * GRP, :].rearrange("h (p j) d -> p h j d", j=J)
-            nc.sync.dma_start(
-                out=rows[:, :, 2 * a : 2 * a + 2, :].rearrange("p h j d -> p h (j d)"),
-                in_=osb[n][:, heads, 2 * a : 2 * a + 2, :].rearrange("p h j d -> p h (j d)"),
-            )
-
-        def plain_rows(n, a):
-            result(n, 0)
-            t = osb[n][:, 0:2, 2 * a : 2 * a + 2, :]
-            nc.vector.tensor_tensor(
-                out=t,
-                in0=m3[n, "rows", a][:].rearrange("p j (h d) -> p h j d", h=2),
-                in1=bias_row[:].rearrange("p (h d) -> p h d", h=2).unsqueeze(2).to_broadcast([P, 2, 2, P]),
-                op=ADD,
-            )
-            give_back(("rows", n, a))
-            store_pair(n, slice(0, 2), a)
-
-        def products_rows(n, a, i):
+        def product_rows(n, h, i):
             pg = n // B
-            angles = rope[i, pg // 2][:, pg % 2, 2 * a : 2 * a + 2, :].rearrange("p j d -> p (j d)")
             nc.vector.tensor_tensor(
-                out=products((n, "rows"))[:, a, i * GRP : (i + 1) * GRP].rearrange("p (h r) -> p h r", h=2),
-                in0=osb[n][:, 0:2, 2 * a : 2 * a + 2, :].rearrange("p h j d -> p h (j d)"),
-                in1=angles.unsqueeze(1).to_broadcast([P, 2, HG]),
+                out=products(n)[:, h, i * GRP : (i + 1) * GRP],
+                in0=result(n, h).rearrange("p j d -> p (j d)"),
+                in1=rope[i, pg // 2][:, pg % 2, :, :].rearrange("p j d -> p (j d)"),
                 op=MULT,
             )
 
-        def rotated_rows(n, a):
-            t = osb[n][:, 2:4, 2 * a : 2 * a + 2, :].rearrange("p h j d -> p h (j d)")
-            x1c, x2c, x1s, x2s = (prod[n, "rows"][:, a, q * HG : (q + 1) * HG] for q in range(4))
-            nc.vector.tensor_tensor(out=t[:, 0, :], in0=x1c, in1=x2s, op=SUB)
-            nc.vector.tensor_tensor(out=t[:, 1, :], in0=x1s, in1=x2c, op=ADD)
-            store_pair(n, slice(2, 4), a)
+        def rotated_rows(n, i):
+            nc.vector.tensor_tensor(
+                out=result(n, 2 + i).rearrange("p j d -> p (j d)"),
+                in0=prod[n][:, 0, i * GRP : (i + 1) * GRP],
+                in1=prod[n][:, 1, (1 - i) * GRP : (2 - i) * GRP],
+                op=(SUB, ADD)[i],
+            )
+            store(n, 2 + i)
 
         def table(pg, h, copy=nc.scalar.copy):
             if pg not in tab:
@@ -627,19 +593,18 @@ def tile_multiheadlatentattention_pa_t_kernel(
         quant(last, 0, HG)
         piece(s - 1, GRP - KP, GRP)
         quant(s, GRP, 2 * GRP)
+        products_gpsimd(s - 1, NV)
         copy_out(s - 2, 2)
         half(s - 1, 0, 0, GRP - KP)
         give_back(("up", s - 1, 0))
-        copy_out(s - 2, 3)
-        products_gpsimd(s - 1, NV)
         down(last, 2)
-        down(last, 3)
         up(s, 1, "o")
+        down(last, 3)
         lat(last, 0)
         up(s, 0, "v")
+        copy_out(s - 2, 3)
         lat(last, 1)
         half(s, 1)
-        give_back(("up", s, 1))
         head_plain(s - 1, 0)
         head_plain(s, 1)
         lat(last, 2)
@@ -648,23 +613,25 @@ def tile_multiheadlatentattention_pa_t_kernel(
         quant(s, 0, HG)
         piece(s, GRP - KP, GRP)
         quant(s, HG, GRP)
-        products_gpsimd(s, NV)
+        products_gpsimd(s, NV, NH)
         products_vector(s, NT, NV)
-        head_rotated(s - 1, 0)
-        up_rows(last, 0)
-        up_rows(last, 1)
-        turn_rotated(s - 1, 1)
+        products_vector(s, NH, 2 * GRP)
+        give_back(("up", s, 1))
+        turn_rotated(s - 1, 0)
+        up_tokens(last, 0)
+        up_tokens(last, 1)
+        copy_out(s - 1, 2)
         half(s, 0, 0, GRP - KP)
         give_back(("up", s, 0))
-        plain_rows(last, 0)
-        plain_rows(last, 1)
-        copy_out(s - 1, 3)
+        plain(last, 0)
+        plain(last, 1)
+        head_rotated(s - 1, 1)
         head_plain(s, 0)
-        products_rows(last, 0, 0)
-        products_rows(last, 0, 1)
-        products_rows(last, 1, 0)
-        head_rotated(s, 0)
+        product_rows(last, 0, 0)
+        product_rows(last, 1, 1)
+        product_rows(last, 0, 1)
         rotated_rows(last, 0)
-        products_rows(last, 1, 1)
+        head_rotated(s, 0)
+        product_rows(last, 1, 0)
         head_rotated(s, 1)
         rotated_rows(last, 1)

@@ -25,13 +25,8 @@ HG = GRP // 2
 PG = S // GRP
 NG = B * PG
 SLOTS = 4
-NV = 480
-KP = 32
+KP = 256
 OUT_BUFS = 5
-PROD_BUFS = 4
-KT = 64
-NT = 192
-NH = 896
 
 
 def tile_multiheadlatentattention_pa_t_kernel(
@@ -44,24 +39,16 @@ def tile_multiheadlatentattention_pa_t_kernel(
         ps = ctx.enter_context(tc.psum_pool(name="ps", bufs=1))
         ctx.enter_context(tc.manual_schedule())
 
-        free = {"v": list(range(0, 4)), "o": list(range(4, 8))}
+        free = list(range(8))
         held = {}
-        merged = []
 
-        def bank(key, ring, shape, dtype):
-            if merged:
-                ring = "v"
-            i = free[ring].pop(0)
-            held[key] = (ps.tile(shape, dtype, name="bank%d" % i), ring, i)
+        def bank(key, shape, dtype):
+            i = free.pop(0)
+            held[key] = (ps.tile(shape, dtype, name="bank%d" % i), i)
             return held[key][0]
 
         def give_back(key):
-            t, ring, i = held.pop(key)
-            free["v" if merged else ring].append(i)
-
-        def merge_rings():
-            merged.append(1)
-            free["v"].extend(free["o"])
+            free.append(held.pop(key)[1])
 
         xb = {}
 
@@ -75,39 +62,39 @@ def tile_multiheadlatentattention_pa_t_kernel(
 
         rope = {}
 
-        def load_rope(pair):
+        def load_rope(lo, hi):
             for i, src in enumerate((rope_cos, rope_sin)):
-                t = keep.tile([P, 2, J, P], BF16, name="rope%d_%d" % (i, pair), align_bytes=64)
+                t = keep.tile([P, hi - lo, J, P], BF16, name="rope%d_%d" % (i, lo), align_bytes=64)
                 nc.sync.dma_start(
-                    out=t[:],
-                    in_=src[pair * 2 * GRP : (pair + 1) * 2 * GRP, :].rearrange("(g p j) c -> p g j c", p=P, j=J),
+                    out=t[:], in_=src[lo * GRP : hi * GRP, :].rearrange("(g p j) c -> p g j c", p=P, j=J)
                 )
-                rope[i, pair] = t
+                for pg in range(lo, hi):
+                    rope[i, pg] = t[:, pg - lo, :, :]
 
         sc = keep.tile([P, T4], F32, name="sc")
         wd = keep.tile([P, T4, H], BF16, name="wd", align_bytes=64)
         wd_rows = wq_down.rearrange("(m t) k -> m t k", t=T4)
         bd = keep.tile([P, T4], BF16, name="bd")
         wu = keep.tile([P, 2, LAT], BF16, name="wu", align_bytes=64)
-        load_x(0, (0, 1, 2, J))
+        bu = keep.tile([P, 2, 2], BF16, name="bu")
+        bias_row = keep.tile([P, HALF], BF16, name="bias_row")
+        load_x(0, (0, 1))
         nc.sync.dma_start(out=sc[:], in_=x_scale.rearrange("a b (p t) -> p (a b t)", t=T4))
-        load_x(1, (0, 2))
+        load_x(0, (1, 2, J))
         nc.sync.dma_start(out=wd[:, 0:2, :], in_=wd_rows[:, 0:2, :])
+        load_x(1, (0, 2))
         nc.sync.dma_start(out=wd[:, 2:4, :], in_=wd_rows[:, 2:4, :])
         load_x(1, (2, J))
-        nc.sync.dma_start(out=bd[:], in_=bq_down.rearrange("(p t) -> p t", t=T4))
         load_x(2, (0, J))
-        load_rope(0)
+        nc.sync.dma_start(out=bd[:], in_=bq_down.rearrange("(p t) -> p t", t=T4))
+        load_rope(0, 1)
         nc.sync.dma_start(out=wu[:], in_=wq_up.rearrange("(h m) k -> m h k", h=2))
         load_x(3, (0, J))
-        load_rope(1)
-        bu = keep.tile([P, 2, 2], BF16, name="bu")
         with nc.allow_non_contiguous_dma(reason="one bias value for each partition and half"):
             nc.sync.dma_start(out=bu[:, :, 0:1], in_=bq_up.rearrange("(h c o) -> c h o", h=2, o=1))
-        load_x(4, (0, J))
-        for n in range(5, NG):
+        load_rope(1, 4)
+        for n in range(4, NG):
             load_x(n, (0, J))
-        bias_row = keep.tile([P, HALF], BF16, name="bias_row")
         nc.sync.dma_start(out=bias_row[:], in_=bq_up.partition_broadcast(P))
 
         idf = keep.tile([P, P], F32, name="idf")
@@ -121,202 +108,194 @@ def tile_multiheadlatentattention_pa_t_kernel(
         wds = keep.tile([P, LAT], U8, name="wds", align_bytes=64)
         wuc = keep.tile([P, HALF], U32, name="wuc", align_bytes=64)
         wus = keep.tile([P, HALF], U8, name="wus", align_bytes=64)
-        wdg = sb.tile([P, LAT, T4], BF16, name="slot0", bufs=1, align_bytes=64)
-        wug = sb.tile([P, HALF, T4], BF16, name="slot1", bufs=1, align_bytes=64)
+        wdg = keep.tile([P, LAT, T4], BF16, name="wdg", align_bytes=64)
+        wug = keep.tile([P, HALF, T4], BF16, name="wug", align_bytes=64)
+        bsum = keep.tile([P, 1], F32, name="bsum")
+        tcos = keep.tile([P, PG, GRP], BF16, name="tcos", align_bytes=64)
+        tmix = keep.tile([P, PG, 2, GRP], F32, name="tmix", align_bytes=64)
 
-        xbf, xt, staged, codes, scales, m1, m2, m3, planes, qt, prod, tab, osb, written = ({} for i in range(14))
+        xbf, xt, xs, xc, xz, ls, lc, lz, m1, m2, m3, planes, qt, pg2, pv, osb, written, rows = ({} for i in range(18))
 
-        def widen(m, copy, lo=0, hi=2):
+        def widen(m, lo=0, hi=2):
             if lo == 0:
                 xbf[m] = sb.tile([P, 2, H], BF16, name="xbf", bufs=6, align_bytes=64)
             j = 2 * (m % 2)
-            copy(out=xbf[m][:, lo:hi, :], in_=xb[m // 2][:, j + lo : j + hi, :].bitcast(FP8))
+            nc.scalar.copy(out=xbf[m][:, lo:hi, :], in_=xb[m // 2][:, j + lo : j + hi, :].bitcast(FP8))
 
-        def turn_words(key, ring, words):
+        def turn_words(key, words):
             tiles = words.shape[1]
-            t = bank(key, ring, [P, 2, tiles * P], F32)
+            t = bank(key, [P, 2, tiles * P], F32)
             for jj in range(tiles):
                 for u in range(2):
                     nc.tensor.transpose(t[:, u, jj * P : (jj + 1) * P], words[:, jj, u : H // 2 : 2], idf[:])
             return t
 
         def turn(m, lo=0, hi=2):
-            xt[m, lo] = turn_words(("x", m, lo), "v", xbf[m][:, lo:hi, :].bitcast(F32))
+            t = turn_words(("x", m, lo), xbf[m][:, lo:hi, :].bitcast(F32))
+            xt[m, lo] = t[:].bitcast(BF16).rearrange("p u (r e) -> p r u e", e=2)
 
-        def staging(s):
-            if s not in staged:
-                staged[s] = sb.tile([P, 2 * GRP, T4], BF16, name="slot%d" % (s % SLOTS), bufs=1, align_bytes=64)
-            return staged[s]
+        def turn_mm(m, lo=0, hi=2):
+            t = bank(("x", m, lo), [P, T4, (hi - lo) * P], BF16)
+            for jj in range(lo, hi):
+                for k in range(T4):
+                    nc.tensor.matmul(
+                        t[:, k, (jj - lo) * P : (jj - lo + 1) * P],
+                        lhsT=xbf[m][:, jj, k:H:T4],
+                        rhs=idb[:],
+                        start=True,
+                        stop=True,
+                    )
+            xt[m, lo] = t[:].rearrange("p (u e) r -> p r u e", e=2)
 
         def x_place(m):
-            return divmod(m - 3, 2) if m < 2 * NG - 1 else (NG - 1, 0)
-
-        def q_place(n):
-            return (n, GRP) if n < NG - 1 else (NG - 2, 0)
+            return divmod(m - 3, 2) if m < 2 * NG - 1 else (NG - 2, 0)
 
         def scale(m, lo=0, hi=2):
             s, pos = x_place(m)
+            if s not in xs:
+                xs[s] = sb.tile([P, GRP, T4], BF16, name="slot%d" % (s % SLOTS), bufs=1, align_bytes=64)
             nc.vector.tensor_tensor(
-                out=staging(s)[:, pos * HG + lo * P : pos * HG + hi * P, :].rearrange("p r (u e) -> p r u e", e=2),
-                in0=xt[m, lo][:].bitcast(BF16).rearrange("p u (r e) -> p r u e", e=2),
+                out=xs[s][:, pos * HG + lo * P : pos * HG + hi * P, :].rearrange("p r (u e) -> p r u e", e=2),
+                in0=xt[m, lo],
                 in1=sc[:].rearrange("p (u e) -> p u e", e=2).unsqueeze(1).to_broadcast([P, (hi - lo) * P, 2, 2]),
                 op=MULT,
             )
             give_back(("x", m, lo))
 
-        def quant(s, lo, hi):
+        def quant(codes, scales, staged, name, s, lo, hi):
             if s not in codes:
-                codes[s] = sb.tile([P, 2 * GRP], U32, name="codes", bufs=4, align_bytes=64)
-                scales[s] = sb.tile([P, 2 * GRP], U8, name="scales", bufs=4, align_bytes=64)
+                codes[s] = sb.tile([P, GRP], U32, name=name + "c", bufs=4, align_bytes=64)
+                scales[s] = sb.tile([P, GRP], U8, name=name + "z", bufs=4, align_bytes=64)
             nc.vector.quantize_mx(
                 out=codes[s][:, lo:hi].bitcast(FP8X4),
                 scales=scales[s][:, lo:hi],
                 in_=staged[s][:, lo:hi, :].rearrange("p r t -> p (r t)"),
             )
 
-        def down_pass(dst, t, s, cols):
-            ws = slice(t * P, (t + 1) * P)
+        def quant_x(s, lo=0, hi=GRP):
+            quant(xc, xz, xs, "x", s, lo, hi)
+
+        def quant_lat(n, lo=0, hi=GRP):
+            quant(lc, lz, ls, "l", n, lo, hi)
+
+        def mx(dst, wc, wz, ws, codes, scales, cols, start=True, stop=True):
             nc.tensor.matmul_mx(
                 out=dst,
-                lhsT=wdc[:, ws].bitcast(FP8X4),
-                lhsT_scale=wds[:, ws],
-                rhs=codes[s][:, cols].bitcast(FP8X4),
-                rhs_scale=scales[s][:, cols],
-                start=True,
-                stop=True,
+                lhsT=wc[:, ws].bitcast(FP8X4),
+                lhsT_scale=wz[:, ws],
+                rhs=codes[:, cols].bitcast(FP8X4),
+                rhs_scale=scales[:, cols],
+                start=start,
+                stop=stop,
             )
 
-        def down(n, j, ring="v"):
-            o = bank(("lat", n, j), ring, [P, T4, P], F32)
+        def down(n, j):
+            o = bank(("lat", n, j), [P, T4, P], F32)
             s, pos = x_place(2 * n + j // 2)
             lo = pos * HG + (j % 2) * P
             for t in range(T4):
-                down_pass(o[:, t, :], t, s, slice(lo, lo + P))
+                mx(o[:, t, :], wdc, wds, slice(t * P, (t + 1) * P), xc[s], xz[s], slice(lo, lo + P))
             m1[n, j] = o
 
+        def lat_stage(n):
+            if n not in ls:
+                ls[n] = sb.tile([P, GRP, T4], BF16, name="lstage%d" % (min(n, NG - 2) % 3), bufs=1, align_bytes=64)
+            return ls[n]
+
         def lat(n, j):
-            s, lo = q_place(n)
             nc.vector.tensor_tensor(
-                out=staging(s)[:, lo + j * P : lo + (j + 1) * P, :],
+                out=lat_stage(n)[:, j * P : (j + 1) * P, :],
                 in0=m1[n, j][:].rearrange("p t r -> p r t"),
                 in1=bd[:].unsqueeze(1).to_broadcast([P, P, T4]),
                 op=ADD,
             )
             give_back(("lat", n, j))
 
-        def down_planes(n):
-            s, pos = x_place(2 * n)
+        def down_planes(m):
+            s, pos = x_place(m)
             for pair in range(2):
-                m1[n, "planes", pair] = bank(("planes", n, pair), "o", [P, 2, HG], F32)
+                m1[m, "planes", pair] = bank(("planes", m, pair), [P, 2, HG], F32)
                 for e in range(2):
-                    down_pass(m1[n, "planes", pair][:, e, :], 2 * pair + e, s, slice(pos * HG, (pos + 1) * HG))
+                    t = 2 * pair + e
+                    mx(
+                        m1[m, "planes", pair][:, e, :], wdc, wds, slice(t * P, (t + 1) * P),
+                        xc[s], xz[s], slice(pos * HG, (pos + 1) * HG),
+                    )
 
-        def biased(n):
-            if n not in qt:
-                qt[n] = sb.tile([P, 2 * GRP], F32, name="qt", bufs=5, align_bytes=64)
-            return qt[n]
-
-        def lat_planes(n):
-            planes[n] = biased(n - 1)[:, 0:GRP].bitcast(BF16).rearrange("p (t r) -> p t r", t=T4)
+        def lat_planes(m):
+            planes[m] = sb.tile([P, T4, HG], BF16, name="planes", bufs=3, align_bytes=64)
             for t in range(T4):
                 nc.scalar.activation(
-                    out=planes[n][:, t, :], in_=m1[n, "planes", t // 2][:, t % 2, :], func=IDENT, bias=bd[:, t : t + 1]
+                    out=planes[m][:, t, :], in_=m1[m, "planes", t // 2][:, t % 2, :], func=IDENT, bias=bd[:, t : t + 1]
                 )
                 if t % 2:
-                    give_back(("planes", n, t // 2))
+                    give_back(("planes", m, t // 2))
 
-        def weave(n):
+        def weave(m):
+            n, a = divmod(m, 2)
             nc.gpsimd.tensor_scalar(
-                out=staging(n)[:, GRP : GRP + HG, :],
-                in0=planes[n].rearrange("p t r -> p r t"),
+                out=lat_stage(n)[:, a * HG : (a + 1) * HG, :],
+                in0=planes[m][:].rearrange("p t r -> p r t"),
                 scalar1=1.0,
                 scalar2=0.0,
                 op0=MULT,
                 op1=ADD,
             )
 
-        def up(n, h, ring):
-            s, lo = q_place(n)
-            o = bank(("up", n, h), ring, [P, GRP], F32)
-            ws = slice(h * P, (h + 1) * P)
-            nc.tensor.matmul_mx(
-                out=o[:],
-                lhsT=wuc[:, ws].bitcast(FP8X4),
-                lhsT_scale=wus[:, ws],
-                rhs=codes[s][:, lo : lo + GRP].bitcast(FP8X4),
-                rhs_scale=scales[s][:, lo : lo + GRP],
-                start=True,
-                stop=True,
-            )
+        def up(n, h):
+            o = bank(("up", n, h), [P, GRP], F32)
+            mx(o[:], wuc, wus, slice(h * P, (h + 1) * P), lc[n], lz[n], slice(0, GRP))
             m2[n, h] = o
 
-        def up_both(n, a):
-            s, lo = q_place(n)
-            o = bank(("both", n, a), "v", [P, 2, HG], F32)
-            cols = slice(lo + a * HG, lo + (a + 1) * HG)
+        def up_sum(n):
+            o = bank(("sum", n), [P, GRP], F32)
             for h in range(2):
-                ws = slice(h * P, (h + 1) * P)
-                nc.tensor.matmul_mx(
-                    out=o[:, h, :],
-                    lhsT=wuc[:, ws].bitcast(FP8X4),
-                    lhsT_scale=wus[:, ws],
-                    rhs=codes[s][:, cols].bitcast(FP8X4),
-                    rhs_scale=scales[s][:, cols],
-                    start=True,
-                    stop=True,
-                )
-            m2[n, "both", a] = o
+                mx(o[:], wuc, wus, slice(h * P, (h + 1) * P), lc[n], lz[n], slice(0, GRP), h == 0, h == 1)
+            m2[n, "sum"] = o
 
-        def products_last(n, a):
-            for h in range(2):
-                cols = slice(h * GRP + a * HG, h * GRP + (a + 1) * HG)
-                nc.vector.scalar_tensor_tensor(
-                    out=products(n)[:, :, cols],
-                    in0=m2[n, "both", a][:, h, :].unsqueeze(1).to_broadcast([P, 2, HG]),
-                    scalar=bu[:, h, 0:1],
-                    in1=tab[n // B][:, :, cols],
-                    op0=ADD,
-                    op1=MULT,
-                )
-            give_back(("both", n, a))
+        def up_more(n):
+            o = m2[n, 0]
+            mx(o[:], wuc, wus, slice(P, 2 * P), lc[n], lz[n], slice(0, GRP), False, True)
+            m2[n, "sum"] = o
+            held["sum", n] = held.pop(("up", n, 0))
+
+        def biased(n):
+            if n not in qt:
+                qt[n] = sb.tile([P, 2, GRP], F32, name="qt", bufs=4, align_bytes=64)
+            return qt[n]
 
         def half(n, h, lo=0, hi=GRP):
-            biased(n)
-            nc.scalar.activation(
-                out=qt[n][:, h * GRP + lo : h * GRP + hi], in_=m2[n, h][:, lo:hi], func=IDENT, bias=bu[:, h, 0:1]
-            )
+            nc.scalar.activation(out=biased(n)[:, h, lo:hi], in_=m2[n, h][:, lo:hi], func=IDENT, bias=bu[:, h, 0:1])
 
-        def piece(n, lo, hi):
-            biased(n)
-            h = lo // GRP
+        def piece(n, h, lo=0, hi=GRP):
             nc.vector.tensor_scalar(
-                out=qt[n][:, lo:hi],
-                in0=m2[n, h][:, lo - h * GRP : hi - h * GRP],
-                scalar1=bu[:, h, 0:1],
-                scalar2=None,
-                op0=ADD,
+                out=biased(n)[:, h, lo:hi], in0=m2[n, h][:, lo:hi], scalar1=bu[:, h, 0:1], scalar2=None, op0=ADD
             )
 
-        def products(n):
-            if n not in prod:
-                prod[n] = sb.tile([P, 2, 2 * GRP], F32, name="prod", bufs=PROD_BUFS, align_bytes=64)
-            return prod[n]
-
-        def products_gpsimd(n, lo, hi=2 * GRP):
-            nc.gpsimd.tensor_tensor(
-                out=products(n)[:, :, lo:hi],
-                in0=qt[n][:, lo:hi].unsqueeze(1).to_broadcast([P, 2, hi - lo]),
-                in1=tab[n // B][:, :, lo:hi],
-                op=MULT,
-            )
-
-        def products_vector(n, lo, hi):
-            h = lo // GRP
+        def common(n):
+            pv[n] = sb.tile([P, GRP], F32, name="pv", bufs=4, align_bytes=64)
             nc.vector.scalar_tensor_tensor(
-                out=products(n)[:, :, lo:hi],
-                in0=m2[n, h][:, lo - h * GRP : hi - h * GRP].unsqueeze(1).to_broadcast([P, 2, hi - lo]),
+                out=pv[n][:], in0=m2[n, "sum"][:], scalar=bsum[:], in1=tcos[:, n // B, :], op0=ADD, op1=MULT
+            )
+            give_back(("sum", n))
+
+        def mixed_tile(n, s):
+            if n not in pg2:
+                name = "lstage%d" % ((NG - 2) % 3) if s == "l" else "slot%d" % (s % SLOTS)
+                pg2[n] = sb.tile([P, 2, GRP], F32, name=name, bufs=1, align_bytes=64)
+            return pg2[n]
+
+        def mixed(n, s, lo=0, hi=GRP):
+            nc.gpsimd.tensor_tensor(
+                out=mixed_tile(n, s)[:, :, lo:hi], in0=qt[n][:, :, lo:hi], in1=tmix[:, n // B, :, lo:hi], op=MULT
+            )
+
+        def mixed_vector(n, s, h, lo=0, hi=GRP):
+            nc.vector.scalar_tensor_tensor(
+                out=mixed_tile(n, s)[:, h, lo:hi],
+                in0=m2[n, h][:, lo:hi],
                 scalar=bu[:, h, 0:1],
-                in1=tab[n // B][:, :, lo:hi],
+                in1=tmix[:, n // B, h, lo:hi],
                 op0=ADD,
                 op1=MULT,
             )
@@ -334,80 +313,33 @@ def tile_multiheadlatentattention_pa_t_kernel(
                     return
                 heads = slice(0, 4)
             pg, b = divmod(n, B)
-            rows = out[b, heads, pg * GRP : (pg + 1) * GRP, :].rearrange("h (p j) d -> p h (j d)", j=J)
-            nc.sync.dma_start(out=rows, in_=osb[n][:, heads, :, :].rearrange("p h j d -> p h (j d)"))
+            dst = out[b, heads, pg * GRP : (pg + 1) * GRP, :].rearrange("h (p j) d -> p h (j d)", j=J)
+            nc.sync.dma_start(out=dst, in_=osb[n][:, heads, :, :].rearrange("p h j d -> p h (j d)"))
 
         def turn_plain(n, h):
-            o = bank(("out", n, h), "o", [P, J, P], F32)
+            o = bank(("out", n, h), [P, J, P], F32)
             for j in range(J):
-                nc.tensor.transpose(o[:, j, :], qt[n][:, h * GRP + j * P : h * GRP + (j + 1) * P], idf[:])
+                nc.tensor.transpose(o[:, j, :], qt[n][:, h, j * P : (j + 1) * P], idf[:])
             m3[n, h] = o
 
-        def head_plain(n, h):
-            turn_plain(n, h)
-            copy_out(n, h)
-
         def turn_rotated(n, i):
-            o = bank(("out", n, 2 + i), "o", [P, J, P], F32)
+            o = bank(("out", n, 2 + i), [P, J, P], F32)
             for j in range(J):
-                for h in range(2):
-                    nc.tensor.matmul(
-                        o[:, j, :],
-                        lhsT=prod[n][:, i, h * GRP + j * P : h * GRP + (j + 1) * P],
-                        rhs=idf[:],
-                        start=h == 0,
-                        stop=h == 1,
-                        is_transpose=True,
-                    )
+                cols = slice(j * P, (j + 1) * P)
+                for k, term in enumerate((pv[n][:, cols], pg2[n][:, 1 - i, cols])):
+                    nc.tensor.matmul(o[:, j, :], lhsT=term, rhs=idf[:], start=k == 0, stop=k == 1, is_transpose=True)
             m3[n, 2 + i] = o
 
-        def copy_out(n, h):
-            nc.scalar.copy(out=result(n, h), in_=m3[n, h][:])
+        def copy_out(n, h, copy=nc.scalar.copy):
+            copy(out=result(n, h), in_=m3[n, h][:])
             give_back(("out", n, h))
             store(n, h)
 
-        def head_rotated(n, i):
-            turn_rotated(n, i)
-            copy_out(n, 2 + i)
-
-        def both_rotated(n, lo, hi):
-            o = bank(("pair", n, lo), "o", [P, 2, hi - lo, P], F32)
-            for i in range(2):
-                for j in range(lo, hi):
-                    for h in range(2):
-                        nc.tensor.matmul(
-                            o[:, i, j - lo, :],
-                            lhsT=prod[n][:, i, h * GRP + j * P : h * GRP + (j + 1) * P],
-                            rhs=idf[:],
-                            start=h == 0,
-                            stop=h == 1,
-                            is_transpose=True,
-                        )
-            result(n, 2)
-            t = osb[n][:, 2:4, lo:hi, :]
-            nc.scalar.copy(out=t, in_=o[:])
-            give_back(("pair", n, lo))
-            pg, b = divmod(n, B)
-            rows = out[b, 2:4, pg * GRP : (pg + 1) * GRP, :].rearrange("h (p j) d -> p h j d", j=J)
-            nc.sync.dma_start(
-                out=rows[:, :, lo:hi, :].rearrange("p h j d -> p h (j d)"), in_=t.rearrange("p h j d -> p h (j d)")
-            )
-
-        def up_tokens(n, h, ring="v"):
-            s, lo = q_place(n)
-            o = bank(("out", n, h), ring, [P, J, P], F32)
+        def up_tokens(n, h):
+            o = bank(("out", n, h), [P, J, P], F32)
             ws = slice(h * P, (h + 1) * P)
             for j in range(J):
-                cols = slice(lo + j * P, lo + (j + 1) * P)
-                nc.tensor.matmul_mx(
-                    out=o[:, j, :],
-                    lhsT=codes[s][:, cols].bitcast(FP8X4),
-                    lhsT_scale=scales[s][:, cols],
-                    rhs=wuc[:, ws].bitcast(FP8X4),
-                    rhs_scale=wus[:, ws],
-                    start=True,
-                    stop=True,
-                )
+                mx(o[:, j, :], lc[n], lz[n], slice(j * P, (j + 1) * P), wuc, wus, ws)
             m3[n, h] = o
 
         def plain(n, h):
@@ -421,217 +353,265 @@ def tile_multiheadlatentattention_pa_t_kernel(
             store(n, h)
 
         def product_rows(n, h, i):
-            pg = n // B
+            if n not in rows:
+                rows[n] = sb.tile([P, 2, 2, GRP], F32, name="rows", bufs=1, align_bytes=64)
             nc.vector.tensor_tensor(
-                out=products(n)[:, h, i * GRP : (i + 1) * GRP],
+                out=rows[n][:, h, i, :],
                 in0=result(n, h).rearrange("p j d -> p (j d)"),
-                in1=rope[i, pg // 2][:, pg % 2, :, :].rearrange("p j d -> p (j d)"),
+                in1=rope[i, n // B].rearrange("p j d -> p (j d)"),
                 op=MULT,
             )
 
         def rotated_rows(n, i):
             nc.vector.tensor_tensor(
                 out=result(n, 2 + i).rearrange("p j d -> p (j d)"),
-                in0=prod[n][:, 0, i * GRP : (i + 1) * GRP],
-                in1=prod[n][:, 1, (1 - i) * GRP : (2 - i) * GRP],
+                in0=rows[n][:, 0, i, :],
+                in1=rows[n][:, 1, 1 - i, :],
                 op=(SUB, ADD)[i],
             )
             store(n, 2 + i)
 
-        def table(pg, h, copy=nc.scalar.copy):
-            if pg not in tab:
-                tab[pg] = keep.tile([P, 2, 2 * GRP], BF16, name="tab%d" % pg, align_bytes=64)
-            o = bank(("tab", pg, h), "o", [P, 2, GRP], BF16)
-            for i in range(2):
-                ident = idn if (h, i) == (1, 0) else idb
-                for j in range(J):
+        def turn_table(pg, k):
+            terms = (((1, idb), (0, idn)), ((1, idn), (0, idn)), ((0, idb),))[k]
+            o = bank(("tab", pg, k), [P, J, P], BF16 if k == 2 else F32)
+            for j in range(J):
+                for a, (i, ident) in enumerate(terms):
                     nc.tensor.matmul(
-                        o[:, i, j * P : (j + 1) * P],
-                        lhsT=rope[(h + i) % 2, pg // 2][:, pg % 2, j, :],
-                        rhs=ident[:],
-                        start=True,
-                        stop=True,
+                        o[:, j, :], lhsT=rope[i, pg][:, j, :], rhs=ident[:], start=a == 0, stop=a == len(terms) - 1
                     )
-            copy(out=tab[pg][:, :, h * GRP : (h + 1) * GRP], in_=o[:])
-            give_back(("tab", pg, h))
+            m3["tab", pg, k] = o
 
-        def turn_weights(w, g, pairs, copy=nc.scalar.copy):
-            for h in pairs:
-                t = turn_words("w", "o", w[:, 2 * h : 2 * h + 2, :].bitcast(F32))
-                copy(
-                    out=g[:, h * 2 * P : (h + 1) * 2 * P, :].bitcast(F32), in_=t[:].rearrange("p u r -> p r u")
-                )
-                give_back("w")
+        def copy_table(pg, k, copy=nc.scalar.copy):
+            dst = tcos[:, pg, :] if k == 2 else tmix[:, pg, k, :]
+            copy(out=dst, in_=m3["tab", pg, k][:].rearrange("p j r -> p (j r)"))
+            give_back(("tab", pg, k))
+
+        def table(pg, k):
+            turn_table(pg, k)
+            copy_table(pg, k)
+
+        def turn_weights(w, h, key):
+            m3[key] = turn_words(key, w[:, 2 * h : 2 * h + 2, :].bitcast(F32))
+
+        def copy_weights(g, h, key):
+            nc.scalar.copy(
+                out=g[:, h * 2 * P : (h + 1) * 2 * P, :].bitcast(F32), in_=m3[key][:].rearrange("p u r -> p r u")
+            )
+            give_back(key)
 
         def quant_weights(g, c, z):
             nc.vector.quantize_mx(out=c[:].bitcast(FP8X4), scales=z[:], in_=g[:].rearrange("p r t -> p (r t)"))
 
-        last = NG - 1
-        widen(0, nc.scalar.copy, 0, 1)
-        widen(0, nc.scalar.copy, 1, 2)
-        widen(1, nc.scalar.copy)
-        turn(0, 0, 1)
-        scale(0, 0, 1)
-        turn(0, 1, 2)
-        scale(0, 1, 2)
-        turn(1)
-        scale(1)
-        widen(2, nc.scalar.copy)
-        turn(2)
-        scale(2)
-        widen(3, nc.scalar.copy)
-        turn_weights(wd, wdg, (0, 1))
-        turn(3)
-        widen(4, nc.scalar.copy)
-        quant_weights(wdg, wdc, wds)
-        quant(-2, HG, GRP)
-        quant(-1, 0, GRP)
-        widen(5, nc.scalar.copy)
-        table(0, 0)
-        turn(4)
-        widen(6, nc.scalar.copy)
-        scale(3)
-        down_planes(0)
-        lat_planes(0)
-        weave(0)
-        down(0, 2)
-        scale(4)
-        down(0, 3)
-        turn_weights(wu, wug, (0,))
-        down_planes(1)
-        lat_planes(1)
-        table(0, 1)
-        lat(0, 2)
-        turn(5)
-        lat(0, 3)
-        turn(6)
-        widen(7, nc.scalar.copy)
-        widen(8, nc.scalar.copy)
-        table(1, 0)
-        table(1, 1)
-        quant_weights(wug, wuc, wus)
-        quant(0, 0, 2 * GRP)
-        weave(1)
+        def sum_biases():
+            nc.vector.tensor_tensor(out=bsum[:], in0=bu[:, 0, 0:1], in1=bu[:, 1, 0:1], op=ADD)
 
-        merge_rings()
+        last = NG - 1
+
+        widen(0, 0, 1)
+        widen(0, 1, 2)
+        widen(1)
+        widen(2)
+        turn_mm(0, 0, 1)
+        turn_mm(0, 1, 2)
+        turn_mm(1)
+        turn_weights(wd, 0, "wa")
+        turn_mm(2)
+        turn_weights(wd, 1, "wb")
+        widen(3)
+        scale(0, 0, 1)
+        scale(0, 1, 2)
+        copy_weights(wdg, 0, "wa")
+        widen(4)
+        turn_mm(3)
+        scale(1)
+        copy_weights(wdg, 1, "wb")
+        turn_table(0, 2)
+        turn(4)
+        turn_table(0, 0)
+        scale(2)
+        turn_weights(wu, 0, "wu")
+        quant_x(-2, HG, GRP)
+        quant_weights(wdg, wdc, wds)
+        quant_x(-1)
+        widen(5)
+        copy_table(0, 2)
+        widen(6)
+        copy_table(0, 0)
+        down(0, 0)
+        down_planes(2)
+        copy_weights(wug, 0, "wu")
+        down(0, 1)
+        down(0, 2)
+        scale(3)
+        down(0, 3)
+        lat_planes(2)
+        weave(2)
+        lat(0, 0)
+        turn(5)
+        turn_table(0, 1)
+        lat(0, 1)
+        turn(6)
+        lat(0, 2)
+        turn_table(1, 2)
+        widen(7)
+        turn_table(1, 0)
+        lat(0, 3)
+        copy_table(0, 1)
+        turn_table(1, 1)
+        scale(4)
+        widen(8)
+        copy_table(1, 2)
+        copy_table(1, 0)
+        quant_weights(wug, wuc, wus)
+        sum_biases()
+        quant_x(0)
+        quant_lat(0)
+
         for s in range(1, last - 1):
             if s >= 2:
-                products_gpsimd(s - 2, NV)
-            down_planes(s + 1)
+                mixed(s - 2, s - 1)
+            down_planes(2 * s + 2)
             down(s, 2)
             down(s, 3)
-            up(s - 1, 1, "o")
             if s >= 2:
-                half(s - 2, 0, 0, GRP - KP)
-                give_back(("up", s - 2, 0))
-            up(s - 1, 0, "v")
+                copy_out(s - 2, 1)
+            else:
+                copy_table(1, 1)
+            if s == 2:
+                copy_table(3, 2)
+            if s == last - 2:
+                copy_table(3, 1)
+            up_sum(s - 1)
+            up(s - 1, 1)
             scale(2 * s + 3)
-            lat_planes(s + 1)
-            weave(s + 1)
+            up(s - 1, 0)
+            if s < last - 2:
+                widen(2 * s + 7)
+            lat_planes(2 * s + 2)
+            weave(2 * s + 2)
+            scale(2 * s + 4)
+            if s == last - 2:
+                turn(2 * s + 5)
             if s >= 3:
                 turn_rotated(s - 3, 1)
+            else:
+                turn_table(s + 1, 0)
             if s >= 2:
                 turn_plain(s - 2, 0)
-            turn(2 * s + 5)
-            scale(2 * s + 4)
-            if s < last - 2:
-                widen(2 * s + 7, nc.scalar.copy)
-            lat(s, 2)
+            else:
+                turn_table(2, 2)
+            if s < last - 3:
+                widen(2 * s + 8)
+            kp = KP if s < last - 2 else 0
             half(s - 1, 1)
             give_back(("up", s - 1, 1))
-            lat(s, 3)
-            if s >= 3:
-                copy_out(s - 3, 3)
-            if s >= 2:
-                copy_out(s - 2, 0)
-            if s < last - 3:
-                widen(2 * s + 8, nc.scalar.copy)
-            if s == 1:
-                table(2, 0)
-                table(2, 1)
-                table(3, 0)
-            if s == last - 2:
-                table(3, 1)
+            half(s - 1, 0, 0, GRP - kp)
+            if not kp:
+                give_back(("up", s - 1, 0))
+            lat(s, 2)
             if s >= 2:
                 turn_rotated(s - 2, 0)
+            else:
+                turn_table(2, 1)
+            lat(s, 3)
             turn_plain(s - 1, 1)
+            common(s - 1)
+            if s >= 3:
+                copy_out(s - 3, 3)
+            else:
+                copy_table(s + 1, 0)
+            if s < last - 2:
+                turn(2 * s + 5)
+                piece(s - 1, 0, GRP - kp, GRP)
+                give_back(("up", s - 1, 0))
+            else:
+                turn_rotated(s - 2, 1)
+                scale(2 * s + 5)
+            if s >= 2:
+                copy_out(s - 2, 0)
+            else:
+                copy_table(2, 2)
             if s < last - 2:
                 turn(2 * s + 6)
             else:
-                turn_rotated(s - 2, 1)
-            products_vector(s - 1, 0, NV)
+                turn_plain(s - 1, 0)
             if s >= 2:
                 copy_out(s - 2, 2)
-            copy_out(s - 1, 1)
-            quant(s, 0, GRP)
-            piece(s - 1, GRP - KP, GRP)
-            quant(s, GRP, 2 * GRP)
+            else:
+                copy_table(2, 1)
+            if s == 1:
+                turn_table(3, 2)
+            if s == last - 3:
+                turn_table(3, 1)
+            quant_x(s)
+            if s == last - 2:
+                quant_x(s + 1, 0, HG)
+            quant_lat(s)
 
         s = last - 1
-        products_gpsimd(s - 2, NV)
+        mixed(s - 2, s - 1)
         down(s, 2)
         down(s, 3)
-        up(s - 1, 1, "o")
-        half(s - 2, 0, 0, GRP - KP)
-        give_back(("up", s - 2, 0))
+        down_planes(2 * last)
+        copy_out(s - 2, 1)
+        up_sum(s - 1)
         copy_out(s - 3, 3)
-        up(s - 1, 0, "v")
-        down(last, 0)
-        scale(2 * NG - 1)
-        down(last, 1)
+        up(s - 1, 1)
+        copy_out(s - 2, 0)
+        up(s - 1, 0)
+        lat(s, 2)
+        down(last, 2)
+        lat(s, 3)
+        down(last, 3)
+        lat_planes(2 * last)
+        common(s - 1)
+        quant_lat(s)
+        weave(2 * last)
+        turn_rotated(s - 2, 0)
+        turn_rotated(s - 2, 1)
         half(s - 1, 1)
         give_back(("up", s - 1, 1))
-        turn_plain(s - 2, 0)
-        lat(s, 2)
-        lat(s, 3)
-        turn_plain(s - 1, 1)
-        turn_rotated(s - 2, 0)
-        copy_out(s - 2, 0)
-        turn_rotated(s - 2, 1)
-        copy_out(s - 1, 1)
-        products_vector(s - 1, 0, NV)
-        quant(last, 0, HG)
-        piece(s - 1, GRP - KP, GRP)
-        quant(s, GRP, 2 * GRP)
-        products_gpsimd(s - 1, NV)
-        copy_out(s - 2, 2)
-        half(s - 1, 0, 0, GRP - KP)
+        half(s - 1, 0)
         give_back(("up", s - 1, 0))
-        down(last, 2)
-        up(s, 1, "o")
-        down(last, 3)
-        lat(last, 0)
-        up(s, 0, "v")
-        copy_out(s - 2, 3)
-        lat(last, 1)
-        half(s, 1)
-        head_plain(s - 1, 0)
-        head_plain(s, 1)
         lat(last, 2)
         lat(last, 3)
-        products_vector(s, 0, NT)
-        quant(s, 0, HG)
-        piece(s, GRP - KP, GRP)
-        quant(s, HG, GRP)
-        products_gpsimd(s, NV, NH)
-        products_vector(s, NT, NV)
-        products_vector(s, NH, 2 * GRP)
-        give_back(("up", s, 1))
-        turn_rotated(s - 1, 0)
+        up_sum(s)
+        up(s, 1)
+        up(s, 0)
+        copy_out(s - 2, 2)
+        turn_plain(s - 1, 1)
+        turn_plain(s - 1, 0)
+        copy_out(s - 2, 3)
+        quant_lat(last)
+        mixed(s - 1, "l")
+        common(s)
+        half(s, 1)
         up_tokens(last, 0)
         up_tokens(last, 1)
-        copy_out(s - 1, 2)
-        half(s, 0, 0, GRP - KP)
+        copy_out(s - 1, 1)
+        mixed_vector(s, last, 1)
+        give_back(("up", s, 1))
+        mixed_vector(s, last, 0)
+        copy_out(s - 1, 0)
+        half(s, 0)
         give_back(("up", s, 0))
+        turn_plain(s, 1)
+        turn_rotated(s, 0)
         plain(last, 0)
         plain(last, 1)
-        head_rotated(s - 1, 1)
-        head_plain(s, 0)
+        turn_rotated(s, 1)
+        turn_plain(s, 0)
+        turn_rotated(s - 1, 0)
+        turn_rotated(s - 1, 1)
+        copy_out(s, 1)
+        copy_out(s, 2)
         product_rows(last, 0, 0)
         product_rows(last, 1, 1)
         product_rows(last, 0, 1)
+        copy_out(s, 3)
+        copy_out(s, 0)
         rotated_rows(last, 0)
-        head_rotated(s, 0)
         product_rows(last, 1, 0)
-        head_rotated(s, 1)
+        copy_out(s - 1, 2)
+        copy_out(s - 1, 3)
         rotated_rows(last, 1)

@@ -25,7 +25,6 @@ HG = GRP // 2
 PG = S // GRP
 NG = B * PG
 SLOTS = 4
-KP = 256
 OUT_BUFS = 5
 
 
@@ -111,27 +110,44 @@ def tile_multiheadlatentattention_pa_t_kernel(
         wdg = keep.tile([P, LAT, T4], BF16, name="wdg", align_bytes=64)
         wug = keep.tile([P, HALF, T4], BF16, name="wug", align_bytes=64)
         bsum = keep.tile([P, 1], F32, name="bsum")
+        ones = keep.tile([P, 1], F32, name="ones")
+        nc.vector.memset(ones[:], 1.0)
+        in_order = []
         tcos = keep.tile([P, PG, GRP], BF16, name="tcos", align_bytes=64)
         tmix = keep.tile([P, PG, 2, GRP], F32, name="tmix", align_bytes=64)
 
         xbf, xt, xs, xc, xz, ls, lc, lz, m1, m2, m3, planes, qt, pg2, pv, osb, written, rows = ({} for i in range(18))
 
-        def widen(m, lo=0, hi=2):
-            if lo == 0:
+        def wide(m):
+            if m not in xbf:
                 xbf[m] = sb.tile([P, 2, H], BF16, name="xbf", bufs=6, align_bytes=64)
-            j = 2 * (m % 2)
-            nc.scalar.copy(out=xbf[m][:, lo:hi, :], in_=xb[m // 2][:, j + lo : j + hi, :].bitcast(FP8))
+            return xbf[m]
 
-        def turn_words(key, words):
+        def widen(m, lo=0, hi=2):
+            j = 2 * (m % 2)
+            nc.scalar.copy(out=wide(m)[:, lo:hi, :], in_=xb[m // 2][:, j + lo : j + hi, :].bitcast(FP8))
+
+        def widen_sorted(m):
+            nc.vector.tensor_scalar(
+                out=wide(m)[:, 1, :].rearrange("p (u q e) -> p q u e", u=2, e=2),
+                in0=xb[m // 2][:, 2 * (m % 2) + 1, :].bitcast(FP8).rearrange("p (q u e) -> p q u e", u=2, e=2),
+                scalar1=ones[:],
+                scalar2=None,
+                op0=MULT,
+            )
+            in_order.append(m)
+
+        def turn_words(key, words, last_sorted=False):
             tiles = words.shape[1]
             t = bank(key, [P, 2, tiles * P], F32)
             for jj in range(tiles):
                 for u in range(2):
-                    nc.tensor.transpose(t[:, u, jj * P : (jj + 1) * P], words[:, jj, u : H // 2 : 2], idf[:])
+                    pick = slice(u * P, (u + 1) * P) if last_sorted and jj == tiles - 1 else slice(u, H // 2, 2)
+                    nc.tensor.transpose(t[:, u, jj * P : (jj + 1) * P], words[:, jj, pick], idf[:])
             return t
 
         def turn(m, lo=0, hi=2):
-            t = turn_words(("x", m, lo), xbf[m][:, lo:hi, :].bitcast(F32))
+            t = turn_words(("x", m, lo), xbf[m][:, lo:hi, :].bitcast(F32), m in in_order)
             xt[m, lo] = t[:].bitcast(BF16).rearrange("p u (r e) -> p r u e", e=2)
 
         def turn_mm(m, lo=0, hi=2):
@@ -199,7 +215,7 @@ def tile_multiheadlatentattention_pa_t_kernel(
 
         def lat_stage(n):
             if n not in ls:
-                ls[n] = sb.tile([P, GRP, T4], BF16, name="lstage%d" % (min(n, NG - 2) % 3), bufs=1, align_bytes=64)
+                ls[n] = sb.tile([P, GRP, T4], BF16, name="lstage%d" % (n % 3), bufs=1, align_bytes=64)
             return ls[n]
 
         def lat(n, j):
@@ -281,7 +297,7 @@ def tile_multiheadlatentattention_pa_t_kernel(
 
         def mixed_tile(n, s):
             if n not in pg2:
-                name = "lstage%d" % ((NG - 2) % 3) if s == "l" else "slot%d" % (s % SLOTS)
+                name = "lstage%d" % (int(s[1:]) % 3) if isinstance(s, str) else "slot%d" % (s % SLOTS)
                 pg2[n] = sb.tile([P, 2, GRP], F32, name=name, bufs=1, align_bytes=64)
             return pg2[n]
 
@@ -386,6 +402,21 @@ def tile_multiheadlatentattention_pa_t_kernel(
             copy(out=dst, in_=m3["tab", pg, k][:].rearrange("p j r -> p (j r)"))
             give_back(("tab", pg, k))
 
+        def turn_sines(pg):
+            o = bank("sines", [P, 2, J, P], BF16)
+            for a, ident in enumerate((idb, idn)):
+                for j in range(J):
+                    nc.tensor.matmul(o[:, a, j, :], lhsT=rope[1, pg][:, j, :], rhs=ident[:], start=True, stop=True)
+            m3["sines"] = o
+
+        def mix_sines(pg):
+            sines = keep.tile([P, 2, GRP], BF16, name="wdg", align_bytes=64)
+            nc.scalar.copy(out=sines[:], in_=m3["sines"][:].rearrange("p a j r -> p a (j r)"))
+            give_back("sines")
+            nc.gpsimd.tensor_tensor(
+                out=tmix[:, pg, :, :], in0=sines[:], in1=tcos[:, pg : pg + 1, :].to_broadcast([P, 2, GRP]), op=SUB
+            )
+
         def table(pg, k):
             turn_table(pg, k)
             copy_table(pg, k)
@@ -411,23 +442,23 @@ def tile_multiheadlatentattention_pa_t_kernel(
         widen(0, 1, 2)
         widen(1)
         widen(2)
-        turn_mm(0, 0, 1)
-        turn_mm(0, 1, 2)
-        turn_mm(1)
+        turn(0, 0, 1)
+        turn(0, 1, 2)
+        turn(1)
         turn_weights(wd, 0, "wa")
-        turn_mm(2)
+        turn(2)
         turn_weights(wd, 1, "wb")
         widen(3)
         scale(0, 0, 1)
         scale(0, 1, 2)
         copy_weights(wdg, 0, "wa")
         widen(4)
-        turn_mm(3)
+        turn(3)
         scale(1)
         copy_weights(wdg, 1, "wb")
         turn_table(0, 2)
         turn(4)
-        turn_table(0, 0)
+        turn_sines(0)
         scale(2)
         turn_weights(wu, 0, "wu")
         quant_x(-2, HG, GRP)
@@ -436,7 +467,7 @@ def tile_multiheadlatentattention_pa_t_kernel(
         widen(5)
         copy_table(0, 2)
         widen(6)
-        copy_table(0, 0)
+        mix_sines(0)
         down(0, 0)
         down_planes(2)
         copy_weights(wug, 0, "wu")
@@ -448,7 +479,7 @@ def tile_multiheadlatentattention_pa_t_kernel(
         weave(2)
         lat(0, 0)
         turn(5)
-        turn_table(0, 1)
+        turn_table(3, 1)
         lat(0, 1)
         turn(6)
         lat(0, 2)
@@ -456,7 +487,7 @@ def tile_multiheadlatentattention_pa_t_kernel(
         widen(7)
         turn_table(1, 0)
         lat(0, 3)
-        copy_table(0, 1)
+        copy_table(3, 1)
         turn_table(1, 1)
         scale(4)
         widen(8)
@@ -467,31 +498,27 @@ def tile_multiheadlatentattention_pa_t_kernel(
         quant_x(0)
         quant_lat(0)
 
-        for s in range(1, last - 1):
+        for s in range(1, last - 2):
             if s >= 2:
                 mixed(s - 2, s - 1)
             down_planes(2 * s + 2)
             down(s, 2)
             down(s, 3)
             if s >= 2:
-                copy_out(s - 2, 1)
-            else:
+                widen(2 * s + 6, 0, 1)
+            if s == 1:
                 copy_table(1, 1)
             if s == 2:
                 copy_table(3, 2)
-            if s == last - 2:
-                copy_table(3, 1)
             up_sum(s - 1)
-            up(s - 1, 1)
             scale(2 * s + 3)
-            up(s - 1, 0)
-            if s < last - 2:
-                widen(2 * s + 7)
+            up(s - 1, 1)
             lat_planes(2 * s + 2)
             weave(2 * s + 2)
+            up(s - 1, 0)
+            if s >= 2:
+                copy_out(s - 2, 1)
             scale(2 * s + 4)
-            if s == last - 2:
-                turn(2 * s + 5)
             if s >= 3:
                 turn_rotated(s - 3, 1)
             else:
@@ -500,14 +527,9 @@ def tile_multiheadlatentattention_pa_t_kernel(
                 turn_plain(s - 2, 0)
             else:
                 turn_table(2, 2)
-            if s < last - 3:
-                widen(2 * s + 8)
-            kp = KP if s < last - 2 else 0
             half(s - 1, 1)
             give_back(("up", s - 1, 1))
-            half(s - 1, 0, 0, GRP - kp)
-            if not kp:
-                give_back(("up", s - 1, 0))
+            widen(2 * s + 7)
             lat(s, 2)
             if s >= 2:
                 turn_rotated(s - 2, 0)
@@ -520,98 +542,122 @@ def tile_multiheadlatentattention_pa_t_kernel(
                 copy_out(s - 3, 3)
             else:
                 copy_table(s + 1, 0)
-            if s < last - 2:
-                turn(2 * s + 5)
-                piece(s - 1, 0, GRP - kp, GRP)
-                give_back(("up", s - 1, 0))
-            else:
-                turn_rotated(s - 2, 1)
-                scale(2 * s + 5)
+            half(s - 1, 0)
+            give_back(("up", s - 1, 0))
+            turn(2 * s + 5)
             if s >= 2:
                 copy_out(s - 2, 0)
             else:
                 copy_table(2, 2)
-            if s < last - 2:
-                turn(2 * s + 6)
-            else:
-                turn_plain(s - 1, 0)
+            turn(2 * s + 6)
             if s >= 2:
                 copy_out(s - 2, 2)
             else:
                 copy_table(2, 1)
             if s == 1:
                 turn_table(3, 2)
-            if s == last - 3:
-                turn_table(3, 1)
+            if s < last - 3:
+                widen_sorted(2 * s + 8)
             quant_x(s)
-            if s == last - 2:
-                quant_x(s + 1, 0, HG)
             quant_lat(s)
 
-        s = last - 1
-        mixed(s - 2, s - 1)
-        down(s, 2)
-        down(s, 3)
-        down_planes(2 * last)
-        copy_out(s - 2, 1)
-        up_sum(s - 1)
-        copy_out(s - 3, 3)
-        up(s - 1, 1)
-        copy_out(s - 2, 0)
-        up(s - 1, 0)
-        lat(s, 2)
-        down(last, 2)
-        lat(s, 3)
-        down(last, 3)
-        lat_planes(2 * last)
-        common(s - 1)
-        quant_lat(s)
-        weave(2 * last)
-        turn_rotated(s - 2, 0)
-        turn_rotated(s - 2, 1)
-        half(s - 1, 1)
-        give_back(("up", s - 1, 1))
-        half(s - 1, 0)
-        give_back(("up", s - 1, 0))
-        lat(last, 2)
-        lat(last, 3)
-        up_sum(s)
-        up(s, 1)
-        up(s, 0)
-        copy_out(s - 2, 2)
-        turn_plain(s - 1, 1)
-        turn_plain(s - 1, 0)
-        copy_out(s - 2, 3)
-        quant_lat(last)
-        mixed(s - 1, "l")
-        common(s)
-        half(s, 1)
-        up_tokens(last, 0)
-        up_tokens(last, 1)
-        copy_out(s - 1, 1)
-        mixed_vector(s, last, 1)
-        give_back(("up", s, 1))
-        mixed_vector(s, last, 0)
-        copy_out(s - 1, 0)
-        half(s, 0)
-        give_back(("up", s, 0))
-        turn_plain(s, 1)
-        turn_rotated(s, 0)
-        plain(last, 0)
-        plain(last, 1)
-        turn_rotated(s, 1)
-        turn_plain(s, 0)
-        turn_rotated(s - 1, 0)
-        turn_rotated(s - 1, 1)
-        copy_out(s, 1)
-        copy_out(s, 2)
-        product_rows(last, 0, 0)
-        product_rows(last, 1, 1)
-        product_rows(last, 0, 1)
-        copy_out(s, 3)
-        copy_out(s, 0)
-        rotated_rows(last, 0)
-        product_rows(last, 1, 0)
-        copy_out(s - 1, 2)
-        copy_out(s - 1, 3)
-        rotated_rows(last, 1)
+        a, b, c, d, e, f = range(NG - 6, NG)
+        mixed(b, c)
+        down_planes(2 * e)
+        down(d, 2)
+        down(d, 3)
+        up_sum(c)
+        scale(2 * NG - 3)
+        up(c, 1)
+        lat_planes(2 * e)
+        weave(2 * e)
+        up(c, 0)
+        copy_out(b, 1)
+        scale(2 * NG - 2)
+        turn(2 * NG - 1)
+        turn_rotated(a, 1)
+        half(c, 1)
+        give_back(("up", c, 1))
+        half(c, 0)
+        give_back(("up", c, 0))
+        lat(d, 2)
+        turn_plain(b, 0)
+        lat(d, 3)
+        turn_rotated(b, 0)
+        common(c)
+        turn_plain(c, 1)
+        quant_lat(d)
+        quant_x(d)
+        mixed(c, "l%d" % d)
+        copy_out(a, 3)
+        up_sum(d)
+        copy_out(b, 0)
+        up(d, 1)
+        up(d, 0)
+        scale(2 * NG - 1)
+        down(e, 2)
+        copy_out(b, 2)
+        down(e, 3)
+        common(d)
+        copy_out(c, 1)
+        down(f, 0)
+        down(f, 1)
+        half(d, 1)
+        give_back(("up", d, 1))
+        turn_rotated(b, 1)
+        half(d, 0)
+        give_back(("up", d, 0))
+        lat(e, 2)
+        turn_plain(c, 0)
+        lat(e, 3)
+        turn_rotated(c, 0)
+        quant_x(e, 0, HG)
+        quant_lat(e)
+        mixed(d, e)
+        copy_out(b, 3)
+        down(f, 2)
+        down(f, 3)
+        copy_out(c, 0)
+        lat(f, 0)
+        up_sum(e)
+        copy_out(c, 2)
+        up(e, 1)
+        up(e, 0)
+        lat(f, 1)
+        turn_rotated(c, 1)
+        lat(f, 2)
+        turn_plain(d, 1)
+        lat(f, 3)
+        turn_plain(d, 0)
+        half(e, 1)
+        give_back(("up", e, 1))
+        half(e, 0)
+        give_back(("up", e, 0))
+        common(e)
+        turn_rotated(d, 0)
+        quant_lat(f)
+        mixed(e, "l%d" % f)
+        copy_out(c, 3)
+        up_tokens(f, 0)
+        up_tokens(f, 1)
+        copy_out(d, 1, nc.vector.tensor_copy)
+        copy_out(d, 0)
+        turn_rotated(d, 1)
+        turn_plain(e, 1)
+        turn_plain(e, 0)
+        copy_out(d, 2)
+        plain(f, 0)
+        plain(f, 1)
+        turn_rotated(e, 0)
+        turn_rotated(e, 1)
+        copy_out(d, 3)
+        copy_out(e, 1)
+        product_rows(f, 0, 0)
+        product_rows(f, 1, 1)
+        copy_out(e, 0)
+        product_rows(f, 0, 1)
+        rotated_rows(f, 0)
+        copy_out(e, 2)
+        product_rows(f, 1, 0)
+        copy_out(e, 3)
+        rotated_rows(f, 1)

@@ -25,6 +25,9 @@ HG = GRP // 2
 PG = S // GRP
 NG = B * PG
 SLOTS = 4
+KP = 256
+GAUSS = (1, 0, 1, 0)
+QUARTER = [n % PG for n in range(NG)]
 OUT_BUFS = 5
 
 
@@ -49,10 +52,16 @@ def tile_multiheadlatentattention_pa_t_kernel(
         def give_back(key):
             free.append(held.pop(key)[1])
 
+        def place(n):
+            return QUARTER[n], n // PG
+
+        def three(n):
+            return GAUSS[QUARTER[n]]
+
         xb = {}
 
         def load_x(n, cuts):
-            pg, b = divmod(n, B)
+            pg, b = place(n)
             rows = x_bytes[b, pg * GRP : (pg + 1) * GRP, :].rearrange("(p j) k -> p j k", j=J)
             if n not in xb:
                 xb[n] = sb.tile([P, J, H], U8, name="xbytes", bufs=NG, align_bytes=64)
@@ -77,21 +86,20 @@ def tile_multiheadlatentattention_pa_t_kernel(
         wu = keep.tile([P, 2, LAT], BF16, name="wu", align_bytes=64)
         bu = keep.tile([P, 2, 2], BF16, name="bu")
         bias_row = keep.tile([P, HALF], BF16, name="bias_row")
-        load_x(0, (0, 1))
+        load_x(0, (0, 1, 2, J))
         nc.sync.dma_start(out=sc[:], in_=x_scale.rearrange("a b (p t) -> p (a b t)", t=T4))
-        load_x(0, (1, 2, J))
-        nc.sync.dma_start(out=wd[:, 0:2, :], in_=wd_rows[:, 0:2, :])
         load_x(1, (0, 2))
+        nc.sync.dma_start(out=wd[:, 0:2, :], in_=wd_rows[:, 0:2, :])
         nc.sync.dma_start(out=wd[:, 2:4, :], in_=wd_rows[:, 2:4, :])
         load_x(1, (2, J))
-        load_x(2, (0, J))
         nc.sync.dma_start(out=bd[:], in_=bq_down.rearrange("(p t) -> p t", t=T4))
-        load_rope(0, 1)
+        load_x(2, (0, J))
+        load_rope(0, 2)
         nc.sync.dma_start(out=wu[:], in_=wq_up.rearrange("(h m) k -> m h k", h=2))
         load_x(3, (0, J))
+        load_rope(2, 4)
         with nc.allow_non_contiguous_dma(reason="one bias value for each partition and half"):
             nc.sync.dma_start(out=bu[:, :, 0:1], in_=bq_up.rearrange("(h c o) -> c h o", h=2, o=1))
-        load_rope(1, 4)
         for n in range(4, NG):
             load_x(n, (0, J))
         nc.sync.dma_start(out=bias_row[:], in_=bq_up.partition_broadcast(P))
@@ -108,12 +116,10 @@ def tile_multiheadlatentattention_pa_t_kernel(
         wuc = keep.tile([P, HALF], U32, name="wuc", align_bytes=64)
         wus = keep.tile([P, HALF], U8, name="wus", align_bytes=64)
         wdg = keep.tile([P, LAT, T4], BF16, name="wdg", align_bytes=64)
-        wug = keep.tile([P, HALF, T4], BF16, name="wug", align_bytes=64)
+        wug = sb.tile([P, HALF, T4], BF16, name="lstage1", bufs=1, align_bytes=64)
         bsum = keep.tile([P, 1], F32, name="bsum")
-        ones = keep.tile([P, 1], F32, name="ones")
-        nc.vector.memset(ones[:], 1.0)
         in_order = []
-        tcos = keep.tile([P, PG, GRP], BF16, name="tcos", align_bytes=64)
+        tab = keep.tile([P, PG, 3, GRP], BF16, name="tab", align_bytes=64)
         tmix = keep.tile([P, PG, 2, GRP], F32, name="tmix", align_bytes=64)
 
         xbf, xt, xs, xc, xz, ls, lc, lz, m1, m2, m3, planes, qt, pg2, pv, osb, written, rows = ({} for i in range(18))
@@ -127,16 +133,6 @@ def tile_multiheadlatentattention_pa_t_kernel(
             j = 2 * (m % 2)
             nc.scalar.copy(out=wide(m)[:, lo:hi, :], in_=xb[m // 2][:, j + lo : j + hi, :].bitcast(FP8))
 
-        def widen_sorted(m):
-            nc.vector.tensor_scalar(
-                out=wide(m)[:, 1, :].rearrange("p (u q e) -> p q u e", u=2, e=2),
-                in0=xb[m // 2][:, 2 * (m % 2) + 1, :].bitcast(FP8).rearrange("p (q u e) -> p q u e", u=2, e=2),
-                scalar1=ones[:],
-                scalar2=None,
-                op0=MULT,
-            )
-            in_order.append(m)
-
         def turn_words(key, words, last_sorted=False):
             tiles = words.shape[1]
             t = bank(key, [P, 2, tiles * P], F32)
@@ -149,19 +145,6 @@ def tile_multiheadlatentattention_pa_t_kernel(
         def turn(m, lo=0, hi=2):
             t = turn_words(("x", m, lo), xbf[m][:, lo:hi, :].bitcast(F32), m in in_order)
             xt[m, lo] = t[:].bitcast(BF16).rearrange("p u (r e) -> p r u e", e=2)
-
-        def turn_mm(m, lo=0, hi=2):
-            t = bank(("x", m, lo), [P, T4, (hi - lo) * P], BF16)
-            for jj in range(lo, hi):
-                for k in range(T4):
-                    nc.tensor.matmul(
-                        t[:, k, (jj - lo) * P : (jj - lo + 1) * P],
-                        lhsT=xbf[m][:, jj, k:H:T4],
-                        rhs=idb[:],
-                        start=True,
-                        stop=True,
-                    )
-            xt[m, lo] = t[:].rearrange("p (u e) r -> p r u e", e=2)
 
         def x_place(m):
             return divmod(m - 3, 2) if m < 2 * NG - 1 else (NG - 2, 0)
@@ -264,16 +247,12 @@ def tile_multiheadlatentattention_pa_t_kernel(
             m2[n, h] = o
 
         def up_sum(n):
+            if not three(n):
+                return
             o = bank(("sum", n), [P, GRP], F32)
             for h in range(2):
                 mx(o[:], wuc, wus, slice(h * P, (h + 1) * P), lc[n], lz[n], slice(0, GRP), h == 0, h == 1)
             m2[n, "sum"] = o
-
-        def up_more(n):
-            o = m2[n, 0]
-            mx(o[:], wuc, wus, slice(P, 2 * P), lc[n], lz[n], slice(0, GRP), False, True)
-            m2[n, "sum"] = o
-            held["sum", n] = held.pop(("up", n, 0))
 
         def biased(n):
             if n not in qt:
@@ -289,11 +268,23 @@ def tile_multiheadlatentattention_pa_t_kernel(
             )
 
         def common(n):
-            pv[n] = sb.tile([P, GRP], F32, name="pv", bufs=4, align_bytes=64)
+            pg = QUARTER[n]
+            if three(n):
+                pv[n] = sb.tile([P, 1, GRP], F32, name="pv", bufs=3, align_bytes=64)
+                src, bias, factor = m2[n, "sum"], bsum[:], tab[:, pg, 1:2, :]
+            else:
+                pv[n] = sb.tile([P, 2, GRP], F32, name="pv", bufs=3, align_bytes=64)
+                src, bias, factor = m2[n, 0], bu[:, 0, 0:1], tab[:, pg, 1:3, :]
             nc.vector.scalar_tensor_tensor(
-                out=pv[n][:], in0=m2[n, "sum"][:], scalar=bsum[:], in1=tcos[:, n // B, :], op0=ADD, op1=MULT
+                out=pv[n][:],
+                in0=src[:].unsqueeze(1).to_broadcast([P, 1 if three(n) else 2, GRP]),
+                scalar=bias,
+                in1=factor,
+                op0=ADD,
+                op1=MULT,
             )
-            give_back(("sum", n))
+            if three(n):
+                give_back(("sum", n))
 
         def mixed_tile(n, s):
             if n not in pg2:
@@ -301,20 +292,13 @@ def tile_multiheadlatentattention_pa_t_kernel(
                 pg2[n] = sb.tile([P, 2, GRP], F32, name=name, bufs=1, align_bytes=64)
             return pg2[n]
 
-        def mixed(n, s, lo=0, hi=GRP):
-            nc.gpsimd.tensor_tensor(
-                out=mixed_tile(n, s)[:, :, lo:hi], in0=qt[n][:, :, lo:hi], in1=tmix[:, n // B, :, lo:hi], op=MULT
-            )
-
-        def mixed_vector(n, s, h, lo=0, hi=GRP):
-            nc.vector.scalar_tensor_tensor(
-                out=mixed_tile(n, s)[:, h, lo:hi],
-                in0=m2[n, h][:, lo:hi],
-                scalar=bu[:, h, 0:1],
-                in1=tmix[:, n // B, h, lo:hi],
-                op0=ADD,
-                op1=MULT,
-            )
+        def mixed(n, s):
+            pg = QUARTER[n]
+            if three(n):
+                src, factor = qt[n][:], tmix[:, pg, :, :]
+            else:
+                src, factor = qt[n][:, 1:2, :].to_broadcast([P, 2, GRP]), tab[:, pg, 0:2, :]
+            nc.gpsimd.tensor_tensor(out=mixed_tile(n, s)[:], in0=src, in1=factor, op=MULT)
 
         def result(n, h):
             if n not in osb:
@@ -328,7 +312,7 @@ def tile_multiheadlatentattention_pa_t_kernel(
                 if len(written[n]) < 4:
                     return
                 heads = slice(0, 4)
-            pg, b = divmod(n, B)
+            pg, b = place(n)
             dst = out[b, heads, pg * GRP : (pg + 1) * GRP, :].rearrange("h (p j) d -> p h (j d)", j=J)
             nc.sync.dma_start(out=dst, in_=osb[n][:, heads, :, :].rearrange("p h j d -> p h (j d)"))
 
@@ -342,7 +326,7 @@ def tile_multiheadlatentattention_pa_t_kernel(
             o = bank(("out", n, 2 + i), [P, J, P], F32)
             for j in range(J):
                 cols = slice(j * P, (j + 1) * P)
-                for k, term in enumerate((pv[n][:, cols], pg2[n][:, 1 - i, cols])):
+                for k, term in enumerate((pv[n][:, 0, cols], pg2[n][:, 1 - i, cols]) if three(n) else (pv[n][:, i, cols], pg2[n][:, i, cols])):
                     nc.tensor.matmul(o[:, j, :], lhsT=term, rhs=idf[:], start=k == 0, stop=k == 1, is_transpose=True)
             m3[n, 2 + i] = o
 
@@ -374,7 +358,7 @@ def tile_multiheadlatentattention_pa_t_kernel(
             nc.vector.tensor_tensor(
                 out=rows[n][:, h, i, :],
                 in0=result(n, h).rearrange("p j d -> p (j d)"),
-                in1=rope[i, n // B].rearrange("p j d -> p (j d)"),
+                in1=rope[i, QUARTER[n]].rearrange("p j d -> p (j d)"),
                 op=MULT,
             )
 
@@ -388,38 +372,28 @@ def tile_multiheadlatentattention_pa_t_kernel(
             store(n, 2 + i)
 
         def turn_table(pg, k):
-            terms = (((1, idb), (0, idn)), ((1, idn), (0, idn)), ((0, idb),))[k]
-            o = bank(("tab", pg, k), [P, J, P], BF16 if k == 2 else F32)
-            for j in range(J):
-                for a, (i, ident) in enumerate(terms):
-                    nc.tensor.matmul(
-                        o[:, j, :], lhsT=rope[i, pg][:, j, :], rhs=ident[:], start=a == 0, stop=a == len(terms) - 1
-                    )
-            m3["tab", pg, k] = o
+            if GAUSS[pg]:
+                terms = ([[(1, idb), (0, idn)]], [[(1, idn), (0, idn)]], [[(0, idb)]])[k]
+            else:
+                terms = ([[(1, idn)], [(0, idb)]], [], [[(1, idb)]])[k]
+            if terms:
+                o = bank(("tab", pg, k), [P, len(terms), J, P], F32 if len(terms[0]) == 2 else BF16)
+                for q, plane in enumerate(terms):
+                    for j in range(J):
+                        for a, (i, ident) in enumerate(plane):
+                            nc.tensor.matmul(
+                                o[:, q, j, :], lhsT=rope[i, pg][:, j, :], rhs=ident[:], start=a == 0, stop=a == len(plane) - 1
+                            )
+                m3["tab", pg, k] = o
 
-        def copy_table(pg, k, copy=nc.scalar.copy):
-            dst = tcos[:, pg, :] if k == 2 else tmix[:, pg, k, :]
-            copy(out=dst, in_=m3["tab", pg, k][:].rearrange("p j r -> p (j r)"))
-            give_back(("tab", pg, k))
-
-        def turn_sines(pg):
-            o = bank("sines", [P, 2, J, P], BF16)
-            for a, ident in enumerate((idb, idn)):
-                for j in range(J):
-                    nc.tensor.matmul(o[:, a, j, :], lhsT=rope[1, pg][:, j, :], rhs=ident[:], start=True, stop=True)
-            m3["sines"] = o
-
-        def mix_sines(pg):
-            sines = keep.tile([P, 2, GRP], BF16, name="wdg", align_bytes=64)
-            nc.scalar.copy(out=sines[:], in_=m3["sines"][:].rearrange("p a j r -> p a (j r)"))
-            give_back("sines")
-            nc.gpsimd.tensor_tensor(
-                out=tmix[:, pg, :, :], in0=sines[:], in1=tcos[:, pg : pg + 1, :].to_broadcast([P, 2, GRP]), op=SUB
-            )
-
-        def table(pg, k):
-            turn_table(pg, k)
-            copy_table(pg, k)
+        def copy_table(pg, k):
+            if ("tab", pg, k) in m3:
+                if GAUSS[pg]:
+                    dst = tab[:, pg, 1:2, :] if k == 2 else tmix[:, pg, k : k + 1, :]
+                else:
+                    dst = tab[:, pg, 2:3, :] if k == 2 else tab[:, pg, 0:2, :]
+                nc.scalar.copy(out=dst, in_=m3["tab", pg, k][:].rearrange("p a j r -> p a (j r)"))
+                give_back(("tab", pg, k))
 
         def turn_weights(w, h, key):
             m3[key] = turn_words(key, w[:, 2 * h : 2 * h + 2, :].bitcast(F32))
@@ -441,62 +415,60 @@ def tile_multiheadlatentattention_pa_t_kernel(
         widen(0, 0, 1)
         widen(0, 1, 2)
         widen(1)
-        widen(2)
         turn(0, 0, 1)
-        turn(0, 1, 2)
-        turn(1)
-        turn_weights(wd, 0, "wa")
-        turn(2)
-        turn_weights(wd, 1, "wb")
-        widen(3)
         scale(0, 0, 1)
+        turn(0, 1, 2)
         scale(0, 1, 2)
-        copy_weights(wdg, 0, "wa")
-        widen(4)
-        turn(3)
+        turn(1)
         scale(1)
-        copy_weights(wdg, 1, "wb")
-        turn_table(0, 2)
-        turn(4)
-        turn_sines(0)
+        widen(2)
+        turn(2)
         scale(2)
-        turn_weights(wu, 0, "wu")
+        widen(3)
+        turn_weights(wd, 0, "wa")
+        turn_weights(wd, 1, "wb")
+        copy_weights(wdg, 0, "wa")
+        copy_weights(wdg, 1, "wb")
+        turn(3)
+        widen(4)
         quant_x(-2, HG, GRP)
         quant_weights(wdg, wdc, wds)
         quant_x(-1)
         widen(5)
-        copy_table(0, 2)
+        turn_table(0, 0)
+        copy_table(0, 0)
+        turn(4)
         widen(6)
-        mix_sines(0)
-        down(0, 0)
-        down_planes(2)
-        copy_weights(wug, 0, "wu")
-        down(0, 1)
-        down(0, 2)
         scale(3)
-        down(0, 3)
-        lat_planes(2)
-        weave(2)
-        lat(0, 0)
-        turn(5)
-        turn_table(3, 1)
-        lat(0, 1)
-        turn(6)
-        lat(0, 2)
-        turn_table(1, 2)
-        widen(7)
-        turn_table(1, 0)
-        lat(0, 3)
-        copy_table(3, 1)
-        turn_table(1, 1)
+        down_planes(0)
+        lat_planes(0)
+        weave(0)
+        down(0, 2)
         scale(4)
+        down(0, 3)
+        turn_weights(wu, 0, "wu")
+        copy_weights(wug, 0, "wu")
+        down_planes(2)
+        lat_planes(2)
+        turn_table(0, 2)
+        lat(0, 2)
+        turn(5)
+        lat(0, 3)
+        turn(6)
+        copy_table(0, 2)
+        widen(7)
+        turn_table(0, 1)
+        turn_table(1, 0)
+        turn_table(1, 2)
         widen(8)
-        copy_table(1, 2)
+        copy_table(0, 1)
         copy_table(1, 0)
-        quant_weights(wug, wuc, wus)
-        sum_biases()
+        copy_table(1, 2)
         quant_x(0)
+        quant_weights(wug, wuc, wus)
         quant_lat(0)
+        sum_biases()
+        weave(2)
 
         for s in range(1, last - 2):
             if s >= 2:
@@ -505,19 +477,15 @@ def tile_multiheadlatentattention_pa_t_kernel(
             down(s, 2)
             down(s, 3)
             if s >= 2:
-                widen(2 * s + 6, 0, 1)
-            if s == 1:
-                copy_table(1, 1)
-            if s == 2:
-                copy_table(3, 2)
-            up_sum(s - 1)
-            scale(2 * s + 3)
+                copy_out(s - 2, 1)
             up(s - 1, 1)
+            scale(2 * s + 3)
+            up(s - 1, 0)
             lat_planes(2 * s + 2)
             weave(2 * s + 2)
-            up(s - 1, 0)
+            up_sum(s - 1)
             if s >= 2:
-                copy_out(s - 2, 1)
+                widen(2 * s + 6)
             scale(2 * s + 4)
             if s >= 3:
                 turn_rotated(s - 3, 1)
@@ -526,38 +494,49 @@ def tile_multiheadlatentattention_pa_t_kernel(
             if s >= 2:
                 turn_plain(s - 2, 0)
             else:
-                turn_table(2, 2)
+                turn_table(1, 1)
             half(s - 1, 1)
             give_back(("up", s - 1, 1))
-            widen(2 * s + 7)
             lat(s, 2)
+            turn(2 * s + 5)
+            if not three(s - 1):
+                common(s - 1)
+            elif KP:
+                piece(s - 1, 0, GRP - KP, GRP)
             if s >= 2:
                 turn_rotated(s - 2, 0)
             else:
                 turn_table(2, 1)
             lat(s, 3)
             turn_plain(s - 1, 1)
-            common(s - 1)
+            if three(s - 1):
+                common(s - 1)
             if s >= 3:
                 copy_out(s - 3, 3)
             else:
                 copy_table(s + 1, 0)
-            half(s - 1, 0)
-            give_back(("up", s - 1, 0))
-            turn(2 * s + 5)
+            if three(s - 1):
+                half(s - 1, 0, 0, GRP - KP)
+                give_back(("up", s - 1, 0))
             if s >= 2:
                 copy_out(s - 2, 0)
             else:
-                copy_table(2, 2)
+                copy_table(1, 1)
+            widen(2 * s + 7)
+            if not three(s - 1):
+                half(s - 1, 0)
+                give_back(("up", s - 1, 0))
             turn(2 * s + 6)
             if s >= 2:
                 copy_out(s - 2, 2)
             else:
                 copy_table(2, 1)
-            if s == 1:
-                turn_table(3, 2)
-            if s < last - 3:
-                widen_sorted(2 * s + 8)
+            if s <= 2:
+                turn_table(s + 1, 2)
+                copy_table(s + 1, 2)
+            if s == 3:
+                turn_table(3, 1)
+                copy_table(3, 1)
             quant_x(s)
             quant_lat(s)
 
@@ -566,25 +545,25 @@ def tile_multiheadlatentattention_pa_t_kernel(
         down_planes(2 * e)
         down(d, 2)
         down(d, 3)
+        copy_out(b, 1)
         up_sum(c)
         scale(2 * NG - 3)
         up(c, 1)
         lat_planes(2 * e)
         weave(2 * e)
         up(c, 0)
-        copy_out(b, 1)
         scale(2 * NG - 2)
         turn(2 * NG - 1)
         turn_rotated(a, 1)
         half(c, 1)
         give_back(("up", c, 1))
-        half(c, 0)
-        give_back(("up", c, 0))
         lat(d, 2)
         turn_plain(b, 0)
         lat(d, 3)
         turn_rotated(b, 0)
         common(c)
+        half(c, 0)
+        give_back(("up", c, 0))
         turn_plain(c, 1)
         quant_lat(d)
         quant_x(d)
@@ -631,9 +610,9 @@ def tile_multiheadlatentattention_pa_t_kernel(
         turn_plain(d, 0)
         half(e, 1)
         give_back(("up", e, 1))
+        common(e)
         half(e, 0)
         give_back(("up", e, 0))
-        common(e)
         turn_rotated(d, 0)
         quant_lat(f)
         mixed(e, "l%d" % f)

@@ -26,6 +26,7 @@ PG = S // GRP
 NG = B * PG
 SLOTS = 4
 KP = 256
+LEND = 0
 GAUSS = (1, 0, 1, 0)
 QUARTER = [n % PG for n in range(NG)]
 OUT_BUFS = 5
@@ -119,7 +120,7 @@ def tile_multiheadlatentattention_pa_t_kernel(
         wug = sb.tile([P, HALF, T4], BF16, name="lstage1", bufs=1, align_bytes=64)
         bsum = keep.tile([P, 1], F32, name="bsum")
         in_order = []
-        tab = keep.tile([P, PG, 3, GRP], BF16, name="tab", align_bytes=64)
+        tab = keep.tile([P, PG, 3 * GRP + LEND], BF16, name="tab", align_bytes=64)
         tmix = keep.tile([P, PG, 2, GRP], F32, name="tmix", align_bytes=64)
 
         xbf, xt, xs, xc, xz, ls, lc, lz, m1, m2, m3, planes, qt, pg2, pv, osb, written, rows = ({} for i in range(18))
@@ -260,24 +261,30 @@ def tile_multiheadlatentattention_pa_t_kernel(
             return qt[n]
 
         def half(n, h, lo=0, hi=GRP):
-            nc.scalar.activation(out=biased(n)[:, h, lo:hi], in_=m2[n, h][:, lo:hi], func=IDENT, bias=bu[:, h, 0:1])
+            nc.scalar.activation(out=biased(n)[:, 1 - h, lo:hi], in_=m2[n, h][:, lo:hi], func=IDENT, bias=bu[:, h, 0:1])
 
         def piece(n, h, lo=0, hi=GRP):
             nc.vector.tensor_scalar(
-                out=biased(n)[:, h, lo:hi], in0=m2[n, h][:, lo:hi], scalar1=bu[:, h, 0:1], scalar2=None, op0=ADD
+                out=biased(n)[:, 1 - h, lo:hi], in0=m2[n, h][:, lo:hi], scalar1=bu[:, h, 0:1], scalar2=None, op0=ADD
             )
 
+        def cos_sin(pg):
+            return tab[:, pg, GRP + LEND :].rearrange("p (i r) -> p i r", i=2)
+
+        def lent(n):
+            return LEND if n < NG - 4 and not three(n) else 0
+
         def common(n):
-            pg = QUARTER[n]
+            pg, lo = QUARTER[n], lent(n)
             if three(n):
                 pv[n] = sb.tile([P, 1, GRP], F32, name="pv", bufs=3, align_bytes=64)
-                src, bias, factor = m2[n, "sum"], bsum[:], tab[:, pg, 1:2, :]
+                src, bias, factor = m2[n, "sum"], bsum[:], cos_sin(pg)[:, 0:1, :]
             else:
                 pv[n] = sb.tile([P, 2, GRP], F32, name="pv", bufs=3, align_bytes=64)
-                src, bias, factor = m2[n, 0], bu[:, 0, 0:1], tab[:, pg, 1:3, :]
+                src, bias, factor = m2[n, 0], bu[:, 0, 0:1], cos_sin(pg)[:, :, lo:GRP]
             nc.vector.scalar_tensor_tensor(
-                out=pv[n][:],
-                in0=src[:].unsqueeze(1).to_broadcast([P, 1 if three(n) else 2, GRP]),
+                out=pv[n][:, :, lo:GRP],
+                in0=src[:, lo:GRP].unsqueeze(1).to_broadcast([P, 1 if three(n) else 2, GRP - lo]),
                 scalar=bias,
                 in1=factor,
                 op0=ADD,
@@ -289,15 +296,16 @@ def tile_multiheadlatentattention_pa_t_kernel(
         def mixed_tile(n, s):
             if n not in pg2:
                 name = "lstage%d" % (int(s[1:]) % 3) if isinstance(s, str) else "slot%d" % (s % SLOTS)
-                pg2[n] = sb.tile([P, 2, GRP], F32, name=name, bufs=1, align_bytes=64)
+                pg2[n] = sb.tile([P, 2, GRP + lent(n)], F32, name=name, bufs=1, align_bytes=64)
             return pg2[n]
 
         def mixed(n, s):
-            pg = QUARTER[n]
+            pg, cols = QUARTER[n], GRP + lent(n)
             if three(n):
                 src, factor = qt[n][:], tmix[:, pg, :, :]
             else:
-                src, factor = qt[n][:, 1:2, :].to_broadcast([P, 2, GRP]), tab[:, pg, 0:2, :]
+                src = qt[n][:].rearrange("p h r -> p (h r)")[:, 0:cols].unsqueeze(1).to_broadcast([P, 2, cols])
+                factor = tab[:, pg, 0 : 2 * (GRP + LEND)].rearrange("p (i r) -> p i r", i=2)[:, :, 0:cols]
             nc.gpsimd.tensor_tensor(out=mixed_tile(n, s)[:], in0=src, in1=factor, op=MULT)
 
         def result(n, h):
@@ -319,14 +327,21 @@ def tile_multiheadlatentattention_pa_t_kernel(
         def turn_plain(n, h):
             o = bank(("out", n, h), [P, J, P], F32)
             for j in range(J):
-                nc.tensor.transpose(o[:, j, :], qt[n][:, h, j * P : (j + 1) * P], idf[:])
+                nc.tensor.transpose(o[:, j, :], qt[n][:, 1 - h, j * P : (j + 1) * P], idf[:])
             m3[n, h] = o
+
+        def terms(n, i, j):
+            cols = slice(j * P, (j + 1) * P)
+            if three(n):
+                return pv[n][:, 0, cols], pg2[n][:, i, cols]
+            if j * P < lent(n):
+                return pg2[n][:, i, GRP + j * P : GRP + (j + 1) * P], pg2[n][:, i, cols]
+            return pv[n][:, i, cols], pg2[n][:, i, cols]
 
         def turn_rotated(n, i):
             o = bank(("out", n, 2 + i), [P, J, P], F32)
             for j in range(J):
-                cols = slice(j * P, (j + 1) * P)
-                for k, term in enumerate((pv[n][:, 0, cols], pg2[n][:, 1 - i, cols]) if three(n) else (pv[n][:, i, cols], pg2[n][:, i, cols])):
+                for k, term in enumerate(terms(n, i, j)):
                     nc.tensor.matmul(o[:, j, :], lhsT=term, rhs=idf[:], start=k == 0, stop=k == 1, is_transpose=True)
             m3[n, 2 + i] = o
 
@@ -352,13 +367,24 @@ def tile_multiheadlatentattention_pa_t_kernel(
             give_back(("out", n, h))
             store(n, h)
 
+        def mixed_vector(n, s, h):
+            pg = QUARTER[n]
+            nc.vector.scalar_tensor_tensor(
+                out=mixed_tile(n, s)[:, h, :],
+                in0=m2[n, 1 - h if three(n) else 1][:],
+                scalar=bu[:, 1 - h if three(n) else 1, 0:1],
+                in1=tmix[:, pg, h, :] if three(n) else tab[:, pg, h * (GRP + LEND) : h * (GRP + LEND) + GRP],
+                op0=ADD,
+                op1=MULT,
+            )
+
         def product_rows(n, h, i):
             if n not in rows:
                 rows[n] = sb.tile([P, 2, 2, GRP], F32, name="rows", bufs=1, align_bytes=64)
             nc.vector.tensor_tensor(
                 out=rows[n][:, h, i, :],
                 in0=result(n, h).rearrange("p j d -> p (j d)"),
-                in1=rope[i, QUARTER[n]].rearrange("p j d -> p (j d)"),
+                in1=m3["angles"][:, i, :] if "angles" in m3 else rope[i, QUARTER[n]].rearrange("p j d -> p (j d)"),
                 op=MULT,
             )
 
@@ -372,28 +398,47 @@ def tile_multiheadlatentattention_pa_t_kernel(
             store(n, 2 + i)
 
         def turn_table(pg, k):
+            tiles = range(J)
             if GAUSS[pg]:
-                terms = ([[(1, idb), (0, idn)]], [[(1, idn), (0, idn)]], [[(0, idb)]])[k]
+                sums = ([(1, idn), (0, idn)], [(1, idb), (0, idn)], [(0, idb)])[k]
+                plan = [[(i, j, ident) for i, ident in sums] for j in tiles]
             else:
-                terms = ([[(1, idn)], [(0, idb)]], [], [[(1, idb)]])[k]
-            if terms:
-                o = bank(("tab", pg, k), [P, len(terms), J, P], F32 if len(terms[0]) == 2 else BF16)
-                for q, plane in enumerate(terms):
-                    for j in range(J):
-                        for a, (i, ident) in enumerate(plane):
-                            nc.tensor.matmul(
-                                o[:, q, j, :], lhsT=rope[i, pg][:, j, :], rhs=ident[:], start=a == 0, stop=a == len(plane) - 1
-                            )
+                first = [[(1, j, idn)] for j in tiles] + [[(0, j, idb)] for j in range(LEND // P)]
+                plan = ([[(i, j, idb)] for i in range(2) for j in tiles], [], first)[k]
+            if plan:
+                o = bank(("tab", pg, k), [P, len(plan), P], F32 if len(plan[0]) == 2 else BF16)
+                for q, group in enumerate(plan):
+                    for a, (i, j, ident) in enumerate(group):
+                        nc.tensor.matmul(
+                            o[:, q, :], lhsT=rope[i, pg][:, j, :], rhs=ident[:], start=a == 0, stop=a == len(group) - 1
+                        )
                 m3["tab", pg, k] = o
 
         def copy_table(pg, k):
             if ("tab", pg, k) in m3:
                 if GAUSS[pg]:
-                    dst = tab[:, pg, 1:2, :] if k == 2 else tmix[:, pg, k : k + 1, :]
+                    dst = cos_sin(pg)[:, 0, :] if k == 2 else tmix[:, pg, k, :]
                 else:
-                    dst = tab[:, pg, 2:3, :] if k == 2 else tab[:, pg, 0:2, :]
-                nc.scalar.copy(out=dst, in_=m3["tab", pg, k][:].rearrange("p a j r -> p a (j r)"))
+                    dst = tab[:, pg, 0 : GRP + LEND] if k == 2 else tab[:, pg, GRP + LEND :]
+                nc.scalar.copy(out=dst, in_=m3["tab", pg, k][:].rearrange("p q r -> p (q r)"))
                 give_back(("tab", pg, k))
+
+        def turn_sines(pg, signs):
+            o = bank("sines", [P, len(signs), J, P], BF16)
+            for a, ident in enumerate(signs):
+                for j in range(J):
+                    nc.tensor.matmul(o[:, a, j, :], lhsT=rope[1, pg][:, j, :], rhs=ident[:], start=True, stop=True)
+            m3["sines"] = o
+
+        def copy_sines(k, pool, name):
+            m3["signed"] = pool.tile([P, k, GRP], BF16, name=name, bufs=1, align_bytes=64)
+            nc.scalar.copy(out=m3["signed"][:], in_=m3["sines"][:].rearrange("p a j r -> p a (j r)"))
+            give_back("sines")
+
+        def mix_sines(pg, k):
+            nc.gpsimd.tensor_tensor(
+                out=tmix[:, pg, k, :], in0=m3["signed"][:, k, :], in1=cos_sin(pg)[:, 0, :], op=SUB
+            )
 
         def turn_weights(w, h, key):
             m3[key] = turn_words(key, w[:, 2 * h : 2 * h + 2, :].bitcast(F32))
@@ -427,18 +472,21 @@ def tile_multiheadlatentattention_pa_t_kernel(
         widen(3)
         turn_weights(wd, 0, "wa")
         turn_weights(wd, 1, "wb")
+        widen(4)
         copy_weights(wdg, 0, "wa")
         copy_weights(wdg, 1, "wb")
         turn(3)
-        widen(4)
         quant_x(-2, HG, GRP)
-        quant_weights(wdg, wdc, wds)
         quant_x(-1)
+        quant_weights(wdg, wdc, wds)
         widen(5)
-        turn_table(0, 0)
-        copy_table(0, 0)
         turn(4)
+        turn_table(0, 2)
+        turn_sines(0, (idn, idb))
+        copy_table(0, 2)
         widen(6)
+        copy_sines(2, keep, "wdg")
+        mix_sines(0, 0)
         scale(3)
         down_planes(0)
         lat_planes(0)
@@ -446,29 +494,29 @@ def tile_multiheadlatentattention_pa_t_kernel(
         down(0, 2)
         scale(4)
         down(0, 3)
+        turn(5)
         turn_weights(wu, 0, "wu")
+        widen(7)
         copy_weights(wug, 0, "wu")
         down_planes(2)
-        lat_planes(2)
-        turn_table(0, 2)
         lat(0, 2)
-        turn(5)
+        turn_table(1, 2)
         lat(0, 3)
         turn(6)
-        copy_table(0, 2)
-        widen(7)
-        turn_table(0, 1)
+        lat_planes(2)
         turn_table(1, 0)
-        turn_table(1, 2)
-        widen(8)
-        copy_table(0, 1)
-        copy_table(1, 0)
+        scale(5)
+        turn(7)
         copy_table(1, 2)
+        widen(8)
+        turn_table(2, 0)
+        copy_table(1, 0)
         quant_x(0)
         quant_weights(wug, wuc, wus)
         quant_lat(0)
         sum_biases()
         weave(2)
+        mix_sines(0, 1)
 
         for s in range(1, last - 2):
             if s >= 2:
@@ -478,28 +526,31 @@ def tile_multiheadlatentattention_pa_t_kernel(
             down(s, 3)
             if s >= 2:
                 copy_out(s - 2, 1)
+            else:
+                copy_table(2, 0)
             up(s - 1, 1)
-            scale(2 * s + 3)
+            scale(2 * s + 4)
             up(s - 1, 0)
             lat_planes(2 * s + 2)
             weave(2 * s + 2)
             up_sum(s - 1)
-            if s >= 2:
-                widen(2 * s + 6)
-            scale(2 * s + 4)
+            widen(2 * s + 7)
+            scale(2 * s + 5)
             if s >= 3:
                 turn_rotated(s - 3, 1)
             else:
-                turn_table(s + 1, 0)
+                turn_table(3, 2 * s - 2)
             if s >= 2:
                 turn_plain(s - 2, 0)
             else:
-                turn_table(1, 1)
+                turn_table(2, 2)
             half(s - 1, 1)
             give_back(("up", s - 1, 1))
             lat(s, 2)
-            turn(2 * s + 5)
+            turn(2 * s + 6)
             if not three(s - 1):
+                if lent(s - 1):
+                    piece(s - 1, 0, 0, lent(s - 1))
                 common(s - 1)
             elif KP:
                 piece(s - 1, 0, GRP - KP, GRP)
@@ -514,29 +565,24 @@ def tile_multiheadlatentattention_pa_t_kernel(
             if s >= 3:
                 copy_out(s - 3, 3)
             else:
-                copy_table(s + 1, 0)
+                copy_table(3, 2 * s - 2)
             if three(s - 1):
                 half(s - 1, 0, 0, GRP - KP)
                 give_back(("up", s - 1, 0))
             if s >= 2:
                 copy_out(s - 2, 0)
             else:
-                copy_table(1, 1)
-            widen(2 * s + 7)
+                copy_table(2, 2)
+            if s < last - 3:
+                widen(2 * s + 8)
             if not three(s - 1):
-                half(s - 1, 0)
+                half(s - 1, 0, lent(s - 1), GRP)
                 give_back(("up", s - 1, 0))
-            turn(2 * s + 6)
+            turn(2 * s + 7)
             if s >= 2:
                 copy_out(s - 2, 2)
             else:
                 copy_table(2, 1)
-            if s <= 2:
-                turn_table(s + 1, 2)
-                copy_table(s + 1, 2)
-            if s == 3:
-                turn_table(3, 1)
-                copy_table(3, 1)
             quant_x(s)
             quant_lat(s)
 
@@ -547,96 +593,94 @@ def tile_multiheadlatentattention_pa_t_kernel(
         down(d, 3)
         copy_out(b, 1)
         up_sum(c)
-        scale(2 * NG - 3)
+        scale(2 * NG - 2)
         up(c, 1)
         lat_planes(2 * e)
         weave(2 * e)
         up(c, 0)
-        scale(2 * NG - 2)
-        turn(2 * NG - 1)
+        scale(2 * NG - 1)
         turn_rotated(a, 1)
         half(c, 1)
         give_back(("up", c, 1))
+        half(c, 0)
+        give_back(("up", c, 0))
         lat(d, 2)
         turn_plain(b, 0)
         lat(d, 3)
         turn_rotated(b, 0)
         common(c)
-        half(c, 0)
-        give_back(("up", c, 0))
         turn_plain(c, 1)
-        quant_lat(d)
-        quant_x(d)
-        mixed(c, "l%d" % d)
         copy_out(a, 3)
-        up_sum(d)
+        turn_rotated(b, 1)
         copy_out(b, 0)
+        quant_x(d)
+        quant_x(e, 0, HG)
+        quant_lat(d)
+        mixed(c, e)
+        copy_out(b, 2)
+        down(e, 2)
+        down(e, 3)
+        copy_out(c, 1, nc.vector.tensor_copy)
         up(d, 1)
         up(d, 0)
-        scale(2 * NG - 1)
-        down(e, 2)
-        copy_out(b, 2)
-        down(e, 3)
-        common(d)
-        copy_out(c, 1)
+        copy_out(b, 3)
         down(f, 0)
+        lat(e, 2)
         down(f, 1)
+        lat(e, 3)
         half(d, 1)
         give_back(("up", d, 1))
-        turn_rotated(b, 1)
+        turn_plain(c, 0)
+        common(d)
+        turn_plain(d, 1)
+        turn_rotated(c, 0)
+        copy_out(c, 0)
+        quant_lat(e)
+        mixed(d, "l%d" % e)
+        copy_out(d, 1)
         half(d, 0)
         give_back(("up", d, 0))
-        lat(e, 2)
-        turn_plain(c, 0)
-        lat(e, 3)
-        turn_rotated(c, 0)
-        quant_x(e, 0, HG)
-        quant_lat(e)
-        mixed(d, e)
-        copy_out(b, 3)
+        lat(f, 0)
         down(f, 2)
         down(f, 3)
-        copy_out(c, 0)
-        lat(f, 0)
+        lat(f, 1)
         up_sum(e)
         copy_out(c, 2)
         up(e, 1)
-        up(e, 0)
-        lat(f, 1)
-        turn_rotated(c, 1)
         lat(f, 2)
-        turn_plain(d, 1)
+        up(e, 0)
         lat(f, 3)
+        turn_rotated(c, 1)
         turn_plain(d, 0)
         half(e, 1)
-        give_back(("up", e, 1))
-        common(e)
         half(e, 0)
-        give_back(("up", e, 0))
-        turn_rotated(d, 0)
+        common(e)
+        turn_plain(e, 1)
         quant_lat(f)
-        mixed(e, "l%d" % f)
         copy_out(c, 3)
         up_tokens(f, 0)
+        mixed_vector(e, f, 0)
+        give_back(("up", e, 1))
         up_tokens(f, 1)
-        copy_out(d, 1, nc.vector.tensor_copy)
         copy_out(d, 0)
+        mixed_vector(e, f, 1)
+        give_back(("up", e, 0))
+        turn_rotated(d, 0)
         turn_rotated(d, 1)
-        turn_plain(e, 1)
-        turn_plain(e, 0)
-        copy_out(d, 2)
+        copy_out(e, 1)
         plain(f, 0)
-        plain(f, 1)
         turn_rotated(e, 0)
+        copy_out(d, 2)
+        plain(f, 1)
         turn_rotated(e, 1)
         copy_out(d, 3)
-        copy_out(e, 1)
+        turn_plain(e, 0)
+        copy_out(e, 2)
         product_rows(f, 0, 0)
         product_rows(f, 1, 1)
-        copy_out(e, 0)
+        copy_out(e, 3)
         product_rows(f, 0, 1)
         rotated_rows(f, 0)
-        copy_out(e, 2)
+        copy_out(e, 0)
         product_rows(f, 1, 0)
-        copy_out(e, 3)
         rotated_rows(f, 1)

@@ -105,6 +105,8 @@ def tile_multiheadlatentattention_pa_t_kernel(
             load_x(n, (0, J))
         nc.sync.dma_start(out=bias_row[:], in_=bq_up.partition_broadcast(P))
 
+        zeros = keep.tile([P, GRP], BF16, name="zeros")
+        nc.vector.memset(zeros[:], 0.0)
         idf = keep.tile([P, P], F32, name="idf")
         make_identity(nc, idf[:])
         idb = keep.tile([P, P], BF16, name="idb")
@@ -146,6 +148,12 @@ def tile_multiheadlatentattention_pa_t_kernel(
         def turn(m, lo=0, hi=2):
             t = turn_words(("x", m, lo), xbf[m][:, lo:hi, :].bitcast(F32), m in in_order)
             xt[m, lo] = t[:].bitcast(BF16).rearrange("p u (r e) -> p r u e", e=2)
+
+        def warm_up(count):
+            o = bank("warm", [P, GRP], F32)
+            for i in range(count):
+                nc.tensor.matmul(o[:], lhsT=zeros[:, 0:P], rhs=zeros[:], start=True, stop=True)
+            give_back("warm")
 
         def x_place(m):
             return divmod(m - 3, 2) if m < 2 * NG - 1 else (NG - 2, 0)
@@ -456,6 +464,7 @@ def tile_multiheadlatentattention_pa_t_kernel(
             nc.vector.tensor_tensor(out=bsum[:], in0=bu[:, 0, 0:1], in1=bu[:, 1, 0:1], op=ADD)
 
         last = NG - 1
+        warm_up(5)
 
         widen(0, 0, 1)
         widen(0, 1, 2)

@@ -12,6 +12,7 @@ FP8X4 = mybir.dt.float8_e4m3fn_x4
 ADD = mybir.AluOpType.add
 MULT = mybir.AluOpType.mult
 SUB = mybir.AluOpType.subtract
+COPY = mybir.ActivationFunctionType.Copy
 IDENT = mybir.ActivationFunctionType.Identity
 
 B, S, H, LAT, HALF = 4, 2048, 512, 512, 256
@@ -27,9 +28,13 @@ NG = B * PG
 SLOTS = 4
 KP = 256
 LEND = 0
+KEEP = 0
 GAUSS = (1, 0, 1, 0)
 QUARTER = [n % PG for n in range(NG)]
+FOUR = ()
+DIRECT = ()
 OUT_BUFS = 5
+WIDE_BUFS = 6
 
 
 def tile_multiheadlatentattention_pa_t_kernel(
@@ -45,19 +50,23 @@ def tile_multiheadlatentattention_pa_t_kernel(
         free = list(range(8))
         held = {}
 
-        def bank(key, shape, dtype):
+        def bank(key, shape, dtype, readers=1):
             i = free.pop(0)
-            held[key] = (ps.tile(shape, dtype, name="bank%d" % i), i)
+            held[key] = (ps.tile(shape, dtype, name="bank%d" % i), i, readers)
             return held[key][0]
 
         def give_back(key):
-            free.append(held.pop(key)[1])
+            t, i, readers = held.pop(key)
+            if readers > 1:
+                held[key] = (t, i, readers - 1)
+            else:
+                free.append(i)
 
         def place(n):
             return QUARTER[n], n // PG
 
         def three(n):
-            return GAUSS[QUARTER[n]]
+            return GAUSS[QUARTER[n]] and n not in FOUR
 
         xb = {}
 
@@ -89,19 +98,20 @@ def tile_multiheadlatentattention_pa_t_kernel(
         bias_row = keep.tile([P, HALF], BF16, name="bias_row")
         load_x(0, (0, 1, 2, J))
         nc.sync.dma_start(out=sc[:], in_=x_scale.rearrange("a b (p t) -> p (a b t)", t=T4))
-        load_x(1, (0, 2))
         nc.sync.dma_start(out=wd[:, 0:2, :], in_=wd_rows[:, 0:2, :])
+        load_x(1, (0, 2))
         nc.sync.dma_start(out=wd[:, 2:4, :], in_=wd_rows[:, 2:4, :])
         load_x(1, (2, J))
-        nc.sync.dma_start(out=bd[:], in_=bq_down.rearrange("(p t) -> p t", t=T4))
         load_x(2, (0, J))
-        load_rope(0, 2)
+        nc.sync.dma_start(out=bd[:], in_=bq_down.rearrange("(p t) -> p t", t=T4))
+        load_rope(0, 1)
         nc.sync.dma_start(out=wu[:], in_=wq_up.rearrange("(h m) k -> m h k", h=2))
         load_x(3, (0, J))
-        load_rope(2, 4)
+        load_x(4, (0, J))
+        load_rope(1, 4)
         with nc.allow_non_contiguous_dma(reason="one bias value for each partition and half"):
             nc.sync.dma_start(out=bu[:, :, 0:1], in_=bq_up.rearrange("(h c o) -> c h o", h=2, o=1))
-        for n in range(4, NG):
+        for n in range(5, NG):
             load_x(n, (0, J))
         nc.sync.dma_start(out=bias_row[:], in_=bq_up.partition_broadcast(P))
 
@@ -123,13 +133,13 @@ def tile_multiheadlatentattention_pa_t_kernel(
         bsum = keep.tile([P, 1], F32, name="bsum")
         in_order = []
         tab = keep.tile([P, PG, 3 * GRP + LEND], BF16, name="tab", align_bytes=64)
-        tmix = keep.tile([P, PG, 2, GRP], F32, name="tmix", align_bytes=64)
+        tmix = keep.tile([P, sum(GAUSS), 2, GRP], F32, name="tmix", align_bytes=64)
 
         xbf, xt, xs, xc, xz, ls, lc, lz, m1, m2, m3, planes, qt, pg2, pv, osb, written, rows = ({} for i in range(18))
 
         def wide(m):
             if m not in xbf:
-                xbf[m] = sb.tile([P, 2, H], BF16, name="xbf", bufs=6, align_bytes=64)
+                xbf[m] = sb.tile([P, 2, H], BF16, name="xbf", bufs=WIDE_BUFS, align_bytes=64)
             return xbf[m]
 
         def widen(m, lo=0, hi=2):
@@ -159,16 +169,40 @@ def tile_multiheadlatentattention_pa_t_kernel(
             return divmod(m - 3, 2) if m < 2 * NG - 1 else (NG - 2, 0)
 
         def scale(m, lo=0, hi=2):
-            s, pos = x_place(m)
-            if s not in xs:
-                xs[s] = sb.tile([P, GRP, T4], BF16, name="slot%d" % (s % SLOTS), bufs=1, align_bytes=64)
             nc.vector.tensor_tensor(
-                out=xs[s][:, pos * HG + lo * P : pos * HG + hi * P, :].rearrange("p r (u e) -> p r u e", e=2),
+                out=x_stage(m)[:, lo * P : hi * P, :].rearrange("p r (u e) -> p r u e", e=2),
                 in0=xt[m, lo],
                 in1=sc[:].rearrange("p (u e) -> p u e", e=2).unsqueeze(1).to_broadcast([P, (hi - lo) * P, 2, 2]),
                 op=MULT,
             )
             give_back(("x", m, lo))
+
+        def x_stage(m):
+            s, pos = x_place(m)
+            if s not in xs:
+                xs[s] = sb.tile([P, GRP, T4], BF16, name="slot%d" % (s % SLOTS), bufs=1, align_bytes=64)
+            return xs[s][:, pos * HG : (pos + 1) * HG, :]
+
+        def x_planes(m):
+            planes["x", m] = sb.tile([P, T4, HG], BF16, name="planes", bufs=3, align_bytes=64)
+            for t in range(T4):
+                nc.scalar.activation(
+                    out=planes["x", m][:, t, :], in_=xt[m, 0][:, :, t // 2, t % 2], func=COPY, scale=sc[:, t : t + 1]
+                )
+            give_back(("x", m, 0))
+
+        def interleave(dst, src):
+            nc.gpsimd.tensor_scalar(
+                out=dst, in0=src.rearrange("p t r -> p r t"), scalar1=1.0, scalar2=0.0, op0=MULT, op1=ADD
+            )
+
+        def weave_x(m):
+            interleave(x_stage(m), planes["x", m][:])
+
+        def negate(pg):
+            nc.gpsimd.tensor_scalar(
+                out=tab[:, pg, 0:GRP], in0=cos_sin(pg)[:, 1, :], scalar1=-1.0, scalar2=0.0, op0=MULT, op1=ADD
+            )
 
         def quant(codes, scales, staged, name, s, lo, hi):
             if s not in codes:
@@ -239,19 +273,21 @@ def tile_multiheadlatentattention_pa_t_kernel(
                 if t % 2:
                     give_back(("planes", m, t // 2))
 
+        def tile_planes(n, j):
+            planes[n, j] = sb.tile([P, T4, P], BF16, name="planes", bufs=3, align_bytes=64)
+            for t in range(T4):
+                nc.scalar.activation(out=planes[n, j][:, t, :], in_=m1[n, j][:, t, :], func=IDENT, bias=bd[:, t : t + 1])
+            give_back(("lat", n, j))
+
+        def weave_tile(n, j):
+            interleave(lat_stage(n)[:, j * P : (j + 1) * P, :], planes[n, j][:])
+
         def weave(m):
             n, a = divmod(m, 2)
-            nc.gpsimd.tensor_scalar(
-                out=lat_stage(n)[:, a * HG : (a + 1) * HG, :],
-                in0=planes[m][:].rearrange("p t r -> p r t"),
-                scalar1=1.0,
-                scalar2=0.0,
-                op0=MULT,
-                op1=ADD,
-            )
+            interleave(lat_stage(n)[:, a * HG : (a + 1) * HG, :], planes[m][:])
 
-        def up(n, h):
-            o = bank(("up", n, h), [P, GRP], F32)
+        def up(n, h, readers=None):
+            o = bank(("up", n, h), [P, GRP], F32, readers or (1 if h or three(n) else 1 + (not direct(n))))
             mx(o[:], wuc, wus, slice(h * P, (h + 1) * P), lc[n], lz[n], slice(0, GRP))
             m2[n, h] = o
 
@@ -270,58 +306,69 @@ def tile_multiheadlatentattention_pa_t_kernel(
 
         def half(n, h, lo=0, hi=GRP):
             nc.scalar.activation(out=biased(n)[:, 1 - h, lo:hi], in_=m2[n, h][:, lo:hi], func=IDENT, bias=bu[:, h, 0:1])
+            give_back(("up", n, h))
 
         def piece(n, h, lo=0, hi=GRP):
             nc.vector.tensor_scalar(
                 out=biased(n)[:, 1 - h, lo:hi], in0=m2[n, h][:, lo:hi], scalar1=bu[:, h, 0:1], scalar2=None, op0=ADD
             )
+            give_back(("up", n, h))
 
         def cos_sin(pg):
             return tab[:, pg, GRP + LEND :].rearrange("p (i r) -> p i r", i=2)
 
+        def direct(n):
+            return n in DIRECT
+
         def lent(n):
             return LEND if n < NG - 4 and not three(n) else 0
 
-        def common(n):
-            pg, lo = QUARTER[n], lent(n)
-            if three(n):
-                pv[n] = sb.tile([P, 1, GRP], F32, name="pv", bufs=3, align_bytes=64)
-                src, bias, factor = m2[n, "sum"], bsum[:], cos_sin(pg)[:, 0:1, :]
-            else:
+        def vector_tile(n):
+            if n not in pv:
                 pv[n] = sb.tile([P, 2, GRP], F32, name="pv", bufs=3, align_bytes=64)
-                src, bias, factor = m2[n, 0], bu[:, 0, 0:1], cos_sin(pg)[:, :, lo:GRP]
+            return pv[n]
+
+        def kept(n):
+            return KEEP if three(n) and n < NG - 4 else 0
+
+        def common(n, lo=0, hi=GRP):
+            pg = QUARTER[n]
+            if three(n):
+                src, bias, factor = m2[n, "sum"], bsum[:], cos_sin(pg)[:, 0:1, lo:hi]
+            else:
+                src, bias, factor = m2[n, 0], bu[:, 0, 0:1], cos_sin(pg)[:, :, lo:hi]
             nc.vector.scalar_tensor_tensor(
-                out=pv[n][:, :, lo:GRP],
-                in0=src[:, lo:GRP].unsqueeze(1).to_broadcast([P, 1 if three(n) else 2, GRP - lo]),
+                out=vector_tile(n)[:, 0 : 1 if three(n) else 2, lo:hi],
+                in0=src[:, lo:hi].unsqueeze(1).to_broadcast([P, 1 if three(n) else 2, hi - lo]),
                 scalar=bias,
                 in1=factor,
                 op0=ADD,
                 op1=MULT,
             )
-            if three(n):
-                give_back(("sum", n))
+            give_back(("sum", n) if three(n) else ("up", n, 0))
 
         def mixed_tile(n, s):
             if n not in pg2:
-                name = "lstage%d" % (int(s[1:]) % 3) if isinstance(s, str) else "slot%d" % (s % SLOTS)
-                pg2[n] = sb.tile([P, 2, GRP + lent(n)], F32, name=name, bufs=1, align_bytes=64)
+                pg2[n] = sb.tile([P, 2, GRP], F32, name=s, bufs=1, align_bytes=64)
             return pg2[n]
 
         def mixed(n, s):
             pg, cols = QUARTER[n], GRP + lent(n)
+            dst = mixed_tile(n, s)[:]
             if three(n):
-                src, factor = qt[n][:], tmix[:, pg, :, :]
+                flat = [t.rearrange("p h r -> p (h r)")[:, 0 : 2 * GRP - kept(n)] for t in (dst, qt[n][:], tmix[:, sum(GAUSS[:pg]), :, :])]
+                dst, src, factor = flat
             else:
                 src = qt[n][:].rearrange("p h r -> p (h r)")[:, 0:cols].unsqueeze(1).to_broadcast([P, 2, cols])
                 factor = tab[:, pg, 0 : 2 * (GRP + LEND)].rearrange("p (i r) -> p i r", i=2)[:, :, 0:cols]
-            nc.gpsimd.tensor_tensor(out=mixed_tile(n, s)[:], in0=src, in1=factor, op=MULT)
+            nc.gpsimd.tensor_tensor(out=dst, in0=src, in1=factor, op=MULT)
 
         def result(n, h):
             if n not in osb:
                 osb[n] = sb.tile([P, 4, J, P], F32, name="osb", bufs=OUT_BUFS)
             return osb[n][:, h, :, :]
 
-        def store(n, h):
+        def store(n, h, lo=0, hi=J):
             written.setdefault(n, []).append(h)
             heads = slice(h, h + 1)
             if n < NG - OUT_BUFS:
@@ -329,8 +376,11 @@ def tile_multiheadlatentattention_pa_t_kernel(
                     return
                 heads = slice(0, 4)
             pg, b = place(n)
-            dst = out[b, heads, pg * GRP : (pg + 1) * GRP, :].rearrange("h (p j) d -> p h (j d)", j=J)
-            nc.sync.dma_start(out=dst, in_=osb[n][:, heads, :, :].rearrange("p h j d -> p h (j d)"))
+            dst = out[b, heads, pg * GRP : (pg + 1) * GRP, :].rearrange("h (p j) d -> p h j d", j=J)
+            nc.sync.dma_start(
+                out=dst[:, :, lo:hi, :].rearrange("p h j d -> p h (j d)"),
+                in_=osb[n][:, heads, lo:hi, :].rearrange("p h j d -> p h (j d)"),
+            )
 
         def turn_plain(n, h):
             o = bank(("out", n, h), [P, J, P], F32)
@@ -341,7 +391,8 @@ def tile_multiheadlatentattention_pa_t_kernel(
         def terms(n, i, j):
             cols = slice(j * P, (j + 1) * P)
             if three(n):
-                return pv[n][:, 0, cols], pg2[n][:, i, cols]
+                by_vector = i == 1 and j * P >= GRP - kept(n)
+                return pv[n][:, 0, cols], (pv if by_vector else pg2)[n][:, i, cols]
             if j * P < lent(n):
                 return pg2[n][:, i, GRP + j * P : GRP + (j + 1) * P], pg2[n][:, i, cols]
             return pv[n][:, i, cols], pg2[n][:, i, cols]
@@ -381,29 +432,35 @@ def tile_multiheadlatentattention_pa_t_kernel(
                 out=mixed_tile(n, s)[:, h, :],
                 in0=m2[n, 1 - h if three(n) else 1][:],
                 scalar=bu[:, 1 - h if three(n) else 1, 0:1],
-                in1=tmix[:, pg, h, :] if three(n) else tab[:, pg, h * (GRP + LEND) : h * (GRP + LEND) + GRP],
+                in1=tmix[:, sum(GAUSS[:pg]), h, :] if three(n) else tab[:, pg, h * (GRP + LEND) : h * (GRP + LEND) + GRP],
                 op0=ADD,
                 op1=MULT,
             )
+            give_back(("up", n, 1 - h if three(n) else 1))
 
-        def product_rows(n, h, i):
+        def product_rows(n, h, i, lo=0, hi=J):
             if n not in rows:
-                rows[n] = sb.tile([P, 2, 2, GRP], F32, name="rows", bufs=1, align_bytes=64)
+                rows[n] = sb.tile([P, 2, 2, J, P], F32, name="rows", bufs=1, align_bytes=64)
             nc.vector.tensor_tensor(
-                out=rows[n][:, h, i, :],
-                in0=result(n, h).rearrange("p j d -> p (j d)"),
-                in1=m3["angles"][:, i, :] if "angles" in m3 else rope[i, QUARTER[n]].rearrange("p j d -> p (j d)"),
+                out=rows[n][:, h, i, lo:hi, :],
+                in0=result(n, h)[:, lo:hi, :],
+                in1=rope[i, QUARTER[n]][:, lo:hi, :],
                 op=MULT,
             )
 
-        def rotated_rows(n, i):
+        def rotated_rows(n, i, lo=0, hi=J):
             nc.vector.tensor_tensor(
-                out=result(n, 2 + i).rearrange("p j d -> p (j d)"),
-                in0=rows[n][:, 0, i, :],
-                in1=rows[n][:, 1, 1 - i, :],
+                out=result(n, 2 + i)[:, lo:hi, :],
+                in0=rows[n][:, 0, i, lo:hi, :],
+                in1=rows[n][:, 1, 1 - i, lo:hi, :],
                 op=(SUB, ADD)[i],
             )
-            store(n, 2 + i)
+            store(n, 2 + i, lo, hi)
+
+        def mixed_half(n, s, h):
+            nc.gpsimd.tensor_tensor(
+                out=mixed_tile(n, s)[:, h, :], in0=qt[n][:, h, :], in1=tmix[:, sum(GAUSS[: QUARTER[n]]), h, :], op=MULT
+            )
 
         def turn_table(pg, k):
             tiles = range(J)
@@ -425,27 +482,26 @@ def tile_multiheadlatentattention_pa_t_kernel(
         def copy_table(pg, k):
             if ("tab", pg, k) in m3:
                 if GAUSS[pg]:
-                    dst = cos_sin(pg)[:, 0, :] if k == 2 else tmix[:, pg, k, :]
+                    dst = cos_sin(pg)[:, 0, :] if k == 2 else tmix[:, sum(GAUSS[:pg]), k, :]
                 else:
                     dst = tab[:, pg, 0 : GRP + LEND] if k == 2 else tab[:, pg, GRP + LEND :]
                 nc.scalar.copy(out=dst, in_=m3["tab", pg, k][:].rearrange("p q r -> p (q r)"))
                 give_back(("tab", pg, k))
 
-        def turn_sines(pg, signs):
-            o = bank("sines", [P, len(signs), J, P], BF16)
-            for a, ident in enumerate(signs):
+        def turn_angles(pg):
+            o = bank(("angles", pg), [P, 2, J, P], BF16)
+            for i in range(2):
                 for j in range(J):
-                    nc.tensor.matmul(o[:, a, j, :], lhsT=rope[1, pg][:, j, :], rhs=ident[:], start=True, stop=True)
-            m3["sines"] = o
+                    nc.tensor.matmul(o[:, i, j, :], lhsT=rope[i, pg][:, j, :], rhs=idb[:], start=True, stop=True)
+            m3["angles", pg] = o
 
-        def copy_sines(k, pool, name):
-            m3["signed"] = pool.tile([P, k, GRP], BF16, name=name, bufs=1, align_bytes=64)
-            nc.scalar.copy(out=m3["signed"][:], in_=m3["sines"][:].rearrange("p a j r -> p a (j r)"))
-            give_back("sines")
+        def copy_angles(pg):
+            nc.scalar.copy(out=tab[:, pg, GRP:], in_=m3["angles", pg][:].rearrange("p i j r -> p (i j r)"))
+            give_back(("angles", pg))
 
-        def mix_sines(pg, k):
+        def mix_difference(pg):
             nc.gpsimd.tensor_tensor(
-                out=tmix[:, pg, k, :], in0=m3["signed"][:, k, :], in1=cos_sin(pg)[:, 0, :], op=SUB
+                out=tmix[:, sum(GAUSS[:pg]), 1, :], in0=cos_sin(pg)[:, 1, :], in1=cos_sin(pg)[:, 0, :], op=SUB
             )
 
         def turn_weights(w, h, key):
@@ -476,70 +532,71 @@ def tile_multiheadlatentattention_pa_t_kernel(
         turn(1)
         scale(1)
         widen(2)
-        turn(2)
-        scale(2)
-        widen(3)
         turn_weights(wd, 0, "wa")
-        turn_weights(wd, 1, "wb")
+        turn(2)
+        widen(3)
         widen(4)
+        turn_weights(wd, 1, "wb")
         copy_weights(wdg, 0, "wa")
+        quant_x(-2, HG, GRP)
+        scale(2)
         copy_weights(wdg, 1, "wb")
         turn(3)
-        quant_x(-2, HG, GRP)
-        quant_x(-1)
-        quant_weights(wdg, wdc, wds)
-        widen(5)
+        turn_angles(0)
         turn(4)
-        turn_table(0, 2)
-        turn_sines(0, (idn, idb))
-        copy_table(0, 2)
-        widen(6)
-        copy_sines(2, keep, "wdg")
-        mix_sines(0, 0)
-        scale(3)
-        down_planes(0)
-        lat_planes(0)
-        weave(0)
-        down(0, 2)
+        quant_weights(wdg, wdc, wds)
+        quant_x(-1)
+        x_planes(3)
+        weave_x(3)
+        widen(5)
+        turn_table(0, 0)
+        down(0, 0)
+        down(0, 1)
         scale(4)
+        down(0, 2)
         down(0, 3)
+        copy_angles(0)
+        mix_difference(0)
+        tile_planes(0, 0)
+        weave_tile(0, 0)
+        copy_table(0, 0)
+        lat(0, 1)
         turn(5)
         turn_weights(wu, 0, "wu")
-        widen(7)
-        copy_weights(wug, 0, "wu")
-        down_planes(2)
         lat(0, 2)
-        turn_table(1, 2)
+        widen(6)
+        widen(7)
+        down_planes(2)
+        copy_weights(wug, 0, "wu")
         lat(0, 3)
+        turn_table(1, 0)
+        widen(8)
         turn(6)
         lat_planes(2)
-        turn_table(1, 0)
         scale(5)
         turn(7)
-        copy_table(1, 2)
-        widen(8)
-        turn_table(2, 0)
         copy_table(1, 0)
+        turn_table(2, 2)
         quant_x(0)
         quant_weights(wug, wuc, wus)
         quant_lat(0)
         sum_biases()
         weave(2)
-        mix_sines(0, 1)
-
+        negate(1)
         for s in range(1, last - 2):
             if s >= 2:
-                mixed(s - 2, s - 1)
+                mixed(s - 2, "slot%d" % ((s - 1) % SLOTS))
             down_planes(2 * s + 2)
             down(s, 2)
             down(s, 3)
             if s >= 2:
                 copy_out(s - 2, 1)
             else:
-                copy_table(2, 0)
+                copy_table(2, 2)
             up(s - 1, 1)
             scale(2 * s + 4)
-            up(s - 1, 0)
+            share = KP if three(s - 1) and s > 1 else 0
+            up(s - 1, 0, 2 if share or not three(s - 1) else 1)
             lat_planes(2 * s + 2)
             weave(2 * s + 2)
             up_sum(s - 1)
@@ -549,24 +606,21 @@ def tile_multiheadlatentattention_pa_t_kernel(
                 turn_rotated(s - 3, 1)
             else:
                 turn_table(3, 2 * s - 2)
+            if s == 2:
+                turn_table(2, 1)
             if s >= 2:
                 turn_plain(s - 2, 0)
             else:
-                turn_table(2, 2)
+                turn_table(2, 0)
             half(s - 1, 1)
-            give_back(("up", s - 1, 1))
             lat(s, 2)
             turn(2 * s + 6)
             if not three(s - 1):
-                if lent(s - 1):
-                    piece(s - 1, 0, 0, lent(s - 1))
                 common(s - 1)
-            elif KP:
-                piece(s - 1, 0, GRP - KP, GRP)
+            elif share:
+                piece(s - 1, 0, GRP - share, GRP)
             if s >= 2:
                 turn_rotated(s - 2, 0)
-            else:
-                turn_table(2, 1)
             lat(s, 3)
             turn_plain(s - 1, 1)
             if three(s - 1):
@@ -575,28 +629,26 @@ def tile_multiheadlatentattention_pa_t_kernel(
                 copy_out(s - 3, 3)
             else:
                 copy_table(3, 2 * s - 2)
+            if s == 2:
+                copy_table(2, 1)
             if three(s - 1):
-                half(s - 1, 0, 0, GRP - KP)
-                give_back(("up", s - 1, 0))
+                half(s - 1, 0, 0, GRP - share)
             if s >= 2:
                 copy_out(s - 2, 0)
             else:
-                copy_table(2, 2)
+                copy_table(2, 0)
             if s < last - 3:
                 widen(2 * s + 8)
             if not three(s - 1):
-                half(s - 1, 0, lent(s - 1), GRP)
-                give_back(("up", s - 1, 0))
+                half(s - 1, 0)
             turn(2 * s + 7)
             if s >= 2:
                 copy_out(s - 2, 2)
-            else:
-                copy_table(2, 1)
             quant_x(s)
             quant_lat(s)
 
         a, b, c, d, e, f = range(NG - 6, NG)
-        mixed(b, c)
+        mixed(b, "slot%d" % (c % SLOTS))
         down_planes(2 * e)
         down(d, 2)
         down(d, 3)
@@ -610,9 +662,7 @@ def tile_multiheadlatentattention_pa_t_kernel(
         scale(2 * NG - 1)
         turn_rotated(a, 1)
         half(c, 1)
-        give_back(("up", c, 1))
         half(c, 0)
-        give_back(("up", c, 0))
         lat(d, 2)
         turn_plain(b, 0)
         lat(d, 3)
@@ -625,71 +675,69 @@ def tile_multiheadlatentattention_pa_t_kernel(
         quant_x(d)
         quant_x(e, 0, HG)
         quant_lat(d)
-        mixed(c, e)
+        mixed(c, "slot%d" % (e % SLOTS))
+        copy_out(c, 1, nc.vector.tensor_copy)
         copy_out(b, 2)
         down(e, 2)
         down(e, 3)
-        copy_out(c, 1, nc.vector.tensor_copy)
         up(d, 1)
         up(d, 0)
-        copy_out(b, 3)
         down(f, 0)
         lat(e, 2)
         down(f, 1)
-        lat(e, 3)
         half(d, 1)
-        give_back(("up", d, 1))
+        lat(e, 3)
+        copy_out(b, 3)
         turn_plain(c, 0)
         common(d)
         turn_plain(d, 1)
-        turn_rotated(c, 0)
         copy_out(c, 0)
-        quant_lat(e)
-        mixed(d, "l%d" % e)
-        copy_out(d, 1)
-        half(d, 0)
-        give_back(("up", d, 0))
-        lat(f, 0)
         down(f, 2)
         down(f, 3)
+        half(d, 0)
+        quant_lat(e)
+        mixed(d, "lstage%d" % (e % 3))
+        copy_out(d, 1)
+        lat(f, 0)
+        turn_rotated(c, 0)
         lat(f, 1)
-        up_sum(e)
-        copy_out(c, 2)
-        up(e, 1)
-        lat(f, 2)
-        up(e, 0)
-        lat(f, 3)
         turn_rotated(c, 1)
+        copy_out(c, 2)
+        up_sum(e)
+        lat(f, 2)
+        up(e, 0, 2)
+        copy_out(c, 3)
+        lat(f, 3)
+        up(e, 1)
         turn_plain(d, 0)
-        half(e, 1)
         half(e, 0)
         common(e)
-        turn_plain(e, 1)
+        half(e, 1)
         quant_lat(f)
-        copy_out(c, 3)
-        up_tokens(f, 0)
-        mixed_vector(e, f, 0)
-        give_back(("up", e, 1))
-        up_tokens(f, 1)
-        copy_out(d, 0)
-        mixed_vector(e, f, 1)
-        give_back(("up", e, 0))
+        mixed_half(e, "lstage%d" % (f % 3), 0)
         turn_rotated(d, 0)
-        turn_rotated(d, 1)
-        copy_out(e, 1)
-        plain(f, 0)
-        turn_rotated(e, 0)
+        mixed_vector(e, "lstage%d" % (f % 3), 1)
+        copy_out(d, 0)
+        up_tokens(f, 0)
+        up_tokens(f, 1)
         copy_out(d, 2)
+        turn_plain(e, 0)
+        turn_rotated(d, 1)
+        plain(f, 0)
+        copy_out(e, 0)
         plain(f, 1)
+        turn_plain(e, 1)
         turn_rotated(e, 1)
         copy_out(d, 3)
-        turn_plain(e, 0)
-        copy_out(e, 2)
+        turn_rotated(e, 0)
         product_rows(f, 0, 0)
+        copy_out(e, 1)
         product_rows(f, 1, 1)
-        copy_out(e, 3)
         product_rows(f, 0, 1)
+        copy_out(e, 3)
         rotated_rows(f, 0)
-        copy_out(e, 0)
-        product_rows(f, 1, 0)
-        rotated_rows(f, 1)
+        copy_out(e, 2)
+        product_rows(f, 1, 0, 0, 2)
+        product_rows(f, 1, 0, 2, J)
+        rotated_rows(f, 1, 0, 2)
+        rotated_rows(f, 1, 2, J)

from contextlib import ExitStack

import concourse.mybir as mybir
from concourse.masks import make_identity

F32 = mybir.dt.float32
BF16 = mybir.dt.bfloat16
U32 = mybir.dt.uint32
U8 = mybir.dt.uint8
FP8 = mybir.dt.float8_e4m3fn
FP8X4 = mybir.dt.float8_e4m3fn_x4
ADD = mybir.AluOpType.add
MULT = mybir.AluOpType.mult
SUB = mybir.AluOpType.subtract
COPY = mybir.ActivationFunctionType.Copy
IDENT = mybir.ActivationFunctionType.Identity

B, S, H, LAT, HALF = 4, 2048, 512, 512, 256
FLOPS = 2 * B * S * H * LAT + 2 * B * S * LAT * HALF

P = 128
T4 = 4
J = 4
GRP = P * J
HG = GRP // 2
PG = S // GRP
NG = B * PG
SLOTS = 4
KP = 256
LEND = 0
KEEP = 0
GAUSS = (1, 0, 1, 0)
QUARTER = [n % PG for n in range(NG)]
FOUR = ()
DIRECT = ()
OUT_BUFS = 5
WIDE_BUFS = 6


def tile_multiheadlatentattention_pa_t_kernel(
    tc, x_bytes, x_scale, wq_down, bq_down, wq_up, bq_up, rope_cos, rope_sin, out
):
    nc = tc.nc
    with ExitStack() as ctx:
        keep = ctx.enter_context(tc.tile_pool(name="keep", bufs=1))
        sb = ctx.enter_context(tc.tile_pool(name="sb", bufs=3))
        ps = ctx.enter_context(tc.psum_pool(name="ps", bufs=1))
        ctx.enter_context(tc.manual_schedule())

        free = list(range(8))
        held = {}

        def bank(key, shape, dtype, readers=1):
            i = free.pop(0)
            held[key] = (ps.tile(shape, dtype, name="bank%d" % i), i, readers)
            return held[key][0]

        def give_back(key):
            t, i, readers = held.pop(key)
            if readers > 1:
                held[key] = (t, i, readers - 1)
            else:
                free.append(i)

        def place(n):
            return QUARTER[n], n // PG

        def three(n):
            return GAUSS[QUARTER[n]] and n not in FOUR

        xb = {}

        def load_x(n, cuts):
            pg, b = place(n)
            rows = x_bytes[b, pg * GRP : (pg + 1) * GRP, :].rearrange("(p j) k -> p j k", j=J)
            if n not in xb:
                xb[n] = sb.tile([P, J, H], U8, name="xbytes", bufs=NG, align_bytes=64)
            for lo, hi in zip(cuts, cuts[1:]):
                nc.sync.dma_start(out=xb[n][:, lo:hi, :], in_=rows[:, lo:hi, :])

        rope = {}

        def load_rope(lo, hi):
            for i, src in enumerate((rope_cos, rope_sin)):
                t = keep.tile([P, hi - lo, J, P], BF16, name="rope%d_%d" % (i, lo), align_bytes=64)
                nc.sync.dma_start(
                    out=t[:], in_=src[lo * GRP : hi * GRP, :].rearrange("(g p j) c -> p g j c", p=P, j=J)
                )
                for pg in range(lo, hi):
                    rope[i, pg] = t[:, pg - lo, :, :]

        sc = keep.tile([P, T4], F32, name="sc")
        wd = keep.tile([P, T4, H], BF16, name="wd", align_bytes=64)
        wd_rows = wq_down.rearrange("(m t) k -> m t k", t=T4)
        bd = keep.tile([P, T4], BF16, name="bd")
        wu = keep.tile([P, 2, LAT], BF16, name="wu", align_bytes=64)
        bu = keep.tile([P, 2, 2], BF16, name="bu")
        bias_row = keep.tile([P, HALF], BF16, name="bias_row")
        load_x(0, (0, 1, 2, J))
        nc.sync.dma_start(out=sc[:], in_=x_scale.rearrange("a b (p t) -> p (a b t)", t=T4))
        nc.sync.dma_start(out=wd[:, 0:2, :], in_=wd_rows[:, 0:2, :])
        load_x(1, (0, 2))
        nc.sync.dma_start(out=wd[:, 2:4, :], in_=wd_rows[:, 2:4, :])
        load_x(1, (2, J))
        load_x(2, (0, J))
        nc.sync.dma_start(out=bd[:], in_=bq_down.rearrange("(p t) -> p t", t=T4))
        load_rope(0, 1)
        nc.sync.dma_start(out=wu[:], in_=wq_up.rearrange("(h m) k -> m h k", h=2))
        load_x(3, (0, J))
        load_x(4, (0, J))
        load_rope(1, 4)
        with nc.allow_non_contiguous_dma(reason="one bias value for each partition and half"):
            nc.sync.dma_start(out=bu[:, :, 0:1], in_=bq_up.rearrange("(h c o) -> c h o", h=2, o=1))
        for n in range(5, NG):
            load_x(n, (0, J))
        nc.sync.dma_start(out=bias_row[:], in_=bq_up.partition_broadcast(P))

        zeros = keep.tile([P, GRP], BF16, name="zeros")
        nc.vector.memset(zeros[:], 0.0)
        idf = keep.tile([P, P], F32, name="idf")
        make_identity(nc, idf[:])
        idb = keep.tile([P, P], BF16, name="idb")
        nc.vector.tensor_copy(out=idb[:], in_=idf[:])
        idn = keep.tile([P, P], BF16, name="idn")
        nc.vector.tensor_scalar(out=idn[:], in0=idf[:], scalar1=-1.0, scalar2=None, op0=MULT)

        wdc = keep.tile([P, LAT], U32, name="wdc", align_bytes=64)
        wds = keep.tile([P, LAT], U8, name="wds", align_bytes=64)
        wuc = keep.tile([P, HALF], U32, name="wuc", align_bytes=64)
        wus = keep.tile([P, HALF], U8, name="wus", align_bytes=64)
        wdg = keep.tile([P, LAT, T4], BF16, name="wdg", align_bytes=64)
        wug = sb.tile([P, HALF, T4], BF16, name="lstage1", bufs=1, align_bytes=64)
        bsum = keep.tile([P, 1], F32, name="bsum")
        in_order = []
        tab = keep.tile([P, PG, 3 * GRP + LEND], BF16, name="tab", align_bytes=64)
        tmix = keep.tile([P, sum(GAUSS), 2, GRP], F32, name="tmix", align_bytes=64)

        xbf, xt, xs, xc, xz, ls, lc, lz, m1, m2, m3, planes, qt, pg2, pv, osb, written, rows = ({} for i in range(18))

        def wide(m):
            if m not in xbf:
                xbf[m] = sb.tile([P, 2, H], BF16, name="xbf", bufs=WIDE_BUFS, align_bytes=64)
            return xbf[m]

        def widen(m, lo=0, hi=2):
            j = 2 * (m % 2)
            nc.scalar.copy(out=wide(m)[:, lo:hi, :], in_=xb[m // 2][:, j + lo : j + hi, :].bitcast(FP8))

        def turn_words(key, words, last_sorted=False):
            tiles = words.shape[1]
            t = bank(key, [P, 2, tiles * P], F32)
            for jj in range(tiles):
                for u in range(2):
                    pick = slice(u * P, (u + 1) * P) if last_sorted and jj == tiles - 1 else slice(u, H // 2, 2)
                    nc.tensor.transpose(t[:, u, jj * P : (jj + 1) * P], words[:, jj, pick], idf[:])
            return t

        def turn(m, lo=0, hi=2):
            t = turn_words(("x", m, lo), xbf[m][:, lo:hi, :].bitcast(F32), m in in_order)
            xt[m, lo] = t[:].bitcast(BF16).rearrange("p u (r e) -> p r u e", e=2)

        def warm_up(count):
            o = bank("warm", [P, GRP], F32)
            for i in range(count):
                nc.tensor.matmul(o[:], lhsT=zeros[:, 0:P], rhs=zeros[:], start=True, stop=True)
            give_back("warm")

        def x_place(m):
            return divmod(m - 3, 2) if m < 2 * NG - 1 else (NG - 2, 0)

        def scale(m, lo=0, hi=2):
            nc.vector.tensor_tensor(
                out=x_stage(m)[:, lo * P : hi * P, :].rearrange("p r (u e) -> p r u e", e=2),
                in0=xt[m, lo],
                in1=sc[:].rearrange("p (u e) -> p u e", e=2).unsqueeze(1).to_broadcast([P, (hi - lo) * P, 2, 2]),
                op=MULT,
            )
            give_back(("x", m, lo))

        def x_stage(m):
            s, pos = x_place(m)
            if s not in xs:
                xs[s] = sb.tile([P, GRP, T4], BF16, name="slot%d" % (s % SLOTS), bufs=1, align_bytes=64)
            return xs[s][:, pos * HG : (pos + 1) * HG, :]

        def x_planes(m):
            planes["x", m] = sb.tile([P, T4, HG], BF16, name="planes", bufs=3, align_bytes=64)
            for t in range(T4):
                nc.scalar.activation(
                    out=planes["x", m][:, t, :], in_=xt[m, 0][:, :, t // 2, t % 2], func=COPY, scale=sc[:, t : t + 1]
                )
            give_back(("x", m, 0))

        def interleave(dst, src):
            nc.gpsimd.tensor_scalar(
                out=dst, in0=src.rearrange("p t r -> p r t"), scalar1=1.0, scalar2=0.0, op0=MULT, op1=ADD
            )

        def weave_x(m):
            interleave(x_stage(m), planes["x", m][:])

        def negate(pg):
            nc.gpsimd.tensor_scalar(
                out=tab[:, pg, 0:GRP], in0=cos_sin(pg)[:, 1, :], scalar1=-1.0, scalar2=0.0, op0=MULT, op1=ADD
            )

        def quant(codes, scales, staged, name, s, lo, hi):
            if s not in codes:
                codes[s] = sb.tile([P, GRP], U32, name=name + "c", bufs=4, align_bytes=64)
                scales[s] = sb.tile([P, GRP], U8, name=name + "z", bufs=4, align_bytes=64)
            nc.vector.quantize_mx(
                out=codes[s][:, lo:hi].bitcast(FP8X4),
                scales=scales[s][:, lo:hi],
                in_=staged[s][:, lo:hi, :].rearrange("p r t -> p (r t)"),
            )

        def quant_x(s, lo=0, hi=GRP):
            quant(xc, xz, xs, "x", s, lo, hi)

        def quant_lat(n, lo=0, hi=GRP):
            quant(lc, lz, ls, "l", n, lo, hi)

        def mx(dst, wc, wz, ws, codes, scales, cols, start=True, stop=True):
            nc.tensor.matmul_mx(
                out=dst,
                lhsT=wc[:, ws].bitcast(FP8X4),
                lhsT_scale=wz[:, ws],
                rhs=codes[:, cols].bitcast(FP8X4),
                rhs_scale=scales[:, cols],
                start=start,
                stop=stop,
            )

        def down(n, j):
            o = bank(("lat", n, j), [P, T4, P], F32)
            s, pos = x_place(2 * n + j // 2)
            lo = pos * HG + (j % 2) * P
            for t in range(T4):
                mx(o[:, t, :], wdc, wds, slice(t * P, (t + 1) * P), xc[s], xz[s], slice(lo, lo + P))
            m1[n, j] = o

        def lat_stage(n):
            if n not in ls:
                ls[n] = sb.tile([P, GRP, T4], BF16, name="lstage%d" % (n % 3), bufs=1, align_bytes=64)
            return ls[n]

        def lat(n, j):
            nc.vector.tensor_tensor(
                out=lat_stage(n)[:, j * P : (j + 1) * P, :],
                in0=m1[n, j][:].rearrange("p t r -> p r t"),
                in1=bd[:].unsqueeze(1).to_broadcast([P, P, T4]),
                op=ADD,
            )
            give_back(("lat", n, j))

        def down_planes(m):
            s, pos = x_place(m)
            for pair in range(2):
                m1[m, "planes", pair] = bank(("planes", m, pair), [P, 2, HG], F32)
                for e in range(2):
                    t = 2 * pair + e
                    mx(
                        m1[m, "planes", pair][:, e, :], wdc, wds, slice(t * P, (t + 1) * P),
                        xc[s], xz[s], slice(pos * HG, (pos + 1) * HG),
                    )

        def lat_planes(m):
            planes[m] = sb.tile([P, T4, HG], BF16, name="planes", bufs=3, align_bytes=64)
            for t in range(T4):
                nc.scalar.activation(
                    out=planes[m][:, t, :], in_=m1[m, "planes", t // 2][:, t % 2, :], func=IDENT, bias=bd[:, t : t + 1]
                )
                if t % 2:
                    give_back(("planes", m, t // 2))

        def tile_planes(n, j):
            planes[n, j] = sb.tile([P, T4, P], BF16, name="planes", bufs=3, align_bytes=64)
            for t in range(T4):
                nc.scalar.activation(out=planes[n, j][:, t, :], in_=m1[n, j][:, t, :], func=IDENT, bias=bd[:, t : t + 1])
            give_back(("lat", n, j))

        def weave_tile(n, j):
            interleave(lat_stage(n)[:, j * P : (j + 1) * P, :], planes[n, j][:])

        def weave(m):
            n, a = divmod(m, 2)
            interleave(lat_stage(n)[:, a * HG : (a + 1) * HG, :], planes[m][:])

        def up(n, h, readers=None):
            o = bank(("up", n, h), [P, GRP], F32, readers or (1 if h or three(n) else 1 + (not direct(n))))
            mx(o[:], wuc, wus, slice(h * P, (h + 1) * P), lc[n], lz[n], slice(0, GRP))
            m2[n, h] = o

        def up_sum(n):
            if not three(n):
                return
            o = bank(("sum", n), [P, GRP], F32)
            for h in range(2):
                mx(o[:], wuc, wus, slice(h * P, (h + 1) * P), lc[n], lz[n], slice(0, GRP), h == 0, h == 1)
            m2[n, "sum"] = o

        def biased(n):
            if n not in qt:
                qt[n] = sb.tile([P, 2, GRP], F32, name="qt", bufs=4, align_bytes=64)
            return qt[n]

        def half(n, h, lo=0, hi=GRP):
            nc.scalar.activation(out=biased(n)[:, 1 - h, lo:hi], in_=m2[n, h][:, lo:hi], func=IDENT, bias=bu[:, h, 0:1])
            give_back(("up", n, h))

        def piece(n, h, lo=0, hi=GRP):
            nc.vector.tensor_scalar(
                out=biased(n)[:, 1 - h, lo:hi], in0=m2[n, h][:, lo:hi], scalar1=bu[:, h, 0:1], scalar2=None, op0=ADD
            )
            give_back(("up", n, h))

        def cos_sin(pg):
            return tab[:, pg, GRP + LEND :].rearrange("p (i r) -> p i r", i=2)

        def direct(n):
            return n in DIRECT

        def lent(n):
            return LEND if n < NG - 4 and not three(n) else 0

        def vector_tile(n):
            if n not in pv:
                pv[n] = sb.tile([P, 2, GRP], F32, name="pv", bufs=3, align_bytes=64)
            return pv[n]

        def kept(n):
            return KEEP if three(n) and n < NG - 4 else 0

        def common(n, lo=0, hi=GRP):
            pg = QUARTER[n]
            if three(n):
                src, bias, factor = m2[n, "sum"], bsum[:], cos_sin(pg)[:, 0:1, lo:hi]
            else:
                src, bias, factor = m2[n, 0], bu[:, 0, 0:1], cos_sin(pg)[:, :, lo:hi]
            nc.vector.scalar_tensor_tensor(
                out=vector_tile(n)[:, 0 : 1 if three(n) else 2, lo:hi],
                in0=src[:, lo:hi].unsqueeze(1).to_broadcast([P, 1 if three(n) else 2, hi - lo]),
                scalar=bias,
                in1=factor,
                op0=ADD,
                op1=MULT,
            )
            give_back(("sum", n) if three(n) else ("up", n, 0))

        def mixed_tile(n, s):
            if n not in pg2:
                pg2[n] = sb.tile([P, 2, GRP], F32, name=s, bufs=1, align_bytes=64)
            return pg2[n]

        def mixed(n, s):
            pg, cols = QUARTER[n], GRP + lent(n)
            dst = mixed_tile(n, s)[:]
            if three(n):
                flat = [t.rearrange("p h r -> p (h r)")[:, 0 : 2 * GRP - kept(n)] for t in (dst, qt[n][:], tmix[:, sum(GAUSS[:pg]), :, :])]
                dst, src, factor = flat
            else:
                src = qt[n][:].rearrange("p h r -> p (h r)")[:, 0:cols].unsqueeze(1).to_broadcast([P, 2, cols])
                factor = tab[:, pg, 0 : 2 * (GRP + LEND)].rearrange("p (i r) -> p i r", i=2)[:, :, 0:cols]
            nc.gpsimd.tensor_tensor(out=dst, in0=src, in1=factor, op=MULT)

        def result(n, h):
            if n not in osb:
                osb[n] = sb.tile([P, 4, J, P], F32, name="osb", bufs=OUT_BUFS)
            return osb[n][:, h, :, :]

        def store(n, h, lo=0, hi=J):
            written.setdefault(n, []).append(h)
            heads = slice(h, h + 1)
            if n < NG - OUT_BUFS:
                if len(written[n]) < 4:
                    return
                heads = slice(0, 4)
            pg, b = place(n)
            dst = out[b, heads, pg * GRP : (pg + 1) * GRP, :].rearrange("h (p j) d -> p h j d", j=J)
            nc.sync.dma_start(
                out=dst[:, :, lo:hi, :].rearrange("p h j d -> p h (j d)"),
                in_=osb[n][:, heads, lo:hi, :].rearrange("p h j d -> p h (j d)"),
            )

        def turn_plain(n, h):
            o = bank(("out", n, h), [P, J, P], F32)
            for j in range(J):
                nc.tensor.transpose(o[:, j, :], qt[n][:, 1 - h, j * P : (j + 1) * P], idf[:])
            m3[n, h] = o

        def terms(n, i, j):
            cols = slice(j * P, (j + 1) * P)
            if three(n):
                by_vector = i == 1 and j * P >= GRP - kept(n)
                return pv[n][:, 0, cols], (pv if by_vector else pg2)[n][:, i, cols]
            if j * P < lent(n):
                return pg2[n][:, i, GRP + j * P : GRP + (j + 1) * P], pg2[n][:, i, cols]
            return pv[n][:, i, cols], pg2[n][:, i, cols]

        def turn_rotated(n, i):
            o = bank(("out", n, 2 + i), [P, J, P], F32)
            for j in range(J):
                for k, term in enumerate(terms(n, i, j)):
                    nc.tensor.matmul(o[:, j, :], lhsT=term, rhs=idf[:], start=k == 0, stop=k == 1, is_transpose=True)
            m3[n, 2 + i] = o

        def copy_out(n, h, copy=nc.scalar.copy):
            copy(out=result(n, h), in_=m3[n, h][:])
            give_back(("out", n, h))
            store(n, h)

        def up_tokens(n, h):
            o = bank(("out", n, h), [P, J, P], F32)
            ws = slice(h * P, (h + 1) * P)
            for j in range(J):
                mx(o[:, j, :], lc[n], lz[n], slice(j * P, (j + 1) * P), wuc, wus, ws)
            m3[n, h] = o

        def plain(n, h):
            nc.vector.tensor_tensor(
                out=result(n, h),
                in0=m3[n, h][:],
                in1=bias_row[:, h * P : (h + 1) * P].unsqueeze(1).to_broadcast([P, J, P]),
                op=ADD,
            )
            give_back(("out", n, h))
            store(n, h)

        def mixed_vector(n, s, h):
            pg = QUARTER[n]
            nc.vector.scalar_tensor_tensor(
                out=mixed_tile(n, s)[:, h, :],
                in0=m2[n, 1 - h if three(n) else 1][:],
                scalar=bu[:, 1 - h if three(n) else 1, 0:1],
                in1=tmix[:, sum(GAUSS[:pg]), h, :] if three(n) else tab[:, pg, h * (GRP + LEND) : h * (GRP + LEND) + GRP],
                op0=ADD,
                op1=MULT,
            )
            give_back(("up", n, 1 - h if three(n) else 1))

        def product_rows(n, h, i, lo=0, hi=J):
            if n not in rows:
                rows[n] = sb.tile([P, 2, 2, J, P], F32, name="rows", bufs=1, align_bytes=64)
            nc.vector.tensor_tensor(
                out=rows[n][:, h, i, lo:hi, :],
                in0=result(n, h)[:, lo:hi, :],
                in1=rope[i, QUARTER[n]][:, lo:hi, :],
                op=MULT,
            )

        def rotated_rows(n, i, lo=0, hi=J):
            nc.vector.tensor_tensor(
                out=result(n, 2 + i)[:, lo:hi, :],
                in0=rows[n][:, 0, i, lo:hi, :],
                in1=rows[n][:, 1, 1 - i, lo:hi, :],
                op=(SUB, ADD)[i],
            )
            store(n, 2 + i, lo, hi)

        def mixed_half(n, s, h):
            nc.gpsimd.tensor_tensor(
                out=mixed_tile(n, s)[:, h, :], in0=qt[n][:, h, :], in1=tmix[:, sum(GAUSS[: QUARTER[n]]), h, :], op=MULT
            )

        def turn_table(pg, k):
            tiles = range(J)
            if GAUSS[pg]:
                sums = ([(1, idn), (0, idn)], [(1, idb), (0, idn)], [(0, idb)])[k]
                plan = [[(i, j, ident) for i, ident in sums] for j in tiles]
            else:
                first = [[(1, j, idn)] for j in tiles] + [[(0, j, idb)] for j in range(LEND // P)]
                plan = ([[(i, j, idb)] for i in range(2) for j in tiles], [], first)[k]
            if plan:
                o = bank(("tab", pg, k), [P, len(plan), P], F32 if len(plan[0]) == 2 else BF16)
                for q, group in enumerate(plan):
                    for a, (i, j, ident) in enumerate(group):
                        nc.tensor.matmul(
                            o[:, q, :], lhsT=rope[i, pg][:, j, :], rhs=ident[:], start=a == 0, stop=a == len(group) - 1
                        )
                m3["tab", pg, k] = o

        def copy_table(pg, k):
            if ("tab", pg, k) in m3:
                if GAUSS[pg]:
                    dst = cos_sin(pg)[:, 0, :] if k == 2 else tmix[:, sum(GAUSS[:pg]), k, :]
                else:
                    dst = tab[:, pg, 0 : GRP + LEND] if k == 2 else tab[:, pg, GRP + LEND :]
                nc.scalar.copy(out=dst, in_=m3["tab", pg, k][:].rearrange("p q r -> p (q r)"))
                give_back(("tab", pg, k))

        def turn_angles(pg):
            o = bank(("angles", pg), [P, 2, J, P], BF16)
            for i in range(2):
                for j in range(J):
                    nc.tensor.matmul(o[:, i, j, :], lhsT=rope[i, pg][:, j, :], rhs=idb[:], start=True, stop=True)
            m3["angles", pg] = o

        def copy_angles(pg):
            nc.scalar.copy(out=tab[:, pg, GRP:], in_=m3["angles", pg][:].rearrange("p i j r -> p (i j r)"))
            give_back(("angles", pg))

        def mix_difference(pg):
            nc.gpsimd.tensor_tensor(
                out=tmix[:, sum(GAUSS[:pg]), 1, :], in0=cos_sin(pg)[:, 1, :], in1=cos_sin(pg)[:, 0, :], op=SUB
            )

        def turn_weights(w, h, key):
            m3[key] = turn_words(key, w[:, 2 * h : 2 * h + 2, :].bitcast(F32))

        def copy_weights(g, h, key):
            nc.scalar.copy(
                out=g[:, h * 2 * P : (h + 1) * 2 * P, :].bitcast(F32), in_=m3[key][:].rearrange("p u r -> p r u")
            )
            give_back(key)

        def quant_weights(g, c, z):
            nc.vector.quantize_mx(out=c[:].bitcast(FP8X4), scales=z[:], in_=g[:].rearrange("p r t -> p (r t)"))

        def sum_biases():
            nc.vector.tensor_tensor(out=bsum[:], in0=bu[:, 0, 0:1], in1=bu[:, 1, 0:1], op=ADD)

        last = NG - 1
        warm_up(5)

        widen(0, 0, 1)
        widen(0, 1, 2)
        widen(1)
        turn(0, 0, 1)
        scale(0, 0, 1)
        turn(0, 1, 2)
        scale(0, 1, 2)
        turn(1)
        scale(1)
        widen(2)
        turn_weights(wd, 0, "wa")
        turn(2)
        widen(3)
        widen(4)
        turn_weights(wd, 1, "wb")
        copy_weights(wdg, 0, "wa")
        quant_x(-2, HG, GRP)
        scale(2)
        copy_weights(wdg, 1, "wb")
        turn(3)
        turn_angles(0)
        turn(4)
        quant_weights(wdg, wdc, wds)
        quant_x(-1)
        x_planes(3)
        weave_x(3)
        widen(5)
        turn_table(0, 0)
        down(0, 0)
        down(0, 1)
        scale(4)
        down(0, 2)
        down(0, 3)
        copy_angles(0)
        mix_difference(0)
        tile_planes(0, 0)
        weave_tile(0, 0)
        copy_table(0, 0)
        lat(0, 1)
        turn(5)
        turn_weights(wu, 0, "wu")
        lat(0, 2)
        widen(6)
        widen(7)
        down_planes(2)
        copy_weights(wug, 0, "wu")
        lat(0, 3)
        turn_table(1, 0)
        widen(8)
        turn(6)
        lat_planes(2)
        scale(5)
        turn(7)
        copy_table(1, 0)
        turn_table(2, 2)
        quant_x(0)
        quant_weights(wug, wuc, wus)
        quant_lat(0)
        sum_biases()
        weave(2)
        negate(1)
        for s in range(1, last - 2):
            if s >= 2:
                mixed(s - 2, "slot%d" % ((s - 1) % SLOTS))
            down_planes(2 * s + 2)
            down(s, 2)
            down(s, 3)
            if s >= 2:
                copy_out(s - 2, 1)
            else:
                copy_table(2, 2)
            up(s - 1, 1)
            scale(2 * s + 4)
            share = KP if three(s - 1) and s > 1 else 0
            up(s - 1, 0, 2 if share or not three(s - 1) else 1)
            lat_planes(2 * s + 2)
            weave(2 * s + 2)
            up_sum(s - 1)
            widen(2 * s + 7)
            scale(2 * s + 5)
            if s >= 3:
                turn_rotated(s - 3, 1)
            else:
                turn_table(3, 2 * s - 2)
            if s == 2:
                turn_table(2, 1)
            if s >= 2:
                turn_plain(s - 2, 0)
            else:
                turn_table(2, 0)
            half(s - 1, 1)
            lat(s, 2)
            turn(2 * s + 6)
            if not three(s - 1):
                common(s - 1)
            elif share:
                piece(s - 1, 0, GRP - share, GRP)
            if s >= 2:
                turn_rotated(s - 2, 0)
            lat(s, 3)
            turn_plain(s - 1, 1)
            if three(s - 1):
                common(s - 1)
            if s >= 3:
                copy_out(s - 3, 3)
            else:
                copy_table(3, 2 * s - 2)
            if s == 2:
                copy_table(2, 1)
            if three(s - 1):
                half(s - 1, 0, 0, GRP - share)
            if s >= 2:
                copy_out(s - 2, 0)
            else:
                copy_table(2, 0)
            if s < last - 3:
                widen(2 * s + 8)
            if not three(s - 1):
                half(s - 1, 0)
            turn(2 * s + 7)
            if s >= 2:
                copy_out(s - 2, 2)
            quant_x(s)
            quant_lat(s)

        a, b, c, d, e, f = range(NG - 6, NG)
        mixed(b, "slot%d" % (c % SLOTS))
        down_planes(2 * e)
        down(d, 2)
        down(d, 3)
        copy_out(b, 1)
        up_sum(c)
        scale(2 * NG - 2)
        up(c, 1)
        lat_planes(2 * e)
        weave(2 * e)
        up(c, 0)
        scale(2 * NG - 1)
        turn_rotated(a, 1)
        half(c, 1)
        half(c, 0)
        lat(d, 2)
        turn_plain(b, 0)
        lat(d, 3)
        turn_rotated(b, 0)
        common(c)
        turn_plain(c, 1)
        copy_out(a, 3)
        turn_rotated(b, 1)
        copy_out(b, 0)
        quant_x(d)
        quant_x(e, 0, HG)
        quant_lat(d)
        mixed(c, "slot%d" % (e % SLOTS))
        copy_out(c, 1, nc.vector.tensor_copy)
        copy_out(b, 2)
        down(e, 2)
        down(e, 3)
        up(d, 1)
        up(d, 0)
        down(f, 0)
        lat(e, 2)
        down(f, 1)
        half(d, 1)
        lat(e, 3)
        copy_out(b, 3)
        turn_plain(c, 0)
        common(d)
        turn_plain(d, 1)
        copy_out(c, 0)
        down(f, 2)
        down(f, 3)
        half(d, 0)
        quant_lat(e)
        mixed(d, "lstage%d" % (e % 3))
        copy_out(d, 1)
        lat(f, 0)
        turn_rotated(c, 0)
        lat(f, 1)
        turn_rotated(c, 1)
        copy_out(c, 2)
        up_sum(e)
        lat(f, 2)
        up(e, 0, 2)
        copy_out(c, 3)
        lat(f, 3)
        up(e, 1)
        turn_plain(d, 0)
        half(e, 0)
        common(e)
        half(e, 1)
        quant_lat(f)
        mixed_half(e, "lstage%d" % (f % 3), 0)
        turn_rotated(d, 0)
        mixed_vector(e, "lstage%d" % (f % 3), 1)
        copy_out(d, 0)
        up_tokens(f, 0)
        up_tokens(f, 1)
        copy_out(d, 2)
        turn_plain(e, 0)
        turn_rotated(d, 1)
        plain(f, 0)
        copy_out(e, 0)
        plain(f, 1)
        turn_plain(e, 1)
        turn_rotated(e, 1)
        copy_out(d, 3)
        turn_rotated(e, 0)
        product_rows(f, 0, 0)
        copy_out(e, 1)
        product_rows(f, 1, 1)
        product_rows(f, 0, 1)
        copy_out(e, 3)
        rotated_rows(f, 0)
        copy_out(e, 2)
        product_rows(f, 1, 0, 0, 2)
        product_rows(f, 1, 0, 2, J)
        rotated_rows(f, 1, 0, 2)
        rotated_rows(f, 1, 2, J)
